import numpy as np
import ml_dtypes


def mxq(x, axis, fmt="e4m3"):
    dtype, down = {"e4m3": (ml_dtypes.float8_e4m3fn, 7), "e5m2": (ml_dtypes.float8_e5m2, 14)}[fmt]
    v = np.moveaxis(np.asarray(x, np.float32).astype(ml_dtypes.bfloat16).astype(np.float64), axis, -1)
    blocks = v.reshape(v.shape[:-1] + (-1, 32))
    amax = np.abs(blocks).max(-1, keepdims=True)
    byte = np.maximum(np.where(amax > 0, np.frexp(amax)[1] - 1 + 127, 0) - down, 1)
    scale = np.exp2(byte - 127.0)
    codes = (blocks / scale).astype(np.float32).astype(dtype).astype(np.float64)
    return np.moveaxis((codes * scale).reshape(v.shape), -1, axis)


BF16 = ml_dtypes.bfloat16


def bf(x):
    return np.asarray(x, np.float32).astype(BF16)


def f64(x):
    return np.asarray(x).astype(np.float64)


B, S, H, DK, NW = 8, 512, 2, 512, 8
E = H * DK


def setup_inputs():
    g = np.full(DK, 0.2 * np.sqrt(S))
    g[:NW] = 1.0
    return {"x": bf((np.random.standard_normal((B, S, H, DK)) * g).reshape(B, S, E))}


def reference(x):
    xh = f64(x).reshape(B, S, H, DK).transpose(0, 2, 1, 3)
    xw = xh[..., :NW]
    scores = np.ones((B, H, S, S))
    for w in range(NW):
        diff = xw[:, :, :, None, w] - xw[:, :, None, :, w]
        scores = scores * np.cos(diff * 0.5)
    scores = np.abs(scores)
    e = np.exp(scores - scores.max(-1, keepdims=True))
    out = (mxq(e, 3, "e4m3") @ mxq(xh, 2, "e4m3")) / e.sum(-1, keepdims=True)
    return out.transpose(0, 2, 1, 3).reshape(B, S, E)

@@ -1,0 +1,373 @@
+import math
+from contextlib import ExitStack
+
+import concourse.mybir as mybir
+from concourse.masks import make_identity
+
+FLOPS = 2 * 8 * 2 * 512 * 512 * 512
+
+F32 = mybir.dt.float32
+BF16 = mybir.dt.bfloat16
+I32 = mybir.dt.int32
+U32 = mybir.dt.uint32
+U8 = mybir.dt.uint8
+FP8X4 = mybir.dt.float8_e4m3fn_x4
+ALU = mybir.AluOpType
+ACT = mybir.ActivationFunctionType
+
+P = 128
+B, S, H, DK, NW = 8, 512, 2, 512, 8
+T = 4
+NHEAD = B * H
+GROUP = 8
+SKEW = 2
+AHEAD = 2
+ORDER = (7, 0, 1, 2, 3, 4, 5, 6)
+
+TWO_PI_1 = 6.28125
+TWO_PI_2 = 0.0019350051879882812
+TWO_PI_3 = 2.0 * math.pi - TWO_PI_1 - TWO_PI_2
+HALF_PI_BELOW = 1.5707962512969971
+
+
+def col(b, t, h, w):
+    return ((b * T + t) * H + h) * NW + w
+
+
+def tile_quantumkernelattention_t_kernel(tc, x, out):
+    nc = tc.nc
+    with ExitStack() as ctx:
+        ctx.enter_context(tc.manual_schedule())
+        const = ctx.enter_context(tc.tile_pool(name="const", bufs=1))
+        work = ctx.enter_context(tc.tile_pool(name="work", bufs=2))
+        psum = ctx.enter_context(tc.psum_pool(name="psum", bufs=1))
+
+        xf = const.tile([P, B * 64], BF16, name="xf")
+        for b in range(B):
+            nc.sync.dma_start(
+                out=xf[:, b * 64 : (b + 1) * 64].rearrange("p (k w) -> p k w", w=NW),
+                in_=x[b].rearrange("(p t) (h d) -> p (t h) d", t=T, h=H)[:, :, 0:NW],
+            )
+        xs = {}
+
+        def load_x(b):
+            xs[b] = work.tile([P, T, H * DK], BF16, name="xs", bufs=5)
+            nc.sync.dma_start(out=xs[b][:], in_=x[b].rearrange("(p t) e -> p t e", t=T))
+
+        for b in range(5):
+            load_x(b)
+
+        ident = const.tile([P, P], F32, name="ident")
+        make_identity(nc, ident[:])
+        negone = const.tile([P, 1], F32, name="negone")
+        nc.vector.memset(negone[:], -1.0)
+
+        NC = B * 64
+        k32 = work.tile([P, NC], I32, name="k32", tag="sw", bufs=10)
+        nc.vector.tensor_scalar(out=k32[:], in0=xf[:], scalar1=1.0 / (2.0 * math.pi), scalar2=None, op0=ALU.mult)
+        kf = work.tile([P, NC], F32, name="kf", tag="sw", bufs=10)
+        nc.vector.tensor_copy(out=kf[:], in_=k32[:])
+        t1 = work.tile([P, NC], F32, name="t1", tag="sw", bufs=10)
+        nc.vector.scalar_tensor_tensor(out=t1[:], in0=kf[:], scalar=-TWO_PI_1, in1=xf[:], op0=ALU.mult, op1=ALU.add)
+        t2 = work.tile([P, NC], F32, name="t2", tag="sw", bufs=10)
+        nc.vector.scalar_tensor_tensor(out=t2[:], in0=kf[:], scalar=-TWO_PI_2, in1=t1[:], op0=ALU.mult, op1=ALU.add)
+        nc.vector.scalar_tensor_tensor(out=t1[:], in0=kf[:], scalar=-TWO_PI_3, in1=t2[:], op0=ALU.mult, op1=ALU.add)
+        nc.vector.tensor_scalar(out=t2[:], in0=t1[:], scalar1=0.5, scalar2=HALF_PI_BELOW, op0=ALU.mult, op1=ALU.min)
+        ang = const.tile([P, NC], F32, name="ang")
+        nc.vector.tensor_scalar(out=ang[:], in0=t2[:], scalar1=-HALF_PI_BELOW, scalar2=None, op0=ALU.max)
+        nc.vector.tensor_scalar(out=t2[:], in0=ang[:], scalar1=math.pi / 2.0, scalar2=None, op0=ALU.add)
+        nc.vector.tensor_scalar(out=t1[:], in0=ang[:], scalar1=0.0, scalar2=math.pi, op0=ALU.is_ge, op1=ALU.mult)
+        bias = const.tile([P, NC], F32, name="bias")
+        nc.vector.scalar_tensor_tensor(
+            out=bias[:], in0=t1[:], scalar=-math.pi / 2.0, in1=ang[:], op0=ALU.add, op1=ALU.subtract
+        )
+        cs = work.tile([P, 2, NC], F32, name="cs", tag="e", bufs=4)
+        nc.scalar.activation(out=cs[:, 1, :], in_=ang[:], func=ACT.Sin)
+        nc.scalar.activation(out=cs[:, 0, :], in_=t2[:], func=ACT.Sin)
+        NK = B * T * H
+        cs4 = cs[:].rearrange("p c (k w) -> p k c w", w=NW)
+
+        def outer(dst, left, nl, right, nr):
+            nk = dst.shape[1]
+            nc.vector.tensor_tensor(
+                out=dst,
+                in0=left.unsqueeze(3).to_broadcast([P, nk, nl, nr]),
+                in1=right.unsqueeze(2).to_broadcast([P, nk, nl, nr]),
+                op=ALU.mult,
+            )
+
+        pair = []
+        for q in range(3):
+            pq = work.tile([P, NK, 2, 2], F32, name="pair%d" % q, tag="pr", bufs=4)
+            outer(pq[:], cs4[:, :, :, 2 * q], 2, cs4[:, :, :, 2 * q + 1], 2)
+            pair.append(pq[:].rearrange("p k i j -> p k (i j)"))
+        f16 = const.tile([P, NK, 4, 4], F32, name="f16")
+        outer(f16[:], pair[0], 4, pair[1], 4)
+        f8 = const.tile([P, NK, 4, 2], F32, name="f8")
+        outer(f8[:], pair[2], 4, cs4[:, :, :, 6], 2)
+        f16v = f16[:].rearrange("p k a c -> p k (a c)")
+        f8v = f8[:].rearrange("p k a c -> p k (a c)")
+
+        phi = {}
+
+        def make_phi(b):
+            phi[b] = work.tile([P, 6, 16, 8], F32, name="phi", bufs=2)
+            k0 = b * T * H + H
+            outer(phi[b][:], f16v[:, k0 : k0 + 6, :], 16, f8v[:, k0 : k0 + 6, :], 8)
+
+        st = {}
+
+        def bank(name):
+            return psum.tile([P, 512], F32, name=name, tag="A", bufs=3)
+
+        def pe_job(job):
+            hd = job[1]
+            b, h = divmod(hd, H)
+            tl = bank("tab")
+            if job[0] == "pt":
+                for t in range(1, T):
+                    nc.tensor.transpose(
+                        out=tl[:, (t - 1) * P : t * P],
+                        in_=phi[b][:, (t - 1) * H + h].rearrange("p a c -> p (a c)"),
+                        identity=ident[:],
+                    )
+            else:
+                w = ORDER[job[2]]
+                for t in range(T):
+                    c = col(b, t, h, w)
+                    nc.tensor.transpose(
+                        out=tl[:, t * P : (t + 1) * P], in_=ang[:, c : c + 1].to_broadcast([P, P]), identity=ident[:]
+                    )
+            st[job] = tl
+
+        def mul(dst, a, c):
+            nc.vector.tensor_tensor(out=dst, in0=a, in1=c, op=ALU.mult)
+
+        def blocks_product(hd):
+            d = st[hd]
+            mul(d["ab"][:, 512:1024], d["f7a"][:], d["c7"][:, 0:512])
+            mul(d["ab"][:, 1024:1280], d["f7b"][:, 0:256], d["c7"][:, 512:768])
+
+        def act_job(job):
+            hd = job[1]
+            b, h = divmod(hd, H)
+            tl = st.pop(job)
+            d = st[hd]
+            if job[0] == "pt":
+                pht = work.tile([P, 3 * P], F32, name="pht", bufs=2)
+                nc.scalar.copy(out=pht[:], in_=tl[:, 0 : 3 * P])
+                d["f7a"] = psum.tile([P, 512], F32, name="f7a", tag="B", bufs=3)
+                d["f7b"] = psum.tile([P, 512], F32, name="f7b", tag="B", bufs=3)
+                nc.tensor.matmul(out=d["f7a"][:, 0:384], lhsT=pht[:, 0:128], rhs=pht[:, 0:384], start=True, stop=True)
+                nc.tensor.matmul(out=d["f7b"][:, 0:256], lhsT=pht[:, 128:256], rhs=pht[:, 128:384], start=True, stop=True)
+                d["pht"] = pht
+                return
+            j = job[2]
+            w = ORDER[j]
+            if "pht" in d:
+                pht = d.pop("pht")
+                nc.tensor.matmul(out=d["f7a"][:, 384:512], lhsT=pht[:, 256:384], rhs=pht[:, 256:384], start=True, stop=True)
+                d["f"] = True
+                if "c7" in d:
+                    blocks_product(hd)
+            sw = work.tile([P, 512], F32, name="sw", bufs=10)
+            c = col(b, 0, h, w)
+            nc.scalar.activation(out=sw[:], in_=tl[:], func=ACT.Sin, bias=bias[:, c : c + 1])
+            d["s"].append(sw)
+            if j == 0:
+                c7 = work.tile([P, 768], F32, name="c7", bufs=2)
+                for (t, o0, n) in ((1, 0, 384), (3, 384, 128), (2, 512, 256)):
+                    c = col(b, t, h, w)
+                    nc.scalar.activation(
+                        out=c7[:, o0 : o0 + n], in_=tl[:, 512 - n : 512], func=ACT.Sin, bias=bias[:, c : c + 1]
+                    )
+                d["c7"] = c7
+                if "f" in d:
+                    blocks_product(hd)
+            if j % 2 == 1:
+                pr = work.tile([P, 512], F32, name="pr", bufs=4)
+                mul(pr[:], d["s"][j - 1][:], d["s"][j][:])
+                d["p"].append(pr)
+            if j == 3:
+                qa = work.tile([P, 512], F32, name="qa", bufs=2)
+                mul(qa[:], d["p"][0][:], d["p"][1][:])
+                d["qa"] = qa
+            if j == 7:
+                qb = work.tile([P, 512], F32, name="qb", bufs=2)
+                mul(qb[:], d["p"][2][:], d["p"][3][:])
+                mul(d["ab"][:, 0:512], d["qa"][:], qb[:])
+                nc.vector.scalar_tensor_tensor(
+                    out=d["ab"][:], in0=d["ab"][:], scalar=-1.0, in1=d["ab"][:], op0=ALU.mult, op1=ALU.max
+                )
+
+        def sin_phase(heads, pending):
+            jobs = []
+            for i, hd in enumerate(heads):
+                st[hd] = {"s": [], "p": []}
+                if i > 0:
+                    jobs.append(("pt", hd))
+                for j in range(NW):
+                    jobs.append(("tab", hd, j))
+                    if i == 0 and j == 2:
+                        jobs.append(("pt", hd))
+            done = 0
+            for n, job in enumerate(jobs):
+                hd = job[1]
+                if job[0] == "tab" and job[2] == 0:
+                    st[hd]["ab"] = work.tile([P, 1280], F32, name="ab", bufs=GROUP)
+                if job[0] == "tab" and job[2] == 1 and hd % 2 == 0 and hd + 2 <= heads[-1]:
+                    make_phi(hd // 2 + 1)
+                while done < min(len(jobs), n + 1 + AHEAD):
+                    pe_job(jobs[done])
+                    done += 1
+                act_job(job)
+                if n % 6 == 2 and 1 <= n // 6 <= len(pending):
+                    pending[n // 6 - 1]()
+
+        def mirror_a(hd):
+            ab = st[hd]["ab"]
+            m = psum.tile([P, 512], F32, name="mira", tag="B", bufs=3)
+            for (dst, src) in ((0, 384), (128, 768), (256, 1152), (384, 128)):
+                nc.tensor.transpose(out=m[:, dst : dst + P], in_=ab[:, src : src + P], identity=ident[:])
+            st[hd]["ma"] = m
+
+        def mirror_b(hd):
+            ab = st[hd]["ab"]
+            m = psum.tile([P, 512], F32, name="mirb", tag="B", bufs=3)
+            for (dst, src) in ((0, 256), (128, 640)):
+                nc.tensor.transpose(out=m[:, dst : dst + P], in_=ab[:, src : src + P], identity=ident[:])
+            st[hd]["mb"] = m
+
+        def expo(hd, t, lo, n, src, slot):
+            d = st[hd]
+            nc.scalar.activation(
+                out=d["e"][:, t, lo : lo + n], in_=src, func=ACT.Exp, bias=negone[:],
+                accum_out=d["acc"][:, 2 * t + slot : 2 * t + slot + 1],
+            )
+
+        def regroup(dst, src):
+            nc.vector.tensor_copy(
+                out=dst[:].rearrange("p (c i) t -> p c t i", i=4), in_=src.rearrange("p t (c i) -> p c t i", i=4)
+            )
+
+        def quantise(name, grouped):
+            codes = work.tile([P, 512], U32, name=name + "_codes", bufs=SKEW + 2, align_bytes=64)
+            scales = work.tile([P, 512], U8, name=name + "_scales", bufs=SKEW + 2, align_bytes=64)
+            nc.vector.quantize_mx(
+                out=codes[:].bitcast(FP8X4), scales=scales[:], in_=grouped[:].rearrange("p w t -> p (w t)")
+            )
+            return codes, scales
+
+        def product(hd, t):
+            d = st[hd]
+            ec, es = d["eq"]
+            xc, xsc = d["xq"]
+            o = psum.tile([P, 512], F32, name="o", tag="O", bufs=2)
+            nc.tensor.matmul_mx(
+                out=o[:],
+                lhsT=ec[:, t * P : (t + 1) * P].bitcast(FP8X4),
+                lhsT_scale=es[:, t * P : (t + 1) * P],
+                rhs=xc[:].bitcast(FP8X4),
+                rhs_scale=xsc[:],
+                start=True,
+                stop=True,
+            )
+            d["o"][t] = o
+
+        def begin_product(hd):
+            st[hd]["o"] = {}
+            st[hd]["res"] = work.tile([P, T, DK], F32, name="res", bufs=3)
+            product(hd, 0)
+            product(hd, 1)
+
+        def leave_scalar(hd, t):
+            d = st[hd]
+            nc.scalar.activation(out=d["res"][:, t, :], in_=d["o"][t][:], func=ACT.Copy, scale=d["rc"][:, t : t + 1])
+
+        def leave_vector(hd, t):
+            d = st[hd]
+            nc.vector.tensor_scalar(
+                out=d["res"][:, t, :], in0=d["o"][t][:], scalar1=d["rc"][:, t : t + 1], scalar2=None, op0=ALU.mult
+            )
+
+        def store(hd):
+            b, h = divmod(hd, H)
+            nc.sync.dma_start(
+                out=out[b].rearrange("(p t) e -> p t e", t=T)[:, :, h * DK : (h + 1) * DK], in_=st[hd]["res"][:]
+            )
+
+        def exp_phase(heads):
+            n = len(heads)
+            mirror_a(heads[0])
+            mirror_b(heads[0])
+            mirror_a(heads[1])
+            for i, hd in enumerate(heads):
+                b, h = divmod(hd, H)
+                d = st[hd]
+                prev = heads[i - SKEW] if i >= SKEW else None
+                if prev is not None:
+                    begin_product(prev)
+                d["acc"] = work.tile([P, 2 * T], F32, name="acc", bufs=3)
+                d["e"] = work.tile([P, T, S], BF16, name="e", bufs=4)
+                ab = d["ab"]
+                expo(hd, 3, 0, 384, d["ma"][:, 0:384], 0)
+                expo(hd, 1, 0, 128, d["ma"][:, 384:512], 0)
+                if i + 1 < n:
+                    mirror_b(heads[i + 1])
+                expo(hd, 2, 0, 256, d["mb"][:, 0:256], 0)
+                if i + 2 < n:
+                    mirror_a(heads[i + 2])
+                expo(hd, 0, 0, 256, ab[:, 0:256], 0)
+                expo(hd, 0, 256, 256, ab[:, 256:512], 1)
+                expo(hd, 1, 128, 384, ab[:, 512:896], 1)
+                expo(hd, 3, 384, 128, ab[:, 896:1024], 1)
+                expo(hd, 2, 256, 256, ab[:, 1024:1280], 1)
+                if prev is not None:
+                    leave_scalar(prev, 0)
+                    product(prev, 2)
+                    leave_scalar(prev, 1)
+                    product(prev, 3)
+                    leave_scalar(prev, 2)
+                xg = work.tile([P, DK, T], BF16, name="xg", bufs=2, align_bytes=64)
+                regroup(xg, xs[b][:, :, h * DK : (h + 1) * DK])
+                if h == 1 and b + 5 < B:
+                    load_x(b + 5)
+                if prev is not None:
+                    leave_vector(prev, 3)
+                    store(prev)
+                eg = work.tile([P, S, T], BF16, name="eg", bufs=2, align_bytes=64)
+                regroup(eg, d["e"][:])
+                d["xq"] = quantise("x", xg)
+                d["eq"] = quantise("e", eg)
+                rs = work.tile([P, T], F32, name="rs", bufs=2)
+                nc.vector.tensor_reduce(
+                    out=rs[:], in_=d["acc"][:].rearrange("p (t s) -> p t s", s=2), axis=mybir.AxisListType.X, op=ALU.add
+                )
+                d["rc"] = work.tile([P, T], F32, name="rc", bufs=SKEW + 2)
+                nc.vector.reciprocal(out=d["rc"][:], in_=rs[:])
+
+            def finisher(hd):
+                def finish():
+                    begin_product(hd)
+                    leave_scalar(hd, 0)
+                    product(hd, 2)
+                    leave_vector(hd, 1)
+                    product(hd, 3)
+                    leave_scalar(hd, 2)
+                    leave_vector(hd, 3)
+                    store(hd)
+
+                return finish
+
+            return [finisher(hd) for hd in heads[n - SKEW :]]
+
+        make_phi(0)
+        pending = []
+        for g in range(NHEAD // GROUP):
+            heads = list(range(g * GROUP, (g + 1) * GROUP))
+            sin_phase(heads, pending)
+            if g + 1 < NHEAD // GROUP:
+                make_phi((g + 1) * GROUP // H)
+            pending = exp_phase(heads)
+        for f in pending:
+            f()

@@ -21,7 +21,7 @@ T = 4
 NHEAD = B * H
 GROUP = 8
 SKEW = 2
-AHEAD = 2
+AHEAD = 4
 ORDER = (7, 0, 1, 2, 3, 4, 5, 6)
 
 TWO_PI_1 = 6.28125
@@ -98,7 +98,7 @@ def tile_quantumkernelattention_t_kernel(tc, x, out):
 
         pair = []
         for q in range(3):
-            pq = work.tile([P, NK, 2, 2], F32, name="pair%d" % q, tag="pr", bufs=4)
+            pq = work.tile([P, NK, 2, 2], F32, name="pair%d" % q, tag="pr", bufs=5)
             outer(pq[:], cs4[:, :, :, 2 * q], 2, cs4[:, :, :, 2 * q + 1], 2)
             pair.append(pq[:].rearrange("p k i j -> p k (i j)"))
         f16 = const.tile([P, NK, 4, 4], F32, name="f16")
@@ -116,65 +116,39 @@ def tile_quantumkernelattention_t_kernel(tc, x, out):
             outer(phi[b][:], f16v[:, k0 : k0 + 6, :], 16, f8v[:, k0 : k0 + 6, :], 8)
 
         st = {}
+        for hd in range(NHEAD):
+            st[hd] = {"s": {}, "p": {}, "o": {}}
 
-        def bank(name):
-            return psum.tile([P, 512], F32, name=name, tag="A", bufs=3)
+        def bank():
+            return psum.tile([P, 512], F32, name="a", tag="A", bufs=AHEAD + 1)
 
-        def pe_job(job):
-            hd = job[1]
-            b, h = divmod(hd, H)
-            tl = bank("tab")
-            if job[0] == "pt":
-                for t in range(1, T):
-                    nc.tensor.transpose(
-                        out=tl[:, (t - 1) * P : t * P],
-                        in_=phi[b][:, (t - 1) * H + h].rearrange("p a c -> p (a c)"),
-                        identity=ident[:],
-                    )
-            else:
-                w = ORDER[job[2]]
-                for t in range(T):
-                    c = col(b, t, h, w)
-                    nc.tensor.transpose(
-                        out=tl[:, t * P : (t + 1) * P], in_=ang[:, c : c + 1].to_broadcast([P, P]), identity=ident[:]
-                    )
-            st[job] = tl
+        def side_bank():
+            return psum.tile([P, 512], F32, name="b", tag="B", bufs=3)
 
         def mul(dst, a, c):
             nc.vector.tensor_tensor(out=dst, in0=a, in1=c, op=ALU.mult)
 
-        def blocks_product(hd):
-            d = st[hd]
-            mul(d["ab"][:, 512:1024], d["f7a"][:], d["c7"][:, 0:512])
-            mul(d["ab"][:, 1024:1280], d["f7b"][:, 0:256], d["c7"][:, 512:768])
-
-        def act_job(job):
-            hd = job[1]
+        def spread(hd, j):
             b, h = divmod(hd, H)
-            tl = st.pop(job)
+            tl = bank()
+            for t in range(T):
+                c = col(b, t, h, ORDER[j])
+                nc.tensor.transpose(
+                    out=tl[:, t * P : (t + 1) * P], in_=ang[:, c : c + 1].to_broadcast([P, P]), identity=ident[:]
+                )
+            st[hd]["tab"] = st[hd].get("tab", []) + [tl]
+
+        def sines(hd, j):
+            b, h = divmod(hd, H)
             d = st[hd]
-            if job[0] == "pt":
-                pht = work.tile([P, 3 * P], F32, name="pht", bufs=2)
-                nc.scalar.copy(out=pht[:], in_=tl[:, 0 : 3 * P])
-                d["f7a"] = psum.tile([P, 512], F32, name="f7a", tag="B", bufs=3)
-                d["f7b"] = psum.tile([P, 512], F32, name="f7b", tag="B", bufs=3)
-                nc.tensor.matmul(out=d["f7a"][:, 0:384], lhsT=pht[:, 0:128], rhs=pht[:, 0:384], start=True, stop=True)
-                nc.tensor.matmul(out=d["f7b"][:, 0:256], lhsT=pht[:, 128:256], rhs=pht[:, 128:384], start=True, stop=True)
-                d["pht"] = pht
-                return
-            j = job[2]
+            tl = d["tab"].pop(0)
             w = ORDER[j]
-            if "pht" in d:
-                pht = d.pop("pht")
-                nc.tensor.matmul(out=d["f7a"][:, 384:512], lhsT=pht[:, 256:384], rhs=pht[:, 256:384], start=True, stop=True)
-                d["f"] = True
-                if "c7" in d:
-                    blocks_product(hd)
             sw = work.tile([P, 512], F32, name="sw", bufs=10)
             c = col(b, 0, h, w)
             nc.scalar.activation(out=sw[:], in_=tl[:], func=ACT.Sin, bias=bias[:, c : c + 1])
-            d["s"].append(sw)
+            d["s"][j] = sw
             if j == 0:
+                d["ab"] = work.tile([P, 1280], F32, name="ab", bufs=GROUP + 1)
                 c7 = work.tile([P, 768], F32, name="c7", bufs=2)
                 for (t, o0, n) in ((1, 0, 384), (3, 384, 128), (2, 512, 256)):
                     c = col(b, t, h, w)
@@ -182,58 +156,64 @@ def tile_quantumkernelattention_t_kernel(tc, x, out):
                         out=c7[:, o0 : o0 + n], in_=tl[:, 512 - n : 512], func=ACT.Sin, bias=bias[:, c : c + 1]
                     )
                 d["c7"] = c7
-                if "f" in d:
-                    blocks_product(hd)
-            if j % 2 == 1:
-                pr = work.tile([P, 512], F32, name="pr", bufs=4)
-                mul(pr[:], d["s"][j - 1][:], d["s"][j][:])
-                d["p"].append(pr)
-            if j == 3:
-                qa = work.tile([P, 512], F32, name="qa", bufs=2)
-                mul(qa[:], d["p"][0][:], d["p"][1][:])
-                d["qa"] = qa
-            if j == 7:
-                qb = work.tile([P, 512], F32, name="qb", bufs=2)
-                mul(qb[:], d["p"][2][:], d["p"][3][:])
-                mul(d["ab"][:, 0:512], d["qa"][:], qb[:])
-                nc.vector.scalar_tensor_tensor(
-                    out=d["ab"][:], in0=d["ab"][:], scalar=-1.0, in1=d["ab"][:], op0=ALU.mult, op1=ALU.max
-                )
 
-        def sin_phase(heads, pending):
-            jobs = []
-            for i, hd in enumerate(heads):
-                st[hd] = {"s": [], "p": []}
-                if i > 0:
-                    jobs.append(("pt", hd))
-                for j in range(NW):
-                    jobs.append(("tab", hd, j))
-                    if i == 0 and j == 2:
-                        jobs.append(("pt", hd))
-            done = 0
-            for n, job in enumerate(jobs):
-                hd = job[1]
-                if job[0] == "tab" and job[2] == 0:
-                    st[hd]["ab"] = work.tile([P, 1280], F32, name="ab", bufs=GROUP)
-                if job[0] == "tab" and job[2] == 1 and hd % 2 == 0 and hd + 2 <= heads[-1]:
-                    make_phi(hd // 2 + 1)
-                while done < min(len(jobs), n + 1 + AHEAD):
-                    pe_job(jobs[done])
-                    done += 1
-                act_job(job)
-                if n % 6 == 2 and 1 <= n // 6 <= len(pending):
-                    pending[n // 6 - 1]()
+        def features_t(hd):
+            b, h = divmod(hd, H)
+            tl = bank()
+            for t in range(1, T):
+                nc.tensor.transpose(
+                    out=tl[:, (t - 1) * P : t * P],
+                    in_=phi[b][:, (t - 1) * H + h].rearrange("p a c -> p (a c)"),
+                    identity=ident[:],
+                )
+            st[hd]["pt"] = tl
+
+        def seven(hd):
+            d = st[hd]
+            pht = work.tile([P, 3 * P], F32, name="pht", bufs=2)
+            nc.scalar.copy(out=pht[:], in_=d["pt"][:, 0 : 3 * P])
+            d["f7a"] = side_bank()
+            d["f7b"] = side_bank()
+            nc.tensor.matmul(out=d["f7a"][:, 0:384], lhsT=pht[:, 0:128], rhs=pht[:, 0:384], start=True, stop=True)
+            nc.tensor.matmul(out=d["f7a"][:, 384:512], lhsT=pht[:, 256:384], rhs=pht[:, 256:384], start=True, stop=True)
+            nc.tensor.matmul(out=d["f7b"][:, 0:256], lhsT=pht[:, 128:256], rhs=pht[:, 128:384], start=True, stop=True)
+
+        def blocks_a(hd):
+            d = st[hd]
+            mul(d["ab"][:, 512:1024], d["f7a"][:], d["c7"][:, 0:512])
+
+        def blocks_b(hd):
+            d = st[hd]
+            mul(d["ab"][:, 1024:1280], d["f7b"][:, 0:256], d["c7"][:, 512:768])
+
+        def pair_product(hd, q):
+            d = st[hd]
+            d["p"][q] = work.tile([P, 512], F32, name="pr", bufs=5)
+            mul(d["p"][q][:], d["s"].pop(2 * q)[:], d["s"].pop(2 * q + 1)[:])
+
+        def quad_product(hd, q):
+            d = st[hd]
+            d["q%d" % q] = work.tile([P, 512], F32, name="qd", bufs=4)
+            mul(d["q%d" % q][:], d["p"].pop(2 * q)[:], d["p"].pop(2 * q + 1)[:])
+
+        def row_product(hd):
+            d = st[hd]
+            mul(d["ab"][:, 0:512], d["q0"][:], d["q1"][:])
+
+        def magnitude(hd):
+            ab = st[hd]["ab"]
+            nc.vector.scalar_tensor_tensor(out=ab[:], in0=ab[:], scalar=-1.0, in1=ab[:], op0=ALU.mult, op1=ALU.max)
 
         def mirror_a(hd):
             ab = st[hd]["ab"]
-            m = psum.tile([P, 512], F32, name="mira", tag="B", bufs=3)
+            m = side_bank()
             for (dst, src) in ((0, 384), (128, 768), (256, 1152), (384, 128)):
                 nc.tensor.transpose(out=m[:, dst : dst + P], in_=ab[:, src : src + P], identity=ident[:])
             st[hd]["ma"] = m
 
         def mirror_b(hd):
             ab = st[hd]["ab"]
-            m = psum.tile([P, 512], F32, name="mirb", tag="B", bufs=3)
+            m = side_bank()
             for (dst, src) in ((0, 256), (128, 640)):
                 nc.tensor.transpose(out=m[:, dst : dst + P], in_=ab[:, src : src + P], identity=ident[:])
             st[hd]["mb"] = m
@@ -244,6 +224,24 @@ def tile_quantumkernelattention_t_kernel(tc, x, out):
                 out=d["e"][:, t, lo : lo + n], in_=src, func=ACT.Exp, bias=negone[:],
                 accum_out=d["acc"][:, 2 * t + slot : 2 * t + slot + 1],
             )
+
+        def expo_a(hd):
+            d = st[hd]
+            d["acc"] = work.tile([P, 2 * T], F32, name="acc", bufs=3)
+            d["e"] = work.tile([P, T, S], BF16, name="e", bufs=4)
+            expo(hd, 3, 0, 384, d["ma"][:, 0:384], 0)
+            expo(hd, 1, 0, 128, d["ma"][:, 384:512], 0)
+
+        def expo_b(hd):
+            expo(hd, 2, 0, 256, st[hd]["mb"][:, 0:256], 0)
+
+        def expo_c(hd):
+            ab = st[hd]["ab"]
+            expo(hd, 0, 0, 256, ab[:, 0:256], 0)
+            expo(hd, 0, 256, 256, ab[:, 256:512], 1)
+            expo(hd, 1, 128, 384, ab[:, 512:896], 1)
+            expo(hd, 3, 384, 128, ab[:, 896:1024], 1)
+            expo(hd, 2, 256, 256, ab[:, 1024:1280], 1)
 
         def regroup(dst, src):
             nc.vector.tensor_copy(
@@ -258,11 +256,40 @@ def tile_quantumkernelattention_t_kernel(tc, x, out):
             )
             return codes, scales
 
+        def regroup_x(hd):
+            b, h = divmod(hd, H)
+            st[hd]["xg"] = work.tile([P, DK, T], BF16, name="xg", bufs=2, align_bytes=64)
+            regroup(st[hd]["xg"], xs[b][:, :, h * DK : (h + 1) * DK])
+            if h == 1 and b + 5 < B:
+                load_x(b + 5)
+
+        def regroup_e(hd):
+            st[hd]["eg"] = work.tile([P, S, T], BF16, name="eg", bufs=2, align_bytes=64)
+            regroup(st[hd]["eg"], st[hd]["e"][:])
+
+        def quantise_x(hd):
+            st[hd]["xq"] = quantise("x", st[hd]["xg"])
+
+        def quantise_e(hd):
+            st[hd]["eq"] = quantise("e", st[hd]["eg"])
+
+        def row_sums(hd):
+            d = st[hd]
+            d["rs"] = work.tile([P, T], F32, name="rs", bufs=2)
+            nc.vector.tensor_reduce(
+                out=d["rs"][:], in_=d["acc"][:].rearrange("p (t s) -> p t s", s=2), axis=mybir.AxisListType.X, op=ALU.add
+            )
+
+        def inverse(hd):
+            d = st[hd]
+            d["rc"] = work.tile([P, T], F32, name="rc", bufs=SKEW + 2)
+            nc.vector.reciprocal(out=d["rc"][:], in_=d["rs"][:])
+
         def product(hd, t):
             d = st[hd]
             ec, es = d["eq"]
             xc, xsc = d["xq"]
-            o = psum.tile([P, 512], F32, name="o", tag="O", bufs=2)
+            o = bank()
             nc.tensor.matmul_mx(
                 out=o[:],
                 lhsT=ec[:, t * P : (t + 1) * P].bitcast(FP8X4),
@@ -274,14 +301,10 @@ def tile_quantumkernelattention_t_kernel(tc, x, out):
             )
             d["o"][t] = o
 
-        def begin_product(hd):
-            st[hd]["o"] = {}
-            st[hd]["res"] = work.tile([P, T, DK], F32, name="res", bufs=3)
-            product(hd, 0)
-            product(hd, 1)
-
         def leave_scalar(hd, t):
             d = st[hd]
+            if t == 0:
+                d["res"] = work.tile([P, T, DK], F32, name="res", bufs=3)
             nc.scalar.activation(out=d["res"][:, t, :], in_=d["o"][t][:], func=ACT.Copy, scale=d["rc"][:, t : t + 1])
 
         def leave_vector(hd, t):
@@ -296,78 +319,100 @@ def tile_quantumkernelattention_t_kernel(tc, x, out):
                 out=out[b].rearrange("(p t) e -> p t e", t=T)[:, :, h * DK : (h + 1) * DK], in_=st[hd]["res"][:]
             )
 
-        def exp_phase(heads):
+        items = []
+
+        def plain(f, *a):
+            items.append((None, lambda: f(*a), None))
+
+        def banked(fill, use, *a):
+            items.append((lambda: fill(*a), lambda: use(*a), a[0] if fill is product else None))
+
+        def leave_items(hd, engines):
+            for t in range(T):
+                banked(product, leave_scalar if engines[t] == "s" else leave_vector, hd, t)
+            plain(store, hd)
+
+        groups = [list(range(g * GROUP, (g + 1) * GROUP)) for g in range(NHEAD // GROUP)]
+        late = []
+        for g, heads in enumerate(groups):
             n = len(heads)
-            mirror_a(heads[0])
-            mirror_b(heads[0])
-            mirror_a(heads[1])
             for i, hd in enumerate(heads):
-                b, h = divmod(hd, H)
-                d = st[hd]
+                pv = heads[i - 1] if i > 0 else None
+                for j in range(NW):
+                    banked(spread, sines, hd, j)
+                    if j == 0:
+                        if pv is not None:
+                            plain(blocks_a, hd)
+                            plain(quad_product, pv, 1)
+                            plain(blocks_b, hd)
+                            plain(row_product, pv)
+                    if j == 1:
+                        plain(pair_product, hd, 0)
+                        if pv is not None:
+                            plain(magnitude, pv)
+                    if j == 2 and i == 0:
+                        banked(features_t, seven, hd)
+                    if j == 2 and late:
+                        leave_items(late.pop(0), "sssv")
+                    if j == 3:
+                        if i == 0:
+                            plain(blocks_a, hd)
+                        plain(pair_product, hd, 1)
+                        if i == 0:
+                            plain(blocks_b, hd)
+                        if hd % 2 == 0 and hd + 2 < NHEAD:
+                            plain(make_phi, hd // 2 + 1)
+                    if j == 4 and i + 1 < n:
+                        banked(features_t, seven, heads[i + 1])
+                    if j == 5:
+                        plain(pair_product, hd, 2)
+                        plain(quad_product, hd, 0)
+                    if j == 7:
+                        plain(pair_product, hd, 3)
+            last = heads[-1]
+            plain(mirror_a, heads[0])
+            plain(mirror_b, heads[0])
+            plain(mirror_a, heads[1])
+            for i, hd in enumerate(heads):
                 prev = heads[i - SKEW] if i >= SKEW else None
-                if prev is not None:
-                    begin_product(prev)
-                d["acc"] = work.tile([P, 2 * T], F32, name="acc", bufs=3)
-                d["e"] = work.tile([P, T, S], BF16, name="e", bufs=4)
-                ab = d["ab"]
-                expo(hd, 3, 0, 384, d["ma"][:, 0:384], 0)
-                expo(hd, 1, 0, 128, d["ma"][:, 384:512], 0)
+                plain(expo_a, hd)
+                if i == 0:
+                    plain(quad_product, last, 1)
+                plain(regroup_x, hd)
+                if i == 0:
+                    plain(row_product, last)
                 if i + 1 < n:
-                    mirror_b(heads[i + 1])
-                expo(hd, 2, 0, 256, d["mb"][:, 0:256], 0)
+                    plain(mirror_b, heads[i + 1])
+                plain(expo_b, hd)
                 if i + 2 < n:
-                    mirror_a(heads[i + 2])
-                expo(hd, 0, 0, 256, ab[:, 0:256], 0)
-                expo(hd, 0, 256, 256, ab[:, 256:512], 1)
-                expo(hd, 1, 128, 384, ab[:, 512:896], 1)
-                expo(hd, 3, 384, 128, ab[:, 896:1024], 1)
-                expo(hd, 2, 256, 256, ab[:, 1024:1280], 1)
+                    plain(mirror_a, heads[i + 2])
+                plain(expo_c, hd)
                 if prev is not None:
-                    leave_scalar(prev, 0)
-                    product(prev, 2)
-                    leave_scalar(prev, 1)
-                    product(prev, 3)
-                    leave_scalar(prev, 2)
-                xg = work.tile([P, DK, T], BF16, name="xg", bufs=2, align_bytes=64)
-                regroup(xg, xs[b][:, :, h * DK : (h + 1) * DK])
-                if h == 1 and b + 5 < B:
-                    load_x(b + 5)
-                if prev is not None:
-                    leave_vector(prev, 3)
-                    store(prev)
-                eg = work.tile([P, S, T], BF16, name="eg", bufs=2, align_bytes=64)
-                regroup(eg, d["e"][:])
-                d["xq"] = quantise("x", xg)
-                d["eq"] = quantise("e", eg)
-                rs = work.tile([P, T], F32, name="rs", bufs=2)
-                nc.vector.tensor_reduce(
-                    out=rs[:], in_=d["acc"][:].rearrange("p (t s) -> p t s", s=2), axis=mybir.AxisListType.X, op=ALU.add
-                )
-                d["rc"] = work.tile([P, T], F32, name="rc", bufs=SKEW + 2)
-                nc.vector.reciprocal(out=d["rc"][:], in_=rs[:])
-
-            def finisher(hd):
-                def finish():
-                    begin_product(hd)
-                    leave_scalar(hd, 0)
-                    product(hd, 2)
-                    leave_vector(hd, 1)
-                    product(hd, 3)
-                    leave_scalar(hd, 2)
-                    leave_vector(hd, 3)
-                    store(hd)
-
-                return finish
-
-            return [finisher(hd) for hd in heads[n - SKEW :]]
+                    for t in range(3):
+                        banked(product, leave_scalar, prev, t)
+                    banked(product, leave_vector, prev, 3)
+                    plain(store, prev)
+                plain(regroup_e, hd)
+                if i == 0:
+                    plain(magnitude, last)
+                plain(quantise_x, hd)
+                plain(row_sums, hd)
+                plain(quantise_e, hd)
+                plain(inverse, hd)
+            late = heads[n - SKEW :]
+        for hd in late:
+            leave_items(hd, "svsv")
 
         make_phi(0)
-        pending = []
-        for g in range(NHEAD // GROUP):
-            heads = list(range(g * GROUP, (g + 1) * GROUP))
-            sin_phase(heads, pending)
-            if g + 1 < NHEAD // GROUP:
-                make_phi((g + 1) * GROUP // H)
-            pending = exp_phase(heads)
-        for f in pending:
-            f()
+        fills = [k for k in range(len(items)) if items[k][0] is not None]
+        filled = 0
+        for k, (fill, use, needs) in enumerate(items):
+            if fill is not None:
+                rank = fills.index(k)
+                while filled < min(len(fills), rank + 1 + AHEAD):
+                    needs = items[fills[filled]][2]
+                    if needs is not None and "eq" not in st[needs]:
+                        break
+                    items[fills[filled]][0]()
+                    filled += 1
+            use()

@@ -20,14 +20,16 @@ B, S, H, DK, NW = 8, 512, 2, 512, 8
 T = 4
 NHEAD = B * H
 GROUP = 8
+SOON = 3
 SKEW = 2
 AHEAD = 4
+EARLY_AT = {(0, 0): 1, (0, 2): 2, (0, 4): 3, (8, 0): 8, (8, 2): 9}
+EARLY_X = (0, 1, 2, 3, 8, 9)
 ORDER = (7, 0, 1, 2, 3, 4, 5, 6)
 
 TWO_PI_1 = 6.28125
-TWO_PI_2 = 0.0019350051879882812
-TWO_PI_3 = 2.0 * math.pi - TWO_PI_1 - TWO_PI_2
-HALF_PI_BELOW = 1.5707962512969971
+TWO_PI_2 = 2.0 * math.pi - TWO_PI_1
+PI_BELOW = 3.1415925025939941
 
 
 def col(b, t, h, w):
@@ -51,39 +53,50 @@ def tile_quantumkernelattention_t_kernel(tc, x, out):
         xs = {}
 
         def load_x(b):
-            xs[b] = work.tile([P, T, H * DK], BF16, name="xs", bufs=5)
+            xs[b] = work.tile([P, T, H * DK], BF16, name="xs", bufs=4)
             nc.sync.dma_start(out=xs[b][:], in_=x[b].rearrange("(p t) e -> p t e", t=T))
 
-        for b in range(5):
+        for b in range(4):
             load_x(b)
 
         ident = const.tile([P, P], F32, name="ident")
         make_identity(nc, ident[:])
         negone = const.tile([P, 1], F32, name="negone")
         nc.vector.memset(negone[:], -1.0)
+        warm = const.tile([P, 1], F32, name="warm")
+        nc.scalar.activation(out=warm[:], in_=negone[:], func=ACT.Sin)
 
         NC = B * 64
         k32 = work.tile([P, NC], I32, name="k32", tag="sw", bufs=10)
-        nc.vector.tensor_scalar(out=k32[:], in0=xf[:], scalar1=1.0 / (2.0 * math.pi), scalar2=None, op0=ALU.mult)
-        kf = work.tile([P, NC], F32, name="kf", tag="sw", bufs=10)
-        nc.vector.tensor_copy(out=kf[:], in_=k32[:])
         t1 = work.tile([P, NC], F32, name="t1", tag="sw", bufs=10)
-        nc.vector.scalar_tensor_tensor(out=t1[:], in0=kf[:], scalar=-TWO_PI_1, in1=xf[:], op0=ALU.mult, op1=ALU.add)
         t2 = work.tile([P, NC], F32, name="t2", tag="sw", bufs=10)
-        nc.vector.scalar_tensor_tensor(out=t2[:], in0=kf[:], scalar=-TWO_PI_2, in1=t1[:], op0=ALU.mult, op1=ALU.add)
-        nc.vector.scalar_tensor_tensor(out=t1[:], in0=kf[:], scalar=-TWO_PI_3, in1=t2[:], op0=ALU.mult, op1=ALU.add)
-        nc.vector.tensor_scalar(out=t2[:], in0=t1[:], scalar1=0.5, scalar2=HALF_PI_BELOW, op0=ALU.mult, op1=ALU.min)
         ang = const.tile([P, NC], F32, name="ang")
-        nc.vector.tensor_scalar(out=ang[:], in0=t2[:], scalar1=-HALF_PI_BELOW, scalar2=None, op0=ALU.max)
-        nc.vector.tensor_scalar(out=t2[:], in0=ang[:], scalar1=math.pi / 2.0, scalar2=None, op0=ALU.add)
-        nc.vector.tensor_scalar(out=t1[:], in0=ang[:], scalar1=0.0, scalar2=math.pi, op0=ALU.is_ge, op1=ALU.mult)
+        tab = const.tile([P, NC], F32, name="tab")
         bias = const.tile([P, NC], F32, name="bias")
-        nc.vector.scalar_tensor_tensor(
-            out=bias[:], in0=t1[:], scalar=-math.pi / 2.0, in1=ang[:], op0=ALU.add, op1=ALU.subtract
-        )
+        halves = (slice(0, NC // 2), slice(NC // 2, NC))
+        for c in halves:
+            nc.vector.tensor_scalar(out=k32[:, c], in0=xf[:, c], scalar1=1.0 / (2.0 * math.pi), scalar2=None, op0=ALU.mult)
+        for c in halves:
+            nc.vector.scalar_tensor_tensor(
+                out=t1[:, c], in0=k32[:, c], scalar=-TWO_PI_1, in1=xf[:, c], op0=ALU.mult, op1=ALU.add
+            )
+        for c in halves:
+            nc.vector.scalar_tensor_tensor(
+                out=t2[:, c], in0=k32[:, c], scalar=-TWO_PI_2, in1=t1[:, c], op0=ALU.mult, op1=ALU.add
+            )
+        for c in halves:
+            nc.vector.tensor_scalar(out=ang[:, c], in0=t2[:, c], scalar1=PI_BELOW, scalar2=-PI_BELOW, op0=ALU.min, op1=ALU.max)
+        for c in halves:
+            nc.vector.tensor_scalar(out=tab[:, c], in0=ang[:, c], scalar1=-math.pi, scalar2=None, op0=ALU.add)
+        for c in halves:
+            nc.vector.tensor_scalar(out=t1[:, c], in0=ang[:, c], scalar1=0.0, scalar2=math.pi, op0=ALU.is_ge, op1=ALU.mult)
+        for c in halves:
+            nc.vector.scalar_tensor_tensor(
+                out=bias[:, c], in0=ang[:, c], scalar=-0.5, in1=t1[:, c], op0=ALU.mult, op1=ALU.add
+            )
         cs = work.tile([P, 2, NC], F32, name="cs", tag="e", bufs=4)
-        nc.scalar.activation(out=cs[:, 1, :], in_=ang[:], func=ACT.Sin)
-        nc.scalar.activation(out=cs[:, 0, :], in_=t2[:], func=ACT.Sin)
+        nc.scalar.activation(out=cs[:, 1, :], in_=ang[:], func=ACT.Sin, scale=0.5)
+        nc.scalar.activation(out=cs[:, 0, :], in_=tab[:], func=ACT.Sin, scale=0.5)
         NK = B * T * H
         cs4 = cs[:].rearrange("p c (k w) -> p k c w", w=NW)
 
@@ -96,17 +109,19 @@ def tile_quantumkernelattention_t_kernel(tc, x, out):
                 op=ALU.mult,
             )
 
-        pair = []
-        for q in range(3):
-            pq = work.tile([P, NK, 2, 2], F32, name="pair%d" % q, tag="pr", bufs=5)
-            outer(pq[:], cs4[:, :, :, 2 * q], 2, cs4[:, :, :, 2 * q + 1], 2)
-            pair.append(pq[:].rearrange("p k i j -> p k (i j)"))
         f16 = const.tile([P, NK, 4, 4], F32, name="f16")
-        outer(f16[:], pair[0], 4, pair[1], 4)
         f8 = const.tile([P, NK, 4, 2], F32, name="f8")
-        outer(f8[:], pair[2], 4, cs4[:, :, :, 6], 2)
         f16v = f16[:].rearrange("p k a c -> p k (a c)")
         f8v = f8[:].rearrange("p k a c -> p k (a c)")
+
+        def small_products():
+            pair = []
+            for q in range(3):
+                pq = work.tile([P, NK, 2, 2], F32, name="pair%d" % q, tag="pr", bufs=5)
+                outer(pq[:], cs4[:, :, :, 2 * q], 2, cs4[:, :, :, 2 * q + 1], 2)
+                pair.append(pq[:].rearrange("p k i j -> p k (i j)"))
+            outer(f16[:], pair[0], 4, pair[1], 4)
+            outer(f8[:], pair[2], 4, cs4[:, :, :, 6], 2)
 
         phi = {}
 
@@ -134,7 +149,7 @@ def tile_quantumkernelattention_t_kernel(tc, x, out):
             for t in range(T):
                 c = col(b, t, h, ORDER[j])
                 nc.tensor.transpose(
-                    out=tl[:, t * P : (t + 1) * P], in_=ang[:, c : c + 1].to_broadcast([P, P]), identity=ident[:]
+                    out=tl[:, t * P : (t + 1) * P], in_=tab[:, c : c + 1].to_broadcast([P, P]), identity=ident[:]
                 )
             st[hd]["tab"] = st[hd].get("tab", []) + [tl]
 
@@ -145,7 +160,7 @@ def tile_quantumkernelattention_t_kernel(tc, x, out):
             w = ORDER[j]
             sw = work.tile([P, 512], F32, name="sw", bufs=10)
             c = col(b, 0, h, w)
-            nc.scalar.activation(out=sw[:], in_=tl[:], func=ACT.Sin, bias=bias[:, c : c + 1])
+            nc.scalar.activation(out=sw[:], in_=tl[:], func=ACT.Sin, bias=bias[:, c : c + 1], scale=0.5)
             d["s"][j] = sw
             if j == 0:
                 d["ab"] = work.tile([P, 1280], F32, name="ab", bufs=GROUP + 1)
@@ -153,7 +168,7 @@ def tile_quantumkernelattention_t_kernel(tc, x, out):
                 for (t, o0, n) in ((1, 0, 384), (3, 384, 128), (2, 512, 256)):
                     c = col(b, t, h, w)
                     nc.scalar.activation(
-                        out=c7[:, o0 : o0 + n], in_=tl[:, 512 - n : 512], func=ACT.Sin, bias=bias[:, c : c + 1]
+                        out=c7[:, o0 : o0 + n], in_=tl[:, 512 - n : 512], func=ACT.Sin, bias=bias[:, c : c + 1], scale=0.5
                     )
                 d["c7"] = c7
 
@@ -200,9 +215,9 @@ def tile_quantumkernelattention_t_kernel(tc, x, out):
             d = st[hd]
             mul(d["ab"][:, 0:512], d["q0"][:], d["q1"][:])
 
-        def magnitude(hd):
-            ab = st[hd]["ab"]
-            nc.vector.scalar_tensor_tensor(out=ab[:], in0=ab[:], scalar=-1.0, in1=ab[:], op0=ALU.mult, op1=ALU.max)
+        def magnitude(hd, lo, hi):
+            ab = st[hd]["ab"][:, lo:hi]
+            nc.vector.scalar_tensor_tensor(out=ab, in0=ab, scalar=-1.0, in1=ab, op0=ALU.mult, op1=ALU.max)
 
         def mirror_a(hd):
             ab = st[hd]["ab"]
@@ -249,8 +264,8 @@ def tile_quantumkernelattention_t_kernel(tc, x, out):
             )
 
         def quantise(name, grouped):
-            codes = work.tile([P, 512], U32, name=name + "_codes", bufs=SKEW + 2, align_bytes=64)
-            scales = work.tile([P, 512], U8, name=name + "_scales", bufs=SKEW + 2, align_bytes=64)
+            codes = work.tile([P, 512], U32, name=name + "_codes", bufs=SKEW + 4, align_bytes=64)
+            scales = work.tile([P, 512], U8, name=name + "_scales", bufs=SKEW + 4, align_bytes=64)
             nc.vector.quantize_mx(
                 out=codes[:].bitcast(FP8X4), scales=scales[:], in_=grouped[:].rearrange("p w t -> p (w t)")
             )
@@ -260,8 +275,8 @@ def tile_quantumkernelattention_t_kernel(tc, x, out):
             b, h = divmod(hd, H)
             st[hd]["xg"] = work.tile([P, DK, T], BF16, name="xg", bufs=2, align_bytes=64)
             regroup(st[hd]["xg"], xs[b][:, :, h * DK : (h + 1) * DK])
-            if h == 1 and b + 5 < B:
-                load_x(b + 5)
+            if h == 1 and b + 4 < B:
+                load_x(b + 4)
 
         def regroup_e(hd):
             st[hd]["eg"] = work.tile([P, S, T], BF16, name="eg", bufs=2, align_bytes=64)
@@ -301,23 +316,21 @@ def tile_quantumkernelattention_t_kernel(tc, x, out):
             )
             d["o"][t] = o
 
+        def store(hd, t, res):
+            b, h = divmod(hd, H)
+            nc.sync.dma_start(out=out[b].rearrange("(p t) e -> p t e", t=T)[:, t, h * DK : (h + 1) * DK], in_=res[:])
+
         def leave_scalar(hd, t):
             d = st[hd]
-            if t == 0:
-                d["res"] = work.tile([P, T, DK], F32, name="res", bufs=3)
-            nc.scalar.activation(out=d["res"][:, t, :], in_=d["o"][t][:], func=ACT.Copy, scale=d["rc"][:, t : t + 1])
+            res = work.tile([P, DK], F32, name="res", bufs=8)
+            nc.scalar.activation(out=res[:], in_=d["o"][t][:], func=ACT.Copy, scale=d["rc"][:, t : t + 1])
+            store(hd, t, res)
 
         def leave_vector(hd, t):
             d = st[hd]
-            nc.vector.tensor_scalar(
-                out=d["res"][:, t, :], in0=d["o"][t][:], scalar1=d["rc"][:, t : t + 1], scalar2=None, op0=ALU.mult
-            )
-
-        def store(hd):
-            b, h = divmod(hd, H)
-            nc.sync.dma_start(
-                out=out[b].rearrange("(p t) e -> p t e", t=T)[:, :, h * DK : (h + 1) * DK], in_=st[hd]["res"][:]
-            )
+            res = work.tile([P, DK], F32, name="res", bufs=8)
+            nc.vector.tensor_scalar(out=res[:], in0=d["o"][t][:], scalar1=d["rc"][:, t : t + 1], scalar2=None, op0=ALU.mult)
+            store(hd, t, res)
 
         items = []
 
@@ -330,10 +343,19 @@ def tile_quantumkernelattention_t_kernel(tc, x, out):
         def leave_items(hd, engines):
             for t in range(T):
                 banked(product, leave_scalar if engines[t] == "s" else leave_vector, hd, t)
-            plain(store, hd)
+
+        xdone = []
+
+        def x_regroup(hd):
+            xdone.append(hd)
+            plain(regroup_x, hd)
 
         groups = [list(range(g * GROUP, (g + 1) * GROUP)) for g in range(NHEAD // GROUP)]
         late = []
+        x_regroup(0)
+        plain(small_products)
+        plain(quantise_x, 0)
+        plain(make_phi, 0)
         for g, heads in enumerate(groups):
             n = len(heads)
             for i, hd in enumerate(heads):
@@ -346,10 +368,16 @@ def tile_quantumkernelattention_t_kernel(tc, x, out):
                             plain(quad_product, pv, 1)
                             plain(blocks_b, hd)
                             plain(row_product, pv)
+                    if (hd, j) in EARLY_AT:
+                        x_regroup(EARLY_AT[(hd, j)])
+                    if (hd, j - 1) in EARLY_AT:
+                        plain(quantise_x, EARLY_AT[(hd, j - 1)])
                     if j == 1:
                         plain(pair_product, hd, 0)
-                        if pv is not None:
-                            plain(magnitude, pv)
+                        if pv is not None and i - 1 < SOON:
+                            plain(magnitude, pv, 0, 512)
+                    if j == 2 and i > 0:
+                        plain(magnitude, hd, 512, 1280)
                     if j == 2 and i == 0:
                         banked(features_t, seven, hd)
                     if j == 2 and late:
@@ -367,6 +395,8 @@ def tile_quantumkernelattention_t_kernel(tc, x, out):
                     if j == 5:
                         plain(pair_product, hd, 2)
                         plain(quad_product, hd, 0)
+                        if i == 0:
+                            plain(magnitude, hd, 512, 1280)
                     if j == 7:
                         plain(pair_product, hd, 3)
             last = heads[-1]
@@ -378,7 +408,9 @@ def tile_quantumkernelattention_t_kernel(tc, x, out):
                 plain(expo_a, hd)
                 if i == 0:
                     plain(quad_product, last, 1)
-                plain(regroup_x, hd)
+                own_x = hd not in xdone
+                if own_x:
+                    x_regroup(hd)
                 if i == 0:
                     plain(row_product, last)
                 if i + 1 < n:
@@ -388,14 +420,12 @@ def tile_quantumkernelattention_t_kernel(tc, x, out):
                     plain(mirror_a, heads[i + 2])
                 plain(expo_c, hd)
                 if prev is not None:
-                    for t in range(3):
-                        banked(product, leave_scalar, prev, t)
-                    banked(product, leave_vector, prev, 3)
-                    plain(store, prev)
+                    leave_items(prev, "ssvv" if prev in EARLY_X else "sssv")
                 plain(regroup_e, hd)
-                if i == 0:
-                    plain(magnitude, last)
-                plain(quantise_x, hd)
+                if i + SOON < n:
+                    plain(magnitude, heads[i + SOON], 0, 512)
+                if own_x:
+                    plain(quantise_x, hd)
                 plain(row_sums, hd)
                 plain(quantise_e, hd)
                 plain(inverse, hd)
@@ -403,7 +433,6 @@ def tile_quantumkernelattention_t_kernel(tc, x, out):
         for hd in late:
             leave_items(hd, "svsv")
 
-        make_phi(0)
         fills = [k for k in range(len(items)) if items[k][0] is not None]
         filled = 0
         for k, (fill, use, needs) in enumerate(items):

@@ -25,6 +25,7 @@ SKEW = 2
 AHEAD = 4
 EARLY_AT = {(0, 0): 1, (0, 2): 2, (0, 4): 3, (8, 0): 8, (8, 2): 9}
 EARLY_X = (0, 1, 2, 3, 8, 9)
+PIECES = (("f7a", 0, 0, 0), ("f7a", 128, 0, 1), ("f7a", 256, 0, 2), ("f7a", 384, 2, 2), ("f7b", 0, 1, 1), ("f7b", 128, 1, 2))
 ORDER = (7, 0, 1, 2, 3, 4, 5, 6)
 
 TWO_PI_1 = 6.28125
@@ -189,9 +190,18 @@ def tile_quantumkernelattention_t_kernel(tc, x, out):
             nc.scalar.copy(out=pht[:], in_=d["pt"][:, 0 : 3 * P])
             d["f7a"] = side_bank()
             d["f7b"] = side_bank()
-            nc.tensor.matmul(out=d["f7a"][:, 0:384], lhsT=pht[:, 0:128], rhs=pht[:, 0:384], start=True, stop=True)
-            nc.tensor.matmul(out=d["f7a"][:, 384:512], lhsT=pht[:, 256:384], rhs=pht[:, 256:384], start=True, stop=True)
-            nc.tensor.matmul(out=d["f7b"][:, 0:256], lhsT=pht[:, 128:256], rhs=pht[:, 128:384], start=True, stop=True)
+            d["pht"] = pht
+
+        def seven_block(hd, q):
+            d = st[hd]
+            name, dst, row, c = PIECES[q]
+            nc.tensor.matmul(
+                out=d[name][:, dst : dst + P],
+                lhsT=d["pht"][:, row * P : (row + 1) * P],
+                rhs=d["pht"][:, c * P : (c + 1) * P],
+                start=True,
+                stop=True,
+            )
 
         def blocks_a(hd):
             d = st[hd]
@@ -358,45 +368,53 @@ def tile_quantumkernelattention_t_kernel(tc, x, out):
         plain(make_phi, 0)
         for g, heads in enumerate(groups):
             n = len(heads)
+            todo = {}
+
+            def at(step, f, *a):
+                todo[step] = todo.get(step, []) + [(f, a)]
+
+            joined = 0
+            for i, hd in enumerate(heads):
+                copy_at = 2 if i == 0 else max(NW * (i - 1) + 1, joined + 1)
+                at(copy_at, None, hd)
+                for q in range(len(PIECES)):
+                    at(copy_at + (q // 2 if i == 0 else q), seven_block, hd, q)
+                joined = max(copy_at + (3 if i == 0 else len(PIECES)), NW * i)
+                at(joined, blocks_a, hd)
+                at(joined, blocks_b, hd)
+                at(joined + 2, magnitude, hd, 512, 1280)
             for i, hd in enumerate(heads):
                 pv = heads[i - 1] if i > 0 else None
                 for j in range(NW):
                     banked(spread, sines, hd, j)
-                    if j == 0:
-                        if pv is not None:
-                            plain(blocks_a, hd)
-                            plain(quad_product, pv, 1)
-                            plain(blocks_b, hd)
-                            plain(row_product, pv)
+                    for (f, a) in todo.get(NW * i + j, []):
+                        if f is None:
+                            banked(features_t, seven, a[0])
+                        else:
+                            plain(f, *a)
+                    if j == 0 and pv is not None:
+                        plain(quad_product, pv, 1)
                     if (hd, j) in EARLY_AT:
                         x_regroup(EARLY_AT[(hd, j)])
                     if (hd, j - 1) in EARLY_AT:
                         plain(quantise_x, EARLY_AT[(hd, j - 1)])
                     if j == 1:
                         plain(pair_product, hd, 0)
-                        if pv is not None and i - 1 < SOON:
-                            plain(magnitude, pv, 0, 512)
-                    if j == 2 and i > 0:
-                        plain(magnitude, hd, 512, 1280)
-                    if j == 2 and i == 0:
-                        banked(features_t, seven, hd)
+                        if pv is not None:
+                            plain(row_product, pv)
                     if j == 2 and late:
                         leave_items(late.pop(0), "sssv")
                     if j == 3:
-                        if i == 0:
-                            plain(blocks_a, hd)
                         plain(pair_product, hd, 1)
-                        if i == 0:
-                            plain(blocks_b, hd)
-                        if hd % 2 == 0 and hd + 2 < NHEAD:
-                            plain(make_phi, hd // 2 + 1)
-                    if j == 4 and i + 1 < n:
-                        banked(features_t, seven, heads[i + 1])
+                        if pv is not None and i - 1 < SOON:
+                            plain(magnitude, pv, 0, 512)
+                        if hd == 0:
+                            plain(make_phi, 1)
+                        if hd % 2 == 1 and (hd + 3) // 2 < B:
+                            plain(make_phi, (hd + 3) // 2)
                     if j == 5:
                         plain(pair_product, hd, 2)
                         plain(quad_product, hd, 0)
-                        if i == 0:
-                            plain(magnitude, hd, 512, 1280)
                     if j == 7:
                         plain(pair_product, hd, 3)
             last = heads[-1]

@@ -4,7 +4,8 @@ from contextlib import ExitStack
 import concourse.mybir as mybir
 from concourse.masks import make_identity
 
-FLOPS = 2 * 8 * 2 * 512 * 512 * 512
+B, S, H, DK, NW = 8, 512, 2, 512, 8
+FLOPS = 2 * B * H * S * S * DK
 
 F32 = mybir.dt.float32
 BF16 = mybir.dt.bfloat16
@@ -16,24 +17,22 @@ ALU = mybir.AluOpType
 ACT = mybir.ActivationFunctionType
 
 P = 128
-B, S, H, DK, NW = 8, 512, 2, 512, 8
 T = 4
-NHEAD = B * H
 GROUP = 8
-SOON = 3
-SKEW = 2
 AHEAD = 4
-EARLY_AT = {(0, 0): 1, (0, 2): 2, (0, 4): 3, (8, 0): 8, (8, 2): 9}
-EARLY_X = (0, 1, 2, 3, 8, 9)
-PIECES = (("f7a", 0, 0, 0), ("f7a", 128, 0, 1), ("f7a", 256, 0, 2), ("f7a", 384, 2, 2), ("f7b", 0, 1, 1), ("f7b", 128, 1, 2))
+EARLY = 3
+TWOS = 5
+SINES = 10
+LAG = 2
 ORDER = (7, 0, 1, 2, 3, 4, 5, 6)
-
-TWO_PI_1 = 6.28125
-TWO_PI_2 = 2.0 * math.pi - TWO_PI_1
+ROW = (0, 512, 1024, 896)
+BLOCKS = 1280
+TWO_PI_HIGH = 6.28125
+TWO_PI_LOW = 2.0 * math.pi - TWO_PI_HIGH
 PI_BELOW = 3.1415925025939941
 
 
-def col(b, t, h, w):
+def column(b, t, h, w):
     return ((b * T + t) * H + h) * NW + w
 
 
@@ -45,421 +44,393 @@ def tile_quantumkernelattention_t_kernel(tc, x, out):
         work = ctx.enter_context(tc.tile_pool(name="work", bufs=2))
         psum = ctx.enter_context(tc.psum_pool(name="psum", bufs=1))
 
-        xf = const.tile([P, B * 64], BF16, name="xf")
+        NCOL = B * T * H * NW
+        first8 = const.tile([P, NCOL], BF16, name="first8")
+        per_batch = T * H * NW
         for b in range(B):
             nc.sync.dma_start(
-                out=xf[:, b * 64 : (b + 1) * 64].rearrange("p (k w) -> p k w", w=NW),
+                out=first8[:, b * per_batch : (b + 1) * per_batch].rearrange("p (k w) -> p k w", w=NW),
                 in_=x[b].rearrange("(p t) (h d) -> p (t h) d", t=T, h=H)[:, :, 0:NW],
             )
-        xs = {}
+        X_BUFS = 4
+        x_tile = {}
 
         def load_x(b):
-            xs[b] = work.tile([P, T, H * DK], BF16, name="xs", bufs=4)
-            nc.sync.dma_start(out=xs[b][:], in_=x[b].rearrange("(p t) e -> p t e", t=T))
+            x_tile[b] = work.tile([P, T, H * DK], BF16, name="x_tile", bufs=X_BUFS)
+            nc.sync.dma_start(out=x_tile[b][:], in_=x[b].rearrange("(p t) e -> p t e", t=T))
 
-        for b in range(4):
+        for b in range(X_BUFS):
             load_x(b)
 
-        ident = const.tile([P, P], F32, name="ident")
-        make_identity(nc, ident[:])
-        negone = const.tile([P, 1], F32, name="negone")
-        nc.vector.memset(negone[:], -1.0)
+        identity = const.tile([P, P], F32, name="identity")
+        make_identity(nc, identity[:])
+        minus_one = const.tile([P, 1], F32, name="minus_one")
+        nc.vector.memset(minus_one[:], -1.0)
         warm = const.tile([P, 1], F32, name="warm")
-        nc.scalar.activation(out=warm[:], in_=negone[:], func=ACT.Sin)
+        nc.scalar.activation(out=warm[:], in_=minus_one[:], func=ACT.Sin)
 
-        NC = B * 64
-        k32 = work.tile([P, NC], I32, name="k32", tag="sw", bufs=10)
-        t1 = work.tile([P, NC], F32, name="t1", tag="sw", bufs=10)
-        t2 = work.tile([P, NC], F32, name="t2", tag="sw", bufs=10)
-        ang = const.tile([P, NC], F32, name="ang")
-        tab = const.tile([P, NC], F32, name="tab")
-        bias = const.tile([P, NC], F32, name="bias")
-        halves = (slice(0, NC // 2), slice(NC // 2, NC))
+        turns = work.tile([P, NCOL], I32, name="turns", tag="sine", bufs=SINES)
+        part = work.tile([P, NCOL], F32, name="part", tag="sine", bufs=SINES)
+        full = work.tile([P, NCOL], F32, name="full", tag="sine", bufs=SINES)
+        twice = const.tile([P, NCOL], F32, name="twice")
+        spreadable = const.tile([P, NCOL], F32, name="spreadable")
+        bias = const.tile([P, NCOL], F32, name="bias")
+        halves = (slice(0, NCOL // 2), slice(NCOL // 2, NCOL))
         for c in halves:
-            nc.vector.tensor_scalar(out=k32[:, c], in0=xf[:, c], scalar1=1.0 / (2.0 * math.pi), scalar2=None, op0=ALU.mult)
-        for c in halves:
-            nc.vector.scalar_tensor_tensor(
-                out=t1[:, c], in0=k32[:, c], scalar=-TWO_PI_1, in1=xf[:, c], op0=ALU.mult, op1=ALU.add
+            nc.vector.tensor_scalar(
+                out=turns[:, c], in0=first8[:, c], scalar1=1.0 / (2.0 * math.pi), scalar2=None, op0=ALU.mult
             )
         for c in halves:
             nc.vector.scalar_tensor_tensor(
-                out=t2[:, c], in0=k32[:, c], scalar=-TWO_PI_2, in1=t1[:, c], op0=ALU.mult, op1=ALU.add
+                out=part[:, c], in0=turns[:, c], scalar=-TWO_PI_HIGH, in1=first8[:, c], op0=ALU.mult, op1=ALU.add
             )
-        for c in halves:
-            nc.vector.tensor_scalar(out=ang[:, c], in0=t2[:, c], scalar1=PI_BELOW, scalar2=-PI_BELOW, op0=ALU.min, op1=ALU.max)
-        for c in halves:
-            nc.vector.tensor_scalar(out=tab[:, c], in0=ang[:, c], scalar1=-math.pi, scalar2=None, op0=ALU.add)
-        for c in halves:
-            nc.vector.tensor_scalar(out=t1[:, c], in0=ang[:, c], scalar1=0.0, scalar2=math.pi, op0=ALU.is_ge, op1=ALU.mult)
         for c in halves:
             nc.vector.scalar_tensor_tensor(
-                out=bias[:, c], in0=ang[:, c], scalar=-0.5, in1=t1[:, c], op0=ALU.mult, op1=ALU.add
+                out=full[:, c], in0=turns[:, c], scalar=-TWO_PI_LOW, in1=part[:, c], op0=ALU.mult, op1=ALU.add
             )
-        cs = work.tile([P, 2, NC], F32, name="cs", tag="e", bufs=4)
-        nc.scalar.activation(out=cs[:, 1, :], in_=ang[:], func=ACT.Sin, scale=0.5)
-        nc.scalar.activation(out=cs[:, 0, :], in_=tab[:], func=ACT.Sin, scale=0.5)
-        NK = B * T * H
-        cs4 = cs[:].rearrange("p c (k w) -> p k c w", w=NW)
+        for c in halves:
+            nc.vector.tensor_scalar(
+                out=twice[:, c], in0=full[:, c], scalar1=PI_BELOW, scalar2=-PI_BELOW, op0=ALU.min, op1=ALU.max
+            )
+        for c in halves:
+            nc.vector.tensor_scalar(out=spreadable[:, c], in0=twice[:, c], scalar1=-math.pi, scalar2=None, op0=ALU.add)
+        for c in halves:
+            nc.vector.tensor_scalar(
+                out=part[:, c], in0=twice[:, c], scalar1=0.0, scalar2=math.pi, op0=ALU.is_ge, op1=ALU.mult
+            )
+        for c in halves:
+            nc.vector.scalar_tensor_tensor(
+                out=bias[:, c], in0=twice[:, c], scalar=-0.5, in1=part[:, c], op0=ALU.mult, op1=ALU.add
+            )
+        trig = work.tile([P, 2, NCOL], F32, name="trig", tag="e", bufs=LAG + 2)
+        nc.scalar.activation(out=trig[:, 1, :], in_=twice[:], func=ACT.Sin, scale=0.5)
+        nc.scalar.activation(out=trig[:, 0, :], in_=spreadable[:], func=ACT.Sin, scale=0.5)
+        NTOK = B * T * H
+        by_feature = trig[:].rearrange("p c (k w) -> p k c w", w=NW)
 
-        def outer(dst, left, nl, right, nr):
-            nk = dst.shape[1]
+        def outer(dst, left, n_left, right, n_right):
+            shape = [P, dst.shape[1], n_left, n_right]
             nc.vector.tensor_tensor(
-                out=dst,
-                in0=left.unsqueeze(3).to_broadcast([P, nk, nl, nr]),
-                in1=right.unsqueeze(2).to_broadcast([P, nk, nl, nr]),
-                op=ALU.mult,
+                out=dst, in0=left.unsqueeze(3).to_broadcast(shape), in1=right.unsqueeze(2).to_broadcast(shape), op=ALU.mult
             )
 
-        f16 = const.tile([P, NK, 4, 4], F32, name="f16")
-        f8 = const.tile([P, NK, 4, 2], F32, name="f8")
-        f16v = f16[:].rearrange("p k a c -> p k (a c)")
-        f8v = f8[:].rearrange("p k a c -> p k (a c)")
+        pairs = []
+        for q in range(3):
+            pair = work.tile([P, NTOK, 2, 2], F32, name="pair%d" % q, tag="two", bufs=TWOS)
+            outer(pair[:], by_feature[:, :, :, 2 * q], 2, by_feature[:, :, :, 2 * q + 1], 2)
+            pairs.append(pair[:].rearrange("p k i j -> p k (i j)"))
+        sixteen = const.tile([P, NTOK, 4, 4], F32, name="sixteen")
+        outer(sixteen[:], pairs[0], 4, pairs[1], 4)
+        eight = const.tile([P, NTOK, 4, 2], F32, name="eight")
+        outer(eight[:], pairs[2], 4, by_feature[:, :, :, 6], 2)
 
-        def small_products():
-            pair = []
-            for q in range(3):
-                pq = work.tile([P, NK, 2, 2], F32, name="pair%d" % q, tag="pr", bufs=5)
-                outer(pq[:], cs4[:, :, :, 2 * q], 2, cs4[:, :, :, 2 * q + 1], 2)
-                pair.append(pq[:].rearrange("p k i j -> p k (i j)"))
-            outer(f16[:], pair[0], 4, pair[1], 4)
-            outer(f8[:], pair[2], 4, cs4[:, :, :, 6], 2)
+        terms = {}
 
-        phi = {}
+        def make_terms(b):
+            terms[b] = work.tile([P, (T - 1) * H, 16, 8], F32, name="terms", bufs=2)
+            k = (b * T + 1) * H
+            outer(
+                terms[b][:],
+                sixteen[:, k : k + (T - 1) * H].rearrange("p k i j -> p k (i j)"),
+                16,
+                eight[:, k : k + (T - 1) * H].rearrange("p k i j -> p k (i j)"),
+                8,
+            )
 
-        def make_phi(b):
-            phi[b] = work.tile([P, 6, 16, 8], F32, name="phi", bufs=2)
-            k0 = b * T * H + H
-            outer(phi[b][:], f16v[:, k0 : k0 + 6, :], 16, f8v[:, k0 : k0 + 6, :], 8)
-
-        st = {}
-        for hd in range(NHEAD):
-            st[hd] = {"s": {}, "p": {}, "o": {}}
-
-        def bank():
-            return psum.tile([P, 512], F32, name="a", tag="A", bufs=AHEAD + 1)
+        def queue_bank():
+            return psum.tile([P, 512], F32, name="queue", tag="queue", bufs=AHEAD + 1)
 
         def side_bank():
-            return psum.tile([P, 512], F32, name="b", tag="B", bufs=3)
+            return psum.tile([P, 512], F32, name="side", tag="side", bufs=3)
 
-        def mul(dst, a, c):
+        def multiply(dst, a, c):
             nc.vector.tensor_tensor(out=dst, in0=a, in1=c, op=ALU.mult)
+
+        table = {}
+        sine = {}
+        score = {}
 
         def spread(hd, j):
             b, h = divmod(hd, H)
-            tl = bank()
-            for t in range(T):
-                c = col(b, t, h, ORDER[j])
+            table[hd, j] = queue_bank()
+            for u in range(T):
+                c = column(b, u, h, ORDER[j])
                 nc.tensor.transpose(
-                    out=tl[:, t * P : (t + 1) * P], in_=tab[:, c : c + 1].to_broadcast([P, P]), identity=ident[:]
+                    out=table[hd, j][:, u * P : (u + 1) * P],
+                    in_=spreadable[:, c : c + 1].to_broadcast([P, P]),
+                    identity=identity[:],
                 )
-            st[hd]["tab"] = st[hd].get("tab", []) + [tl]
 
-        def sines(hd, j):
+        def take_sines(hd, j):
             b, h = divmod(hd, H)
-            d = st[hd]
-            tl = d["tab"].pop(0)
-            w = ORDER[j]
-            sw = work.tile([P, 512], F32, name="sw", bufs=10)
-            c = col(b, 0, h, w)
-            nc.scalar.activation(out=sw[:], in_=tl[:], func=ACT.Sin, bias=bias[:, c : c + 1], scale=0.5)
-            d["s"][j] = sw
+            angles = table.pop((hd, j))
+            sine[hd, j] = work.tile([P, S], F32, name="sine", bufs=SINES)
+            c = column(b, 0, h, ORDER[j])
+            nc.scalar.activation(out=sine[hd, j][:], in_=angles[:], func=ACT.Sin, bias=bias[:, c : c + 1], scale=0.5)
             if j == 0:
-                d["ab"] = work.tile([P, 1280], F32, name="ab", bufs=GROUP + 1)
-                c7 = work.tile([P, 768], F32, name="c7", bufs=2)
-                for (t, o0, n) in ((1, 0, 384), (3, 384, 128), (2, 512, 256)):
-                    c = col(b, t, h, w)
+                score[hd] = work.tile([P, BLOCKS], F32, name="score", bufs=GROUP + 1)
+                for t in (1, 3, 2):
+                    c = column(b, t, h, ORDER[j])
                     nc.scalar.activation(
-                        out=c7[:, o0 : o0 + n], in_=tl[:, 512 - n : 512], func=ACT.Sin, bias=bias[:, c : c + 1], scale=0.5
+                        out=score[hd][:, ROW[t] : ROW[t] + (T - t) * P],
+                        in_=angles[:, t * P : S],
+                        func=ACT.Sin,
+                        bias=bias[:, c : c + 1],
+                        scale=0.5,
                     )
-                d["c7"] = c7
 
-        def features_t(hd):
+        turned = {}
+        seven = {}
+
+        def turn_terms(hd):
             b, h = divmod(hd, H)
-            tl = bank()
+            turned[hd] = side_bank()
             for t in range(1, T):
                 nc.tensor.transpose(
-                    out=tl[:, (t - 1) * P : t * P],
-                    in_=phi[b][:, (t - 1) * H + h].rearrange("p a c -> p (a c)"),
-                    identity=ident[:],
+                    out=turned[hd][:, (t - 1) * P : t * P],
+                    in_=terms[b][:, (t - 1) * H + h].rearrange("p i j -> p (i j)"),
+                    identity=identity[:],
                 )
-            st[hd]["pt"] = tl
 
-        def seven(hd):
-            d = st[hd]
-            pht = work.tile([P, 3 * P], F32, name="pht", bufs=2)
-            nc.scalar.copy(out=pht[:], in_=d["pt"][:, 0 : 3 * P])
-            d["f7a"] = side_bank()
-            d["f7b"] = side_bank()
-            d["pht"] = pht
+        def seven_cosines(hd):
+            by_token = work.tile([P, (T - 1) * P], F32, name="by_token", bufs=2)
+            nc.scalar.copy(out=by_token[:], in_=turned.pop(hd)[:, 0 : (T - 1) * P])
+            seven[hd] = (side_bank(), side_bank())
+            for (t, bank, at) in ((1, 0, 0), (3, 0, 384), (2, 1, 0)):
+                nc.tensor.matmul(
+                    out=seven[hd][bank][:, at : at + (T - t) * P],
+                    lhsT=by_token[:, (t - 1) * P : t * P],
+                    rhs=by_token[:, (t - 1) * P : (T - 1) * P],
+                    start=True,
+                    stop=True,
+                )
 
-        def seven_block(hd, q):
-            d = st[hd]
-            name, dst, row, c = PIECES[q]
-            nc.tensor.matmul(
-                out=d[name][:, dst : dst + P],
-                lhsT=d["pht"][:, row * P : (row + 1) * P],
-                rhs=d["pht"][:, c * P : (c + 1) * P],
-                start=True,
-                stop=True,
-            )
+        def join_rows_1_3(hd):
+            multiply(score[hd][:, 512:1024], seven[hd][0][:], score[hd][:, 512:1024])
 
-        def blocks_a(hd):
-            d = st[hd]
-            mul(d["ab"][:, 512:1024], d["f7a"][:], d["c7"][:, 0:512])
+        def join_row_2(hd):
+            multiply(score[hd][:, 1024:1280], seven[hd][1][:, 0:256], score[hd][:, 1024:1280])
 
-        def blocks_b(hd):
-            d = st[hd]
-            mul(d["ab"][:, 1024:1280], d["f7b"][:, 0:256], d["c7"][:, 512:768])
+        two = {}
+        four = {}
 
-        def pair_product(hd, q):
-            d = st[hd]
-            d["p"][q] = work.tile([P, 512], F32, name="pr", bufs=5)
-            mul(d["p"][q][:], d["s"].pop(2 * q)[:], d["s"].pop(2 * q + 1)[:])
+        def product_of_two(hd, q):
+            two[hd, q] = work.tile([P, S], F32, name="two", bufs=TWOS)
+            multiply(two[hd, q][:], sine.pop((hd, 2 * q))[:], sine.pop((hd, 2 * q + 1))[:])
 
-        def quad_product(hd, q):
-            d = st[hd]
-            d["q%d" % q] = work.tile([P, 512], F32, name="qd", bufs=4)
-            mul(d["q%d" % q][:], d["p"].pop(2 * q)[:], d["p"].pop(2 * q + 1)[:])
+        def product_of_four(hd, q):
+            four[hd, q] = work.tile([P, S], F32, name="four", bufs=T)
+            multiply(four[hd, q][:], two.pop((hd, 2 * q))[:], two.pop((hd, 2 * q + 1))[:])
 
-        def row_product(hd):
-            d = st[hd]
-            mul(d["ab"][:, 0:512], d["q0"][:], d["q1"][:])
+        def product_of_eight(hd):
+            multiply(score[hd][:, 0:S], four.pop((hd, 0))[:], four.pop((hd, 1))[:])
 
-        def magnitude(hd, lo, hi):
-            ab = st[hd]["ab"][:, lo:hi]
-            nc.vector.scalar_tensor_tensor(out=ab, in0=ab, scalar=-1.0, in1=ab, op0=ALU.mult, op1=ALU.max)
+        def magnitude(hd):
+            s = score[hd][:]
+            nc.vector.scalar_tensor_tensor(out=s, in0=s, scalar=-1.0, in1=s, op0=ALU.mult, op1=ALU.max)
 
-        def mirror_a(hd):
-            ab = st[hd]["ab"]
-            m = side_bank()
-            for (dst, src) in ((0, 384), (128, 768), (256, 1152), (384, 128)):
-                nc.tensor.transpose(out=m[:, dst : dst + P], in_=ab[:, src : src + P], identity=ident[:])
-            st[hd]["ma"] = m
+        mirror = {}
 
-        def mirror_b(hd):
-            ab = st[hd]["ab"]
-            m = side_bank()
-            for (dst, src) in ((0, 256), (128, 640)):
-                nc.tensor.transpose(out=m[:, dst : dst + P], in_=ab[:, src : src + P], identity=ident[:])
-            st[hd]["mb"] = m
+        def mirror_rows_3_1(hd):
+            mirror[hd, 0] = side_bank()
+            for (at, t, u) in ((0, 0, 3), (128, 1, 3), (256, 2, 3), (384, 0, 1)):
+                src = ROW[t] + (u - t) * P
+                nc.tensor.transpose(out=mirror[hd, 0][:, at : at + P], in_=score[hd][:, src : src + P], identity=identity[:])
 
-        def expo(hd, t, lo, n, src, slot):
-            d = st[hd]
+        def mirror_row_2(hd):
+            mirror[hd, 1] = side_bank()
+            for (at, t, u) in ((0, 0, 2), (128, 1, 2)):
+                src = ROW[t] + (u - t) * P
+                nc.tensor.transpose(out=mirror[hd, 1][:, at : at + P], in_=score[hd][:, src : src + P], identity=identity[:])
+
+        e_tile = {}
+        sums = {}
+
+        def exponential(hd, t, lo, n, src, half):
             nc.scalar.activation(
-                out=d["e"][:, t, lo : lo + n], in_=src, func=ACT.Exp, bias=negone[:],
-                accum_out=d["acc"][:, 2 * t + slot : 2 * t + slot + 1],
+                out=e_tile[hd][:, t, lo : lo + n],
+                in_=src,
+                func=ACT.Exp,
+                bias=minus_one[:],
+                accum_out=sums[hd][:, 2 * t + half : 2 * t + half + 1],
             )
 
-        def expo_a(hd):
-            d = st[hd]
-            d["acc"] = work.tile([P, 2 * T], F32, name="acc", bufs=3)
-            d["e"] = work.tile([P, T, S], BF16, name="e", bufs=4)
-            expo(hd, 3, 0, 384, d["ma"][:, 0:384], 0)
-            expo(hd, 1, 0, 128, d["ma"][:, 384:512], 0)
+        def exponentials_of_mirror_3_1(hd):
+            sums[hd] = work.tile([P, 2 * T], F32, name="sums", bufs=LAG + 1)
+            e_tile[hd] = work.tile([P, T, S], BF16, name="e", bufs=LAG + 2)
+            exponential(hd, 3, 0, 384, mirror[hd, 0][:, 0:384], 0)
+            exponential(hd, 1, 0, 128, mirror.pop((hd, 0))[:, 384:512], 0)
 
-        def expo_b(hd):
-            expo(hd, 2, 0, 256, st[hd]["mb"][:, 0:256], 0)
+        def exponentials_of_mirror_2(hd):
+            exponential(hd, 2, 0, 256, mirror.pop((hd, 1))[:, 0:256], 0)
 
-        def expo_c(hd):
-            ab = st[hd]["ab"]
-            expo(hd, 0, 0, 256, ab[:, 0:256], 0)
-            expo(hd, 0, 256, 256, ab[:, 256:512], 1)
-            expo(hd, 1, 128, 384, ab[:, 512:896], 1)
-            expo(hd, 3, 384, 128, ab[:, 896:1024], 1)
-            expo(hd, 2, 256, 256, ab[:, 1024:1280], 1)
+        def exponentials_of_blocks(hd):
+            s = score.pop(hd)
+            exponential(hd, 0, 0, 256, s[:, 0:256], 0)
+            exponential(hd, 0, 256, 256, s[:, 256:512], 1)
+            for t in (1, 3, 2):
+                exponential(hd, t, t * P, (T - t) * P, s[:, ROW[t] : ROW[t] + (T - t) * P], 1)
 
-        def regroup(dst, src):
+        def regroup(name, src):
+            grouped = work.tile([P, 512, T], BF16, name=name, bufs=2, align_bytes=64)
             nc.vector.tensor_copy(
-                out=dst[:].rearrange("p (c i) t -> p c t i", i=4), in_=src.rearrange("p t (c i) -> p c t i", i=4)
+                out=grouped[:].rearrange("p (c i) t -> p c t i", i=4), in_=src.rearrange("p t (c i) -> p c t i", i=4)
             )
+            return grouped
 
         def quantise(name, grouped):
-            codes = work.tile([P, 512], U32, name=name + "_codes", bufs=SKEW + 4, align_bytes=64)
-            scales = work.tile([P, 512], U8, name=name + "_scales", bufs=SKEW + 4, align_bytes=64)
+            codes = work.tile([P, 512], U32, name=name + "_codes", bufs=EARLY + LAG + 2, align_bytes=64)
+            scales = work.tile([P, 512], U8, name=name + "_scales", bufs=EARLY + LAG + 2, align_bytes=64)
             nc.vector.quantize_mx(
-                out=codes[:].bitcast(FP8X4), scales=scales[:], in_=grouped[:].rearrange("p w t -> p (w t)")
+                out=codes[:].bitcast(FP8X4), scales=scales[:], in_=grouped[:].rearrange("p c t -> p (c t)")
             )
             return codes, scales
 
+        grouped_x = {}
+        grouped_e = {}
+        packed_x = {}
+        packed_e = {}
+        total = {}
+        inverse = {}
+
         def regroup_x(hd):
             b, h = divmod(hd, H)
-            st[hd]["xg"] = work.tile([P, DK, T], BF16, name="xg", bufs=2, align_bytes=64)
-            regroup(st[hd]["xg"], xs[b][:, :, h * DK : (h + 1) * DK])
-            if h == 1 and b + 4 < B:
-                load_x(b + 4)
+            grouped_x[hd] = regroup("grouped_x", x_tile[b][:, :, h * DK : (h + 1) * DK])
+            if h == H - 1 and b + X_BUFS < B:
+                load_x(b + X_BUFS)
 
         def regroup_e(hd):
-            st[hd]["eg"] = work.tile([P, S, T], BF16, name="eg", bufs=2, align_bytes=64)
-            regroup(st[hd]["eg"], st[hd]["e"][:])
+            grouped_e[hd] = regroup("grouped_e", e_tile.pop(hd)[:])
 
         def quantise_x(hd):
-            st[hd]["xq"] = quantise("x", st[hd]["xg"])
+            packed_x[hd] = quantise("x", grouped_x.pop(hd))
 
         def quantise_e(hd):
-            st[hd]["eq"] = quantise("e", st[hd]["eg"])
+            packed_e[hd] = quantise("e", grouped_e.pop(hd))
 
-        def row_sums(hd):
-            d = st[hd]
-            d["rs"] = work.tile([P, T], F32, name="rs", bufs=2)
+        def add_sums(hd):
+            total[hd] = work.tile([P, T], F32, name="total", bufs=2)
             nc.vector.tensor_reduce(
-                out=d["rs"][:], in_=d["acc"][:].rearrange("p (t s) -> p t s", s=2), axis=mybir.AxisListType.X, op=ALU.add
+                out=total[hd][:], in_=sums.pop(hd)[:].rearrange("p (t s) -> p t s", s=2), axis=mybir.AxisListType.X, op=ALU.add
             )
 
-        def inverse(hd):
-            d = st[hd]
-            d["rc"] = work.tile([P, T], F32, name="rc", bufs=SKEW + 2)
-            nc.vector.reciprocal(out=d["rc"][:], in_=d["rs"][:])
+        def invert_sums(hd):
+            inverse[hd] = work.tile([P, T], F32, name="inverse", bufs=LAG + 2)
+            nc.vector.reciprocal(out=inverse[hd][:], in_=total.pop(hd)[:])
 
-        def product(hd, t):
-            d = st[hd]
-            ec, es = d["eq"]
-            xc, xsc = d["xq"]
-            o = bank()
+        mx = {}
+
+        def mx_product(hd, u):
+            mx[hd, u] = queue_bank()
             nc.tensor.matmul_mx(
-                out=o[:],
-                lhsT=ec[:, t * P : (t + 1) * P].bitcast(FP8X4),
-                lhsT_scale=es[:, t * P : (t + 1) * P],
-                rhs=xc[:].bitcast(FP8X4),
-                rhs_scale=xsc[:],
+                out=mx[hd, u][:],
+                lhsT=packed_e[hd][0][:, u * P : (u + 1) * P].bitcast(FP8X4),
+                lhsT_scale=packed_e[hd][1][:, u * P : (u + 1) * P],
+                rhs=packed_x[hd][0][:].bitcast(FP8X4),
+                rhs_scale=packed_x[hd][1][:],
                 start=True,
                 stop=True,
             )
-            d["o"][t] = o
 
-        def store(hd, t, res):
+        def divide_and_store(hd, u, on_vector):
             b, h = divmod(hd, H)
-            nc.sync.dma_start(out=out[b].rearrange("(p t) e -> p t e", t=T)[:, t, h * DK : (h + 1) * DK], in_=res[:])
+            result = work.tile([P, DK], F32, name="result", bufs=2 * T)
+            if on_vector:
+                nc.vector.tensor_scalar(
+                    out=result[:], in0=mx.pop((hd, u))[:], scalar1=inverse[hd][:, u : u + 1], scalar2=None, op0=ALU.mult
+                )
+            else:
+                nc.scalar.activation(out=result[:], in_=mx.pop((hd, u))[:], func=ACT.Copy, scale=inverse[hd][:, u : u + 1])
+            nc.sync.dma_start(out=out[b].rearrange("(p t) e -> p t e", t=T)[:, u, h * DK : (h + 1) * DK], in_=result[:])
 
-        def leave_scalar(hd, t):
-            d = st[hd]
-            res = work.tile([P, DK], F32, name="res", bufs=8)
-            nc.scalar.activation(out=res[:], in_=d["o"][t][:], func=ACT.Copy, scale=d["rc"][:, t : t + 1])
-            store(hd, t, res)
+        def sine_phase(heads):
+            steps = [(hd, j) for hd in heads for j in range(NW)]
+            for s in range(AHEAD):
+                spread(*steps[s])
+            for s, (hd, j) in enumerate(steps):
+                if s + AHEAD < len(steps):
+                    spread(*steps[s + AHEAD])
+                take_sines(hd, j)
+                first = hd == heads[0]
+                if j == 0 and not first:
+                    join_rows_1_3(hd)
+                    product_of_four(hd - 1, 1)
+                    join_row_2(hd)
+                    product_of_eight(hd - 1)
+                if j == 1:
+                    product_of_two(hd, 0)
+                    if first:
+                        turn_terms(hd)
+                    else:
+                        magnitude(hd - 1)
+                if j == 3:
+                    product_of_two(hd, 1)
+                    if first:
+                        seven_cosines(hd)
+                    if hd % H == 0 and hd + H < B * H:
+                        make_terms(hd // H + 1)
+                if j == 4 and first:
+                    join_rows_1_3(hd)
+                    join_row_2(hd)
+                if j == 5:
+                    product_of_two(hd, 2)
+                    product_of_four(hd, 0)
+                    if hd != heads[-1]:
+                        turn_terms(hd + 1)
+                if j == 7:
+                    product_of_two(hd, 3)
+                    if hd != heads[-1]:
+                        seven_cosines(hd + 1)
+                if first and j < 2 * EARLY:
+                    if j % 2 == 0:
+                        regroup_x(heads[j // 2])
+                    else:
+                        quantise_x(heads[j // 2])
 
-        def leave_vector(hd, t):
-            d = st[hd]
-            res = work.tile([P, DK], F32, name="res", bufs=8)
-            nc.vector.tensor_scalar(out=res[:], in0=d["o"][t][:], scalar1=d["rc"][:, t : t + 1], scalar2=None, op0=ALU.mult)
-            store(hd, t, res)
-
-        items = []
-
-        def plain(f, *a):
-            items.append((None, lambda: f(*a), None))
-
-        def banked(fill, use, *a):
-            items.append((lambda: fill(*a), lambda: use(*a), a[0] if fill is product else None))
-
-        def leave_items(hd, engines):
-            for t in range(T):
-                banked(product, leave_scalar if engines[t] == "s" else leave_vector, hd, t)
-
-        xdone = []
-
-        def x_regroup(hd):
-            xdone.append(hd)
-            plain(regroup_x, hd)
-
-        groups = [list(range(g * GROUP, (g + 1) * GROUP)) for g in range(NHEAD // GROUP)]
-        late = []
-        x_regroup(0)
-        plain(small_products)
-        plain(quantise_x, 0)
-        plain(make_phi, 0)
-        for g, heads in enumerate(groups):
+        def exponential_phase(heads, sines_follow):
             n = len(heads)
-            todo = {}
-
-            def at(step, f, *a):
-                todo[step] = todo.get(step, []) + [(f, a)]
-
-            joined = 0
-            for i, hd in enumerate(heads):
-                copy_at = 2 if i == 0 else max(NW * (i - 1) + 1, joined + 1)
-                at(copy_at, None, hd)
-                for q in range(len(PIECES)):
-                    at(copy_at + (q // 2 if i == 0 else q), seven_block, hd, q)
-                joined = max(copy_at + (3 if i == 0 else len(PIECES)), NW * i)
-                at(joined, blocks_a, hd)
-                at(joined, blocks_b, hd)
-                at(joined + 2, magnitude, hd, 512, 1280)
-            for i, hd in enumerate(heads):
-                pv = heads[i - 1] if i > 0 else None
-                for j in range(NW):
-                    banked(spread, sines, hd, j)
-                    for (f, a) in todo.get(NW * i + j, []):
-                        if f is None:
-                            banked(features_t, seven, a[0])
-                        else:
-                            plain(f, *a)
-                    if j == 0 and pv is not None:
-                        plain(quad_product, pv, 1)
-                    if (hd, j) in EARLY_AT:
-                        x_regroup(EARLY_AT[(hd, j)])
-                    if (hd, j - 1) in EARLY_AT:
-                        plain(quantise_x, EARLY_AT[(hd, j - 1)])
-                    if j == 1:
-                        plain(pair_product, hd, 0)
-                        if pv is not None:
-                            plain(row_product, pv)
-                    if j == 2 and late:
-                        leave_items(late.pop(0), "sssv")
-                    if j == 3:
-                        plain(pair_product, hd, 1)
-                        if pv is not None and i - 1 < SOON:
-                            plain(magnitude, pv, 0, 512)
-                        if hd == 0:
-                            plain(make_phi, 1)
-                        if hd % 2 == 1 and (hd + 3) // 2 < B:
-                            plain(make_phi, (hd + 3) // 2)
-                    if j == 5:
-                        plain(pair_product, hd, 2)
-                        plain(quad_product, hd, 0)
-                    if j == 7:
-                        plain(pair_product, hd, 3)
             last = heads[-1]
-            plain(mirror_a, heads[0])
-            plain(mirror_b, heads[0])
-            plain(mirror_a, heads[1])
-            for i, hd in enumerate(heads):
-                prev = heads[i - SKEW] if i >= SKEW else None
-                plain(expo_a, hd)
-                if i == 0:
-                    plain(quad_product, last, 1)
-                own_x = hd not in xdone
-                if own_x:
-                    x_regroup(hd)
-                if i == 0:
-                    plain(row_product, last)
-                if i + 1 < n:
-                    plain(mirror_b, heads[i + 1])
-                plain(expo_b, hd)
-                if i + 2 < n:
-                    plain(mirror_a, heads[i + 2])
-                plain(expo_c, hd)
-                if prev is not None:
-                    leave_items(prev, "ssvv" if prev in EARLY_X else "sssv")
-                plain(regroup_e, hd)
-                if i + SOON < n:
-                    plain(magnitude, heads[i + SOON], 0, 512)
-                if own_x:
-                    plain(quantise_x, hd)
-                plain(row_sums, hd)
-                plain(quantise_e, hd)
-                plain(inverse, hd)
-            late = heads[n - SKEW :]
-        for hd in late:
-            leave_items(hd, "svsv")
+            mirror_rows_3_1(heads[0])
+            mirror_row_2(heads[0])
+            mirror_rows_3_1(heads[1])
+            for i in range(n + LAG):
+                done = heads[i - LAG] if i >= LAG else None
+                if done is not None:
+                    for u in range(T):
+                        mx_product(done, u)
+                if i < n:
+                    hd = heads[i]
+                    ahead = heads[i + EARLY] if i + EARLY < n else None
+                    if ahead is not None:
+                        regroup_x(ahead)
+                    if i == 0:
+                        product_of_four(last, 1)
+                        quantise_x(ahead)
+                        product_of_eight(last)
+                    exponentials_of_mirror_3_1(hd)
+                    if i + 1 < n:
+                        mirror_row_2(heads[i + 1])
+                    exponentials_of_mirror_2(hd)
+                    if i + 2 < n:
+                        mirror_rows_3_1(heads[i + 2])
+                    exponentials_of_blocks(hd)
+                if done is not None:
+                    for u in range(T):
+                        divide_and_store(done, u, u == T - 1 if i < n else u % 2 == 1)
+                if i == n - 1 and sines_follow:
+                    nc.scalar.activation(out=warm[:], in_=minus_one[:], func=ACT.Sin)
+                if i < n:
+                    regroup_e(hd)
+                    if i == 0:
+                        magnitude(last)
+                    elif ahead is not None:
+                        quantise_x(ahead)
+                    add_sums(hd)
+                    quantise_e(hd)
+                    invert_sums(hd)
 
-        fills = [k for k in range(len(items)) if items[k][0] is not None]
-        filled = 0
-        for k, (fill, use, needs) in enumerate(items):
-            if fill is not None:
-                rank = fills.index(k)
-                while filled < min(len(fills), rank + 1 + AHEAD):
-                    needs = items[fills[filled]][2]
-                    if needs is not None and "eq" not in st[needs]:
-                        break
-                    items[fills[filled]][0]()
-                    filled += 1
-            use()
+        make_terms(0)
+        for g in range(B * H // GROUP):
+            heads = list(range(g * GROUP, (g + 1) * GROUP))
+            sine_phase(heads)
+            exponential_phase(heads, heads[-1] + 1 < B * H)

@@ -18,22 +18,15 @@ ACT = mybir.ActivationFunctionType
 
 P = 128
 T = 4
-GROUP = 8
-AHEAD = 4
-EARLY = 3
-TWOS = 5
-SINES = 10
-LAG = 2
-ORDER = (7, 0, 1, 2, 3, 4, 5, 6)
+HEADS = B * H
+HALF = NW // 2
+TABLES = 3
+ORDER = (0, 1, 2, 7, 3, 4, 5, 6)
 ROW = (0, 512, 1024, 896)
 BLOCKS = 1280
 TWO_PI_HIGH = 6.28125
 TWO_PI_LOW = 2.0 * math.pi - TWO_PI_HIGH
 PI_BELOW = 3.1415925025939941
-
-
-def column(b, t, h, w):
-    return ((b * T + t) * H + h) * NW + w
 
 
 def tile_quantumkernelattention_t_kernel(tc, x, out):
@@ -44,85 +37,118 @@ def tile_quantumkernelattention_t_kernel(tc, x, out):
         work = ctx.enter_context(tc.tile_pool(name="work", bufs=2))
         psum = ctx.enter_context(tc.psum_pool(name="psum", bufs=1))
 
-        NCOL = B * T * H * NW
+        NCOL = HEADS * T * NW
+        PER_BATCH = T * H * NW
         first8 = const.tile([P, NCOL], BF16, name="first8")
-        per_batch = T * H * NW
-        for b in range(B):
+
+        def load_first8(b):
             nc.sync.dma_start(
-                out=first8[:, b * per_batch : (b + 1) * per_batch].rearrange("p (k w) -> p k w", w=NW),
+                out=first8[:, b * PER_BATCH : (b + 1) * PER_BATCH].rearrange("p (k w) -> p k w", w=NW),
                 in_=x[b].rearrange("(p t) (h d) -> p (t h) d", t=T, h=H)[:, :, 0:NW],
             )
-        X_BUFS = 4
+
         x_tile = {}
 
         def load_x(b):
-            x_tile[b] = work.tile([P, T, H * DK], BF16, name="x_tile", bufs=X_BUFS)
+            x_tile[b] = work.tile([P, T, H * DK], BF16, name="x_tile", bufs=B)
             nc.sync.dma_start(out=x_tile[b][:], in_=x[b].rearrange("(p t) e -> p t e", t=T))
 
-        for b in range(X_BUFS):
+        for b in range(B):
+            load_first8(b)
+        for b in range(B):
             load_x(b)
 
         identity = const.tile([P, P], F32, name="identity")
         make_identity(nc, identity[:])
         minus_one = const.tile([P, 1], F32, name="minus_one")
         nc.vector.memset(minus_one[:], -1.0)
+        one = const.tile([P, 1], F32, name="one")
+        nc.vector.memset(one[:], 1.0)
         warm = const.tile([P, 1], F32, name="warm")
         nc.scalar.activation(out=warm[:], in_=minus_one[:], func=ACT.Sin)
 
-        turns = work.tile([P, NCOL], I32, name="turns", tag="sine", bufs=SINES)
-        part = work.tile([P, NCOL], F32, name="part", tag="sine", bufs=SINES)
-        full = work.tile([P, NCOL], F32, name="full", tag="sine", bufs=SINES)
+        turns = const.tile([P, NCOL], I32, name="turns")
+        part = const.tile([P, NCOL], F32, name="part")
+        full = const.tile([P, NCOL], F32, name="full")
         twice = const.tile([P, NCOL], F32, name="twice")
-        spreadable = const.tile([P, NCOL], F32, name="spreadable")
-        bias = const.tile([P, NCOL], F32, name="bias")
-        halves = (slice(0, NCOL // 2), slice(NCOL // 2, NCOL))
-        for c in halves:
+        less_pi = const.tile([P, NCOL], F32, name="less_pi")
+        trig = const.tile([P, 2, NCOL], F32, name="trig")
+        inverse_cos = const.tile([P, NCOL], F32, name="inverse_cos")
+        tangent = const.tile([P, NCOL], F32, name="tangent")
+        NTOK = HEADS * T
+        inverse_sin = const.tile([P, HEADS, NW], F32, name="inverse_sin")
+        cotangent = const.tile([P, HEADS, NW], F32, name="cotangent")
+        sin_4 = const.tile([P, HEADS, 4], F32, name="sin_4")
+        sin_2 = const.tile([P, HEADS, 2], F32, name="sin_2")
+        sin_all = const.tile([P, HEADS, 1], F32, name="sin_all")
+        cos_4 = const.tile([P, NTOK, 4], F32, name="cos_4")
+        cos_2 = const.tile([P, NTOK, 2], F32, name="cos_2")
+        cos_all = const.tile([P, NTOK, 1], F32, name="cos_all")
+        by_feature = trig[:].rearrange("p c (k w) -> p k c w", w=NW)
+        seventh = const.tile([P, NTOK, 2], F32, name="seventh")
+        pairs = [const.tile([P, NTOK, 2, 2], F32, name="pair%d" % q) for q in range(3)]
+        sixteen = const.tile([P, NTOK, 4, 4], F32, name="sixteen")
+        eight = const.tile([P, NTOK, 4, 2], F32, name="eight")
+
+        def angles(b0, b1):
+            c = slice(b0 * PER_BATCH, b1 * PER_BATCH)
             nc.vector.tensor_scalar(
-                out=turns[:, c], in0=first8[:, c], scalar1=1.0 / (2.0 * math.pi), scalar2=None, op0=ALU.mult
+                out=turns[:, c], in0=first8[:, c], scalar1=1.0 / (2.0 * math.pi), scalar2=0.25, op0=ALU.mult, op1=ALU.add
             )
-        for c in halves:
             nc.vector.scalar_tensor_tensor(
                 out=part[:, c], in0=turns[:, c], scalar=-TWO_PI_HIGH, in1=first8[:, c], op0=ALU.mult, op1=ALU.add
             )
-        for c in halves:
             nc.vector.scalar_tensor_tensor(
                 out=full[:, c], in0=turns[:, c], scalar=-TWO_PI_LOW, in1=part[:, c], op0=ALU.mult, op1=ALU.add
             )
-        for c in halves:
             nc.vector.tensor_scalar(
-                out=twice[:, c], in0=full[:, c], scalar1=PI_BELOW, scalar2=-PI_BELOW, op0=ALU.min, op1=ALU.max
+                out=twice[:, c], in0=full[:, c], scalar1=math.pi / 2, scalar2=-PI_BELOW, op0=ALU.add, op1=ALU.max
             )
-        for c in halves:
-            nc.vector.tensor_scalar(out=spreadable[:, c], in0=twice[:, c], scalar1=-math.pi, scalar2=None, op0=ALU.add)
-        for c in halves:
-            nc.vector.tensor_scalar(
-                out=part[:, c], in0=twice[:, c], scalar1=0.0, scalar2=math.pi, op0=ALU.is_ge, op1=ALU.mult
-            )
-        for c in halves:
-            nc.vector.scalar_tensor_tensor(
-                out=bias[:, c], in0=twice[:, c], scalar=-0.5, in1=part[:, c], op0=ALU.mult, op1=ALU.add
-            )
-        trig = work.tile([P, 2, NCOL], F32, name="trig", tag="e", bufs=LAG + 2)
-        nc.scalar.activation(out=trig[:, 1, :], in_=twice[:], func=ACT.Sin, scale=0.5)
-        nc.scalar.activation(out=trig[:, 0, :], in_=spreadable[:], func=ACT.Sin, scale=0.5)
-        NTOK = B * T * H
-        by_feature = trig[:].rearrange("p c (k w) -> p k c w", w=NW)
+            nc.vector.tensor_scalar(out=less_pi[:, c], in0=twice[:, c], scalar1=-math.pi, scalar2=None, op0=ALU.add)
 
-        def outer(dst, left, n_left, right, n_right):
+        def sines_and_cosines(b0, b1):
+            c = slice(b0 * PER_BATCH, b1 * PER_BATCH)
+            nc.scalar.activation(out=trig[:, 0, c], in_=less_pi[:, c], func=ACT.Sin, scale=0.5)
+            nc.scalar.activation(out=trig[:, 1, c], in_=twice[:, c], func=ACT.Sin, scale=0.5)
+
+        def times(engine, dst, a, c):
+            engine.tensor_tensor(out=dst, in0=a, in1=c, op=ALU.mult)
+
+        def tangents(b0, b1):
+            c = slice(b0 * PER_BATCH, b1 * PER_BATCH)
+            k = slice(b0 * T * H, b1 * T * H)
+            hd = slice(b0 * H, b1 * H)
+            cosines = by_feature[:, k, 0, :]
+            sin_0 = trig[:, 1, c].rearrange("p (b k w) -> p b k w", k=T * H, w=NW)[:, :, 0:H, :]
+            cos_0 = trig[:, 0, c].rearrange("p (b k w) -> p b k w", k=T * H, w=NW)[:, :, 0:H, :]
+
+            def by_batch(t):
+                return t[:, hd].rearrange("p (b h) w -> p b h w", h=H)
+
+            times(nc.vector, cos_4[:, k], cosines[:, :, 0:4], cosines[:, :, 4:8])
+            nc.vector.reciprocal(out=inverse_cos[:, c], in_=trig[:, 0, c])
+            times(nc.vector, cos_2[:, k], cos_4[:, k, 0:2], cos_4[:, k, 2:4])
+            times(nc.vector, by_batch(sin_4), sin_0[:, :, :, 0:4], sin_0[:, :, :, 4:8])
+            times(nc.vector, cos_all[:, k], cos_2[:, k, 0:1], cos_2[:, k, 1:2])
+            times(nc.vector, tangent[:, c], trig[:, 1, c], inverse_cos[:, c])
+            times(nc.vector, sin_2[:, hd], sin_4[:, hd, 0:2], sin_4[:, hd, 2:4])
+            nc.vector.reciprocal(out=by_batch(inverse_sin), in_=sin_0)
+            times(nc.vector, sin_all[:, hd], sin_2[:, hd, 0:1], sin_2[:, hd, 1:2])
+            times(nc.vector, by_batch(cotangent), cos_0, by_batch(inverse_sin))
+
+        def outer(engine, dst, left, n_left, right, n_right):
             shape = [P, dst.shape[1], n_left, n_right]
-            nc.vector.tensor_tensor(
-                out=dst, in0=left.unsqueeze(3).to_broadcast(shape), in1=right.unsqueeze(2).to_broadcast(shape), op=ALU.mult
-            )
+            times(engine, dst, left.unsqueeze(3).to_broadcast(shape), right.unsqueeze(2).to_broadcast(shape))
 
-        pairs = []
-        for q in range(3):
-            pair = work.tile([P, NTOK, 2, 2], F32, name="pair%d" % q, tag="two", bufs=TWOS)
-            outer(pair[:], by_feature[:, :, :, 2 * q], 2, by_feature[:, :, :, 2 * q + 1], 2)
-            pairs.append(pair[:].rearrange("p k i j -> p k (i j)"))
-        sixteen = const.tile([P, NTOK, 4, 4], F32, name="sixteen")
-        outer(sixteen[:], pairs[0], 4, pairs[1], 4)
-        eight = const.tile([P, NTOK, 4, 2], F32, name="eight")
-        outer(eight[:], pairs[2], 4, by_feature[:, :, :, 6], 2)
+        def factors(b0, b1):
+            k = slice(b0 * T * H, b1 * T * H)
+            for q in range(3):
+                outer(nc.gpsimd, pairs[q][:, k], by_feature[:, k, :, 2 * q], 2, by_feature[:, k, :, 2 * q + 1], 2)
+            n = (b1 - b0) * T * H
+            times(nc.gpsimd, seventh[:, k], by_feature[:, k, :, 6], by_feature[:, k, 0:1, 7].to_broadcast([P, n, 2]))
+            flat = [pairs[q][:, k].rearrange("p k i j -> p k (i j)") for q in range(3)]
+            outer(nc.gpsimd, sixteen[:, k], flat[0], 4, flat[1], 4)
+            outer(nc.gpsimd, eight[:, k], flat[2], 4, seventh[:, k], 2)
 
         terms = {}
 
@@ -130,6 +156,7 @@ def tile_quantumkernelattention_t_kernel(tc, x, out):
             terms[b] = work.tile([P, (T - 1) * H, 16, 8], F32, name="terms", bufs=2)
             k = (b * T + 1) * H
             outer(
+                nc.gpsimd,
                 terms[b][:],
                 sixteen[:, k : k + (T - 1) * H].rearrange("p k i j -> p k (i j)"),
                 16,
@@ -137,49 +164,67 @@ def tile_quantumkernelattention_t_kernel(tc, x, out):
                 8,
             )
 
-        def queue_bank():
-            return psum.tile([P, 512], F32, name="queue", tag="queue", bufs=AHEAD + 1)
+        def table_bank():
+            return psum.tile([P, S], F32, name="table", tag="table", bufs=TABLES)
 
         def side_bank():
-            return psum.tile([P, 512], F32, name="side", tag="side", bufs=3)
-
-        def multiply(dst, a, c):
-            nc.vector.tensor_tensor(out=dst, in0=a, in1=c, op=ALU.mult)
+            return psum.tile([P, S], F32, name="side", tag="side", bufs=3)
 
         table = {}
-        sine = {}
         score = {}
+        running = {}
 
-        def spread(hd, j):
+        def spread(hd, j, columns, w, width):
             b, h = divmod(hd, H)
-            table[hd, j] = queue_bank()
+            table[hd, j] = table_bank()
             for u in range(T):
-                c = column(b, u, h, ORDER[j])
+                c = ((b * T + u) * H + h) * width + w
                 nc.tensor.transpose(
                     out=table[hd, j][:, u * P : (u + 1) * P],
-                    in_=spreadable[:, c : c + 1].to_broadcast([P, P]),
+                    in_=columns[:, c : c + 1].to_broadcast([P, P]),
                     identity=identity[:],
                 )
 
-        def take_sines(hd, j):
+        def spread_tangent(hd, j):
+            spread(hd, j, tangent, ORDER[j], NW)
+
+        def spread_cosines(hd):
+            spread(hd, NW, cos_all[:].rearrange("p k w -> p (k w)"), 0, 1)
+
+        def start_product(hd):
+            running[hd] = work.tile([P, S], F32, name="running", bufs=3)
+            nc.scalar.activation(
+                out=running[hd][:], in_=table.pop((hd, NW))[:], func=ACT.Copy, scale=sin_all[:, hd, :]
+            )
+
+        def next_factor(hd, j):
+            w = ORDER[j]
+            dst = score[hd][:, 0:S] if j == NW - 1 else running[hd][:]
+            nc.vector.scalar_tensor_tensor(
+                out=dst,
+                in0=table.pop((hd, j))[:],
+                scalar=cotangent[:, hd, w : w + 1],
+                in1=running[hd][:],
+                op0=ALU.add,
+                op1=ALU.mult,
+            )
+
+        def eighth_cosine(hd):
             b, h = divmod(hd, H)
-            angles = table.pop((hd, j))
-            sine[hd, j] = work.tile([P, S], F32, name="sine", bufs=SINES)
-            c = column(b, 0, h, ORDER[j])
-            nc.scalar.activation(out=sine[hd, j][:], in_=angles[:], func=ACT.Sin, bias=bias[:, c : c + 1], scale=0.5)
-            if j == 0:
-                score[hd] = work.tile([P, BLOCKS], F32, name="score", bufs=GROUP + 1)
-                for t in (1, 3, 2):
-                    c = column(b, t, h, ORDER[j])
-                    nc.scalar.activation(
-                        out=score[hd][:, ROW[t] : ROW[t] + (T - t) * P],
-                        in_=angles[:, t * P : S],
-                        func=ACT.Sin,
-                        bias=bias[:, c : c + 1],
-                        scale=0.5,
-                    )
+            score[hd] = work.tile([P, BLOCKS], F32, name="score", bufs=3)
+            j = HALF - 1
+            for t in (1, 3, 2):
+                c = ((b * T + t) * H + h) * NW + ORDER[j]
+                nc.scalar.activation(
+                    out=score[hd][:, ROW[t] : ROW[t] + (T - t) * P],
+                    in_=table[hd, j][:, t * P : S],
+                    func=ACT.Identity,
+                    bias=one[:],
+                    scale=tangent[:, c : c + 1],
+                )
 
         turned = {}
+        by_token = {}
         seven = {}
 
         def turn_terms(hd):
@@ -192,136 +237,125 @@ def tile_quantumkernelattention_t_kernel(tc, x, out):
                     identity=identity[:],
                 )
 
-        def seven_cosines(hd):
-            by_token = work.tile([P, (T - 1) * P], F32, name="by_token", bufs=2)
-            nc.scalar.copy(out=by_token[:], in_=turned.pop(hd)[:, 0 : (T - 1) * P])
-            seven[hd] = (side_bank(), side_bank())
-            for (t, bank, at) in ((1, 0, 0), (3, 0, 384), (2, 1, 0)):
-                nc.tensor.matmul(
-                    out=seven[hd][bank][:, at : at + (T - t) * P],
-                    lhsT=by_token[:, (t - 1) * P : t * P],
-                    rhs=by_token[:, (t - 1) * P : (T - 1) * P],
-                    start=True,
-                    stop=True,
-                )
+        def copy_terms(hd):
+            by_token[hd] = work.tile([P, (T - 1) * P], F32, name="by_token", bufs=2)
+            nc.scalar.copy(out=by_token[hd][:], in_=turned.pop(hd)[:, 0 : (T - 1) * P])
+
+        def seven_cosines(hd, t):
+            if t == 1:
+                seven[hd, 0] = side_bank()
+            if t == 2:
+                seven[hd, 1] = side_bank()
+            at = {1: 0, 3: 384, 2: 0}[t]
+            nc.tensor.matmul(
+                out=seven[hd, 1 if t == 2 else 0][:, at : at + (T - t) * P],
+                lhsT=by_token[hd][:, (t - 1) * P : t * P],
+                rhs=by_token[hd][:, (t - 1) * P : (T - 1) * P],
+                start=True,
+                stop=True,
+            )
 
         def join_rows_1_3(hd):
-            multiply(score[hd][:, 512:1024], seven[hd][0][:], score[hd][:, 512:1024])
+            times(nc.vector, score[hd][:, 512:1024], seven.pop((hd, 0))[:], score[hd][:, 512:1024])
 
         def join_row_2(hd):
-            multiply(score[hd][:, 1024:1280], seven[hd][1][:, 0:256], score[hd][:, 1024:1280])
+            times(nc.vector, score[hd][:, 1024:1280], seven.pop((hd, 1))[:, 0:256], score[hd][:, 1024:1280])
 
-        two = {}
-        four = {}
+        def magnitude_of_row_0(hd):
+            nc.scalar.activation(out=score[hd][:, 0:S], in_=score[hd][:, 0:S], func=ACT.Abs)
 
-        def product_of_two(hd, q):
-            two[hd, q] = work.tile([P, S], F32, name="two", bufs=TWOS)
-            multiply(two[hd, q][:], sine.pop((hd, 2 * q))[:], sine.pop((hd, 2 * q + 1))[:])
-
-        def product_of_four(hd, q):
-            four[hd, q] = work.tile([P, S], F32, name="four", bufs=T)
-            multiply(four[hd, q][:], two.pop((hd, 2 * q))[:], two.pop((hd, 2 * q + 1))[:])
-
-        def product_of_eight(hd):
-            multiply(score[hd][:, 0:S], four.pop((hd, 0))[:], four.pop((hd, 1))[:])
-
-        def magnitude(hd):
-            s = score[hd][:]
-            nc.vector.scalar_tensor_tensor(out=s, in0=s, scalar=-1.0, in1=s, op0=ALU.mult, op1=ALU.max)
+        def magnitude_of_rows_1_to_3(hd):
+            nc.scalar.activation(out=score[hd][:, S:BLOCKS], in_=score[hd][:, S:BLOCKS], func=ACT.Abs)
 
         mirror = {}
 
+        def turn_blocks(bank, hd, blocks):
+            for i, (t, u) in enumerate(blocks):
+                src = ROW[t] + (u - t) * P
+                nc.tensor.transpose(out=bank[:, i * P : (i + 1) * P], in_=score[hd][:, src : src + P], identity=identity[:])
+
         def mirror_rows_3_1(hd):
             mirror[hd, 0] = side_bank()
-            for (at, t, u) in ((0, 0, 3), (128, 1, 3), (256, 2, 3), (384, 0, 1)):
-                src = ROW[t] + (u - t) * P
-                nc.tensor.transpose(out=mirror[hd, 0][:, at : at + P], in_=score[hd][:, src : src + P], identity=identity[:])
+            turn_blocks(mirror[hd, 0], hd, ((0, 3), (1, 3), (2, 3), (0, 1)))
 
         def mirror_row_2(hd):
             mirror[hd, 1] = side_bank()
-            for (at, t, u) in ((0, 0, 2), (128, 1, 2)):
-                src = ROW[t] + (u - t) * P
-                nc.tensor.transpose(out=mirror[hd, 1][:, at : at + P], in_=score[hd][:, src : src + P], identity=identity[:])
+            turn_blocks(mirror[hd, 1], hd, ((0, 2), (1, 2)))
 
         e_tile = {}
         sums = {}
+        total = {}
 
-        def exponential(hd, t, lo, n, src, half):
+        def exponential(hd, t, lo, n, src, sum_out):
             nc.scalar.activation(
-                out=e_tile[hd][:, t, lo : lo + n],
-                in_=src,
-                func=ACT.Exp,
-                bias=minus_one[:],
-                accum_out=sums[hd][:, 2 * t + half : 2 * t + half + 1],
+                out=e_tile[hd][:, t, lo : lo + n], in_=src, func=ACT.Exp, bias=minus_one[:], accum_out=sum_out
             )
-
-        def exponentials_of_mirror_3_1(hd):
-            sums[hd] = work.tile([P, 2 * T], F32, name="sums", bufs=LAG + 1)
-            e_tile[hd] = work.tile([P, T, S], BF16, name="e", bufs=LAG + 2)
-            exponential(hd, 3, 0, 384, mirror[hd, 0][:, 0:384], 0)
-            exponential(hd, 1, 0, 128, mirror.pop((hd, 0))[:, 384:512], 0)
-
-        def exponentials_of_mirror_2(hd):
-            exponential(hd, 2, 0, 256, mirror.pop((hd, 1))[:, 0:256], 0)
 
         def exponentials_of_blocks(hd):
-            s = score.pop(hd)
-            exponential(hd, 0, 0, 256, s[:, 0:256], 0)
-            exponential(hd, 0, 256, 256, s[:, 256:512], 1)
+            s = score[hd]
+            sums[hd] = work.tile([P, 2, T], F32, name="sums", bufs=3)
+            total[hd] = work.tile([P, T], F32, name="total", bufs=3)
+            e_tile[hd] = work.tile([P, T, S], BF16, name="e", bufs=2)
+            exponential(hd, 0, 0, S, s[:, 0:S], total[hd][:, 0:1])
             for t in (1, 3, 2):
-                exponential(hd, t, t * P, (T - t) * P, s[:, ROW[t] : ROW[t] + (T - t) * P], 1)
+                exponential(hd, t, t * P, (T - t) * P, s[:, ROW[t] : ROW[t] + (T - t) * P], sums[hd][:, 1, t : t + 1])
 
-        def regroup(name, src):
-            grouped = work.tile([P, 512, T], BF16, name=name, bufs=2, align_bytes=64)
-            nc.vector.tensor_copy(
-                out=grouped[:].rearrange("p (c i) t -> p c t i", i=4), in_=src.rearrange("p t (c i) -> p c t i", i=4)
-            )
-            return grouped
-
-        def quantise(name, grouped):
-            codes = work.tile([P, 512], U32, name=name + "_codes", bufs=EARLY + LAG + 2, align_bytes=64)
-            scales = work.tile([P, 512], U8, name=name + "_scales", bufs=EARLY + LAG + 2, align_bytes=64)
-            nc.vector.quantize_mx(
-                out=codes[:].bitcast(FP8X4), scales=scales[:], in_=grouped[:].rearrange("p c t -> p (c t)")
-            )
-            return codes, scales
+        def exponentials_of_mirrors(hd):
+            exponential(hd, 3, 0, 384, mirror[hd, 0][:, 0:384], sums[hd][:, 0, 3:4])
+            exponential(hd, 1, 0, 128, mirror.pop((hd, 0))[:, 384:512], sums[hd][:, 0, 1:2])
+            exponential(hd, 2, 0, 256, mirror.pop((hd, 1))[:, 0:256], sums[hd][:, 0, 2:3])
 
         grouped_x = {}
         grouped_e = {}
         packed_x = {}
         packed_e = {}
-        total = {}
         inverse = {}
+
+        def views(grouped, src):
+            return (
+                grouped[:].rearrange("p (c i) t -> p c t i", i=4),
+                src.rearrange("p t (c i) -> p c t i", i=4),
+            )
 
         def regroup_x(hd):
             b, h = divmod(hd, H)
-            grouped_x[hd] = regroup("grouped_x", x_tile[b][:, :, h * DK : (h + 1) * DK])
-            if h == H - 1 and b + X_BUFS < B:
-                load_x(b + X_BUFS)
+            grouped_x[hd] = work.tile([P, DK, T], BF16, name="grouped_x", bufs=2, align_bytes=64)
+            dst, src = views(grouped_x[hd], x_tile[b][:, :, h * DK : (h + 1) * DK])
+            nc.gpsimd.tensor_scalar(out=dst, in0=src, scalar1=1.0, scalar2=0.0, op0=ALU.mult, op1=ALU.add)
 
         def regroup_e(hd):
-            grouped_e[hd] = regroup("grouped_e", e_tile.pop(hd)[:])
+            grouped_e[hd] = work.tile([P, S, T], BF16, name="grouped_e", bufs=2, align_bytes=64)
+            dst, src = views(grouped_e[hd], e_tile.pop(hd)[:])
+            nc.vector.tensor_copy(out=dst, in_=src)
+
+        def quantise(name, grouped, bufs):
+            codes = work.tile([P, 512], U32, name=name + "_codes", bufs=bufs, align_bytes=64)
+            scales = work.tile([P, 512], U8, name=name + "_scales", bufs=bufs, align_bytes=64)
+            nc.vector.quantize_mx(
+                out=codes[:].bitcast(FP8X4), scales=scales[:], in_=grouped[:].rearrange("p c t -> p (c t)")
+            )
+            return codes, scales
 
         def quantise_x(hd):
-            packed_x[hd] = quantise("x", grouped_x.pop(hd))
+            packed_x[hd] = quantise("x", grouped_x.pop(hd), 3)
 
         def quantise_e(hd):
-            packed_e[hd] = quantise("e", grouped_e.pop(hd))
+            packed_e[hd] = quantise("e", grouped_e.pop(hd), 3)
 
         def add_sums(hd):
-            total[hd] = work.tile([P, T], F32, name="total", bufs=2)
-            nc.vector.tensor_reduce(
-                out=total[hd][:], in_=sums.pop(hd)[:].rearrange("p (t s) -> p t s", s=2), axis=mybir.AxisListType.X, op=ALU.add
+            times_sums = sums.pop(hd)
+            nc.vector.tensor_tensor(
+                out=total[hd][:, 1:T], in0=times_sums[:, 0, 1:T], in1=times_sums[:, 1, 1:T], op=ALU.add
             )
 
         def invert_sums(hd):
-            inverse[hd] = work.tile([P, T], F32, name="inverse", bufs=LAG + 2)
+            inverse[hd] = work.tile([P, T], F32, name="inverse", bufs=3)
             nc.vector.reciprocal(out=inverse[hd][:], in_=total.pop(hd)[:])
 
         mx = {}
 
         def mx_product(hd, u):
-            mx[hd, u] = queue_bank()
+            mx[hd, u] = psum.tile([P, DK], F32, name="mx", tag="mx", bufs=2)
             nc.tensor.matmul_mx(
                 out=mx[hd, u][:],
                 lhsT=packed_e[hd][0][:, u * P : (u + 1) * P].bitcast(FP8X4),
@@ -343,94 +377,109 @@ def tile_quantumkernelattention_t_kernel(tc, x, out):
                 nc.scalar.activation(out=result[:], in_=mx.pop((hd, u))[:], func=ACT.Copy, scale=inverse[hd][:, u : u + 1])
             nc.sync.dma_start(out=out[b].rearrange("(p t) e -> p t e", t=T)[:, u, h * DK : (h + 1) * DK], in_=result[:])
 
-        def sine_phase(heads):
-            steps = [(hd, j) for hd in heads for j in range(NW)]
-            for s in range(AHEAD):
-                spread(*steps[s])
-            for s, (hd, j) in enumerate(steps):
-                if s + AHEAD < len(steps):
-                    spread(*steps[s + AHEAD])
-                take_sines(hd, j)
-                first = hd == heads[0]
-                if j == 0 and not first:
-                    join_rows_1_3(hd)
-                    product_of_four(hd - 1, 1)
-                    join_row_2(hd)
-                    product_of_eight(hd - 1)
-                if j == 1:
-                    product_of_two(hd, 0)
-                    if first:
-                        turn_terms(hd)
-                    else:
-                        magnitude(hd - 1)
-                if j == 3:
-                    product_of_two(hd, 1)
-                    if first:
-                        seven_cosines(hd)
-                    if hd % H == 0 and hd + H < B * H:
-                        make_terms(hd // H + 1)
-                if j == 4 and first:
-                    join_rows_1_3(hd)
-                    join_row_2(hd)
-                if j == 5:
-                    product_of_two(hd, 2)
-                    product_of_four(hd, 0)
-                    if hd != heads[-1]:
-                        turn_terms(hd + 1)
-                if j == 7:
-                    product_of_two(hd, 3)
-                    if hd != heads[-1]:
-                        seven_cosines(hd + 1)
-                if first and j < 2 * EARLY:
-                    if j % 2 == 0:
-                        regroup_x(heads[j // 2])
-                    else:
-                        quantise_x(heads[j // 2])
+        def exists(hd):
+            return 0 <= hd < HEADS
 
-        def exponential_phase(heads, sines_follow):
-            n = len(heads)
-            last = heads[-1]
-            mirror_rows_3_1(heads[0])
-            mirror_row_2(heads[0])
-            mirror_rows_3_1(heads[1])
-            for i in range(n + LAG):
-                done = heads[i - LAG] if i >= LAG else None
-                if done is not None:
-                    for u in range(T):
-                        mx_product(done, u)
-                if i < n:
-                    hd = heads[i]
-                    ahead = heads[i + EARLY] if i + EARLY < n else None
-                    if ahead is not None:
-                        regroup_x(ahead)
-                    if i == 0:
-                        product_of_four(last, 1)
-                        quantise_x(ahead)
-                        product_of_eight(last)
-                    exponentials_of_mirror_3_1(hd)
-                    if i + 1 < n:
-                        mirror_row_2(heads[i + 1])
-                    exponentials_of_mirror_2(hd)
-                    if i + 2 < n:
-                        mirror_rows_3_1(heads[i + 2])
-                    exponentials_of_blocks(hd)
-                if done is not None:
-                    for u in range(T):
-                        divide_and_store(done, u, u == T - 1 if i < n else u % 2 == 1)
-                if i == n - 1 and sines_follow:
-                    nc.scalar.activation(out=warm[:], in_=minus_one[:], func=ACT.Sin)
-                if i < n:
-                    regroup_e(hd)
-                    if i == 0:
-                        magnitude(last)
-                    elif ahead is not None:
-                        quantise_x(ahead)
-                    add_sums(hd)
-                    quantise_e(hd)
-                    invert_sums(hd)
+        def factors_of_round(r):
+            both = []
+            for j in range(HALF):
+                both += [(hd, k) for hd, k in ((r, HALF + j), (r + 1, j)) if exists(hd)]
+            return both
 
+        queue = []
+        for r in range(-2, HEADS):
+            queue += factors_of_round(r)
+            if exists(r + 2):
+                queue.append((r + 2, NW))
+
+        def spread_next():
+            if queue and len(table) < TABLES:
+                hd, j = queue.pop(0)
+                if j == NW:
+                    spread_cosines(hd)
+                else:
+                    spread_tangent(hd, j)
+
+        def round_of(r):
+            old, last, new, next_new = r - 2, r - 1, r + 1, r + 2
+            pace = factors_of_round(r)
+            mx_left = list(range(T)) if exists(old) else []
+            div_left = list(mx_left)
+
+            def product():
+                if mx_left:
+                    mx_product(old, mx_left.pop(0))
+
+            def divide():
+                if div_left:
+                    divide_and_store(old, div_left.pop(0), False)
+
+            blocks = [1, 3, 2] if exists(new) else []
+            product()
+            product()
+            for i, (hd, j) in enumerate(pace):
+                if i == len(pace) - 1:
+                    if exists(r):
+                        magnitude_of_rows_1_to_3(r)
+                    if exists(new):
+                        eighth_cosine(new)
+                next_factor(hd, j)
+                if i < len(pace) - 2:
+                    spread_next()
+                divide()
+                product()
+                if i >= 3 and blocks:
+                    seven_cosines(new, blocks.pop(0))
+            for t in blocks:
+                seven_cosines(new, t)
+            for u in range(T):
+                divide()
+                product()
+            if exists(r):
+                magnitude_of_row_0(r)
+            if exists(next_new):
+                start_product(next_new)
+            if exists(last):
+                regroup_e(last)
+            if exists(new):
+                join_rows_1_3(new)
+                join_row_2(new)
+            if exists(r):
+                exponentials_of_blocks(r)
+                mirror_rows_3_1(r)
+                mirror_row_2(r)
+                score.pop(r)
+                exponentials_of_mirrors(r)
+            if exists(last):
+                quantise_e(last)
+                quantise_x(last)
+                add_sums(last)
+                invert_sums(last)
+            spread_next()
+            if exists(next_new):
+                turn_terms(next_new)
+                copy_terms(next_new)
+            for i in range(TABLES):
+                spread_next()
+            if exists(new) and new > 0:
+                regroup_x(new)
+            if r % H == 0 and exists(r + 4):
+                make_terms((r + 4) // H)
+
+        angles(0, 1)
+        sines_and_cosines(0, 1)
+        angles(1, B)
+        tangents(0, 1)
+        factors(0, 1)
         make_terms(0)
-        for g in range(B * H // GROUP):
-            heads = list(range(g * GROUP, (g + 1) * GROUP))
-            sine_phase(heads)
-            exponential_phase(heads, heads[-1] + 1 < B * H)
+        for i in range(TABLES):
+            spread_next()
+        sines_and_cosines(1, B)
+        regroup_x(0)
+        factors(1, B)
+        make_terms(1)
+        round_of(-2)
+        round_of(-1)
+        tangents(1, B)
+        for r in range(HEADS + 2):
+            round_of(r)

@@ -19,11 +19,11 @@ ACT = mybir.ActivationFunctionType
 P = 128
 T = 4
 HEADS = B * H
-HALF = NW // 2
-TABLES = 3
-ORDER = (0, 1, 2, 7, 3, 4, 5, 6)
-ROW = (0, 512, 1024, 896)
+FAR = 2 * P
+ORDER = (7, 0, 1, 2, 3, 4, 5, 6)
+ROW = (0, 512, 896, 1152)
 BLOCKS = 1280
+TABLES = 3
 TWO_PI_HIGH = 6.28125
 TWO_PI_LOW = 2.0 * math.pi - TWO_PI_HIGH
 PI_BELOW = 3.1415925025939941
@@ -37,8 +37,9 @@ def tile_quantumkernelattention_t_kernel(tc, x, out):
         work = ctx.enter_context(tc.tile_pool(name="work", bufs=2))
         psum = ctx.enter_context(tc.psum_pool(name="psum", bufs=1))
 
-        NCOL = HEADS * T * NW
         PER_BATCH = T * H * NW
+        NCOL = B * PER_BATCH
+        NTOK = B * T * H
         first8 = const.tile([P, NCOL], BF16, name="first8")
 
         def load_first8(b):
@@ -70,25 +71,21 @@ def tile_quantumkernelattention_t_kernel(tc, x, out):
         turns = const.tile([P, NCOL], I32, name="turns")
         part = const.tile([P, NCOL], F32, name="part")
         full = const.tile([P, NCOL], F32, name="full")
-        twice = const.tile([P, NCOL], F32, name="twice")
-        less_pi = const.tile([P, NCOL], F32, name="less_pi")
+        angle = const.tile([P, 2, NCOL], F32, name="angle")
         trig = const.tile([P, 2, NCOL], F32, name="trig")
-        inverse_cos = const.tile([P, NCOL], F32, name="inverse_cos")
-        tangent = const.tile([P, NCOL], F32, name="tangent")
-        NTOK = HEADS * T
-        inverse_sin = const.tile([P, HEADS, NW], F32, name="inverse_sin")
-        cotangent = const.tile([P, HEADS, NW], F32, name="cotangent")
-        sin_4 = const.tile([P, HEADS, 4], F32, name="sin_4")
-        sin_2 = const.tile([P, HEADS, 2], F32, name="sin_2")
-        sin_all = const.tile([P, HEADS, 1], F32, name="sin_all")
-        cos_4 = const.tile([P, NTOK, 4], F32, name="cos_4")
-        cos_2 = const.tile([P, NTOK, 2], F32, name="cos_2")
-        cos_all = const.tile([P, NTOK, 1], F32, name="cos_all")
+        inverse_den = const.tile([P, NCOL], F32, name="inverse_den")
+        ratio = const.tile([P, NCOL], F32, name="ratio")
+        den_4 = const.tile([P, NTOK, 4], F32, name="den_4")
+        den_2 = const.tile([P, NTOK, 2], F32, name="den_2")
+        den_all = const.tile([P, NTOK, 1], F32, name="den_all")
         by_feature = trig[:].rearrange("p c (k w) -> p k c w", w=NW)
-        seventh = const.tile([P, NTOK, 2], F32, name="seventh")
+        last_two = const.tile([P, NTOK, 2], F32, name="last_two")
         pairs = [const.tile([P, NTOK, 2, 2], F32, name="pair%d" % q) for q in range(3)]
         sixteen = const.tile([P, NTOK, 4, 4], F32, name="sixteen")
         eight = const.tile([P, NTOK, 4, 2], F32, name="eight")
+
+        def times(engine, dst, a, c):
+            engine.tensor_tensor(out=dst, in0=a, in1=c, op=ALU.mult)
 
         def angles(b0, b1):
             c = slice(b0 * PER_BATCH, b1 * PER_BATCH)
@@ -101,40 +98,40 @@ def tile_quantumkernelattention_t_kernel(tc, x, out):
             nc.vector.scalar_tensor_tensor(
                 out=full[:, c], in0=turns[:, c], scalar=-TWO_PI_LOW, in1=part[:, c], op0=ALU.mult, op1=ALU.add
             )
-            nc.vector.tensor_scalar(
-                out=twice[:, c], in0=full[:, c], scalar1=math.pi / 2, scalar2=-PI_BELOW, op0=ALU.add, op1=ALU.max
-            )
-            nc.vector.tensor_scalar(out=less_pi[:, c], in0=twice[:, c], scalar1=-math.pi, scalar2=None, op0=ALU.add)
+            half = T * H * NW // 2
 
-        def sines_and_cosines(b0, b1):
+            def slots(a, pair):
+                return a.rearrange("p (b s k) -> p b s k", s=2, k=half)[:, :, pair, :]
+
+            for i in range(2):
+                for pair in range(2):
+                    nc.vector.tensor_scalar(
+                        out=slots(angle[:, i, c], pair),
+                        in0=slots(full[:, c], pair),
+                        scalar1=-PI_BELOW - math.pi / 2,
+                        scalar2=math.pi / 2 if i == pair else -math.pi / 2,
+                        op0=ALU.max,
+                        op1=ALU.add,
+                    )
+
+        def sines(b0, b1):
             c = slice(b0 * PER_BATCH, b1 * PER_BATCH)
-            nc.scalar.activation(out=trig[:, 0, c], in_=less_pi[:, c], func=ACT.Sin, scale=0.5)
-            nc.scalar.activation(out=trig[:, 1, c], in_=twice[:, c], func=ACT.Sin, scale=0.5)
+            nc.scalar.activation(out=trig[:, :, c], in_=angle[:, :, c], func=ACT.Sin, scale=0.5)
 
-        def times(engine, dst, a, c):
-            engine.tensor_tensor(out=dst, in0=a, in1=c, op=ALU.mult)
-
-        def tangents(b0, b1):
+        def invert(b0, b1):
             c = slice(b0 * PER_BATCH, b1 * PER_BATCH)
+            nc.vector.reciprocal(out=inverse_den[:, c], in_=trig[:, 0, c])
+
+        def ratios(b0, b1):
+            c = slice(b0 * PER_BATCH, b1 * PER_BATCH)
+            times(nc.vector, ratio[:, c], trig[:, 1, c], inverse_den[:, c])
+
+        def den_products(engine, b0, b1):
             k = slice(b0 * T * H, b1 * T * H)
-            hd = slice(b0 * H, b1 * H)
-            cosines = by_feature[:, k, 0, :]
-            sin_0 = trig[:, 1, c].rearrange("p (b k w) -> p b k w", k=T * H, w=NW)[:, :, 0:H, :]
-            cos_0 = trig[:, 0, c].rearrange("p (b k w) -> p b k w", k=T * H, w=NW)[:, :, 0:H, :]
-
-            def by_batch(t):
-                return t[:, hd].rearrange("p (b h) w -> p b h w", h=H)
-
-            times(nc.vector, cos_4[:, k], cosines[:, :, 0:4], cosines[:, :, 4:8])
-            nc.vector.reciprocal(out=inverse_cos[:, c], in_=trig[:, 0, c])
-            times(nc.vector, cos_2[:, k], cos_4[:, k, 0:2], cos_4[:, k, 2:4])
-            times(nc.vector, by_batch(sin_4), sin_0[:, :, :, 0:4], sin_0[:, :, :, 4:8])
-            times(nc.vector, cos_all[:, k], cos_2[:, k, 0:1], cos_2[:, k, 1:2])
-            times(nc.vector, tangent[:, c], trig[:, 1, c], inverse_cos[:, c])
-            times(nc.vector, sin_2[:, hd], sin_4[:, hd, 0:2], sin_4[:, hd, 2:4])
-            nc.vector.reciprocal(out=by_batch(inverse_sin), in_=sin_0)
-            times(nc.vector, sin_all[:, hd], sin_2[:, hd, 0:1], sin_2[:, hd, 1:2])
-            times(nc.vector, by_batch(cotangent), cos_0, by_batch(inverse_sin))
+            den = by_feature[:, k, 0, :]
+            times(engine, den_4[:, k], den[:, :, 0:4], den[:, :, 4:8])
+            times(engine, den_2[:, k], den_4[:, k, 0:2], den_4[:, k, 2:4])
+            times(engine, den_all[:, k], den_2[:, k, 0:1], den_2[:, k, 1:2])
 
         def outer(engine, dst, left, n_left, right, n_right):
             shape = [P, dst.shape[1], n_left, n_right]
@@ -142,145 +139,156 @@ def tile_quantumkernelattention_t_kernel(tc, x, out):
 
         def factors(b0, b1):
             k = slice(b0 * T * H, b1 * T * H)
+            n = (b1 - b0) * T * H
             for q in range(3):
                 outer(nc.gpsimd, pairs[q][:, k], by_feature[:, k, :, 2 * q], 2, by_feature[:, k, :, 2 * q + 1], 2)
-            n = (b1 - b0) * T * H
-            times(nc.gpsimd, seventh[:, k], by_feature[:, k, :, 6], by_feature[:, k, 0:1, 7].to_broadcast([P, n, 2]))
+            times(nc.gpsimd, last_two[:, k], by_feature[:, k, :, 6], by_feature[:, k, 0:1, 7].to_broadcast([P, n, 2]))
             flat = [pairs[q][:, k].rearrange("p k i j -> p k (i j)") for q in range(3)]
             outer(nc.gpsimd, sixteen[:, k], flat[0], 4, flat[1], 4)
-            outer(nc.gpsimd, eight[:, k], flat[2], 4, seventh[:, k], 2)
+            outer(nc.gpsimd, eight[:, k], flat[2], 4, last_two[:, k], 2)
 
         terms = {}
 
         def make_terms(b):
-            terms[b] = work.tile([P, (T - 1) * H, 16, 8], F32, name="terms", bufs=2)
-            k = (b * T + 1) * H
+            terms[b] = work.tile([P, T * H, 16, 8], F32, name="terms", bufs=2)
+            k = slice(b * T * H, (b + 1) * T * H)
             outer(
                 nc.gpsimd,
                 terms[b][:],
-                sixteen[:, k : k + (T - 1) * H].rearrange("p k i j -> p k (i j)"),
+                sixteen[:, k].rearrange("p k i j -> p k (i j)"),
                 16,
-                eight[:, k : k + (T - 1) * H].rearrange("p k i j -> p k (i j)"),
+                eight[:, k].rearrange("p k i j -> p k (i j)"),
                 8,
             )
-
-        def table_bank():
-            return psum.tile([P, S], F32, name="table", tag="table", bufs=TABLES)
 
         def side_bank():
             return psum.tile([P, S], F32, name="side", tag="side", bufs=3)
 
+        def token(hd, t):
+            b, h = divmod(hd, H)
+            return (b * T + t) * H + h
+
+        def ratio_of(hd, t, w):
+            c = token(hd, t) * NW + w
+            return ratio[:, c : c + 1]
+
+        def den_of(hd, t):
+            return den_all[:, token(hd, t), :]
+
+        def spread(bank, at, column):
+            nc.tensor.transpose(out=bank[:, at : at + P], in_=column.to_broadcast([P, P]), identity=identity[:])
+
+        BANKS = 5
+        queue = [(hd, i) for hd in range(HEADS) for i in range(BANKS)]
         table = {}
+
+        def spread_next():
+            if not queue or len(table) == TABLES:
+                return
+            hd, i = queue.pop(0)
+            bank = psum.tile([P, S], F32, name="table", tag="table", bufs=TABLES)
+            table[hd, i] = bank
+            if i == 0:
+                for t in range(T):
+                    spread(bank, t * P, ratio_of(hd, t, ORDER[0]))
+                return
+            for half in range(2):
+                for t in (2, 3):
+                    at = half * FAR + (t - 2) * P
+                    if i == 1 and half == 0:
+                        spread(bank, at, den_of(hd, t))
+                    else:
+                        spread(bank, at, ratio_of(hd, t, ORDER[2 * i - 2 + half]))
+
         score = {}
         running = {}
 
-        def spread(hd, j, columns, w, width):
-            b, h = divmod(hd, H)
-            table[hd, j] = table_bank()
-            for u in range(T):
-                c = ((b * T + u) * H + h) * width + w
-                nc.tensor.transpose(
-                    out=table[hd, j][:, u * P : (u + 1) * P],
-                    in_=columns[:, c : c + 1].to_broadcast([P, P]),
-                    identity=identity[:],
-                )
-
-        def spread_tangent(hd, j):
-            spread(hd, j, tangent, ORDER[j], NW)
-
-        def spread_cosines(hd):
-            spread(hd, NW, cos_all[:].rearrange("p k w -> p (k w)"), 0, 1)
-
-        def start_product(hd):
-            running[hd] = work.tile([P, S], F32, name="running", bufs=3)
-            nc.scalar.activation(
-                out=running[hd][:], in_=table.pop((hd, NW))[:], func=ACT.Copy, scale=sin_all[:, hd, :]
-            )
-
-        def next_factor(hd, j):
-            w = ORDER[j]
-            dst = score[hd][:, 0:S] if j == NW - 1 else running[hd][:]
-            nc.vector.scalar_tensor_tensor(
-                out=dst,
-                in0=table.pop((hd, j))[:],
-                scalar=cotangent[:, hd, w : w + 1],
-                in1=running[hd][:],
-                op0=ALU.add,
-                op1=ALU.mult,
-            )
+        def block(hd, t, u, n=1):
+            lo = ROW[t] + (u - t) * P
+            return score[hd][:, lo : lo + n * P]
 
         def eighth_cosine(hd):
-            b, h = divmod(hd, H)
             score[hd] = work.tile([P, BLOCKS], F32, name="score", bufs=3)
-            j = HALF - 1
-            for t in (1, 3, 2):
-                c = ((b * T + t) * H + h) * NW + ORDER[j]
+            for t, n in ((0, 2), (1, 1), (2, 2), (3, 1)):
                 nc.scalar.activation(
-                    out=score[hd][:, ROW[t] : ROW[t] + (T - t) * P],
-                    in_=table[hd, j][:, t * P : S],
+                    out=block(hd, t, t, n),
+                    in_=table[hd, 0][:, t * P : (t + n) * P],
                     func=ACT.Identity,
                     bias=one[:],
-                    scale=tangent[:, c : c + 1],
+                    scale=ratio_of(hd, t, ORDER[0]),
                 )
+
+        def start_product(hd):
+            running[hd] = work.tile([P, 2, FAR], F32, name="running", bufs=2)
+            for t in range(2):
+                nc.scalar.activation(
+                    out=running[hd][:, t, :], in_=table[hd, 1][:, 0:FAR], func=ACT.Copy, scale=den_of(hd, t)
+                )
+
+        def next_factor(hd, j):
+            i, half = divmod(j + 2, 2) if j else (0, 1)
+            at = half * FAR
+            for t in range(2):
+                nc.vector.scalar_tensor_tensor(
+                    out=block(hd, t, 2, 2) if j == NW - 1 else running[hd][:, t, :],
+                    in0=table[hd, i][:, at : at + FAR],
+                    scalar=ratio_of(hd, t, ORDER[j]),
+                    in1=running[hd][:, t, :],
+                    op0=ALU.add,
+                    op1=ALU.mult,
+                )
+            if half == 1:
+                table.pop((hd, i))
 
         turned = {}
         by_token = {}
-        seven = {}
+        near = {}
 
         def turn_terms(hd):
             b, h = divmod(hd, H)
             turned[hd] = side_bank()
-            for t in range(1, T):
+            for t in range(T):
                 nc.tensor.transpose(
-                    out=turned[hd][:, (t - 1) * P : t * P],
-                    in_=terms[b][:, (t - 1) * H + h].rearrange("p i j -> p (i j)"),
+                    out=turned[hd][:, t * P : (t + 1) * P],
+                    in_=terms[b][:, t * H + h].rearrange("p i j -> p (i j)"),
                     identity=identity[:],
                 )
 
         def copy_terms(hd):
-            by_token[hd] = work.tile([P, (T - 1) * P], F32, name="by_token", bufs=2)
-            nc.scalar.copy(out=by_token[hd][:], in_=turned.pop(hd)[:, 0 : (T - 1) * P])
+            by_token[hd] = work.tile([P, S], F32, name="by_token", bufs=2)
+            nc.scalar.copy(out=by_token[hd][:], in_=turned.pop(hd)[:])
 
-        def seven_cosines(hd, t):
-            if t == 1:
-                seven[hd, 0] = side_bank()
-            if t == 2:
-                seven[hd, 1] = side_bank()
-            at = {1: 0, 3: 384, 2: 0}[t]
-            nc.tensor.matmul(
-                out=seven[hd, 1 if t == 2 else 0][:, at : at + (T - t) * P],
-                lhsT=by_token[hd][:, (t - 1) * P : t * P],
-                rhs=by_token[hd][:, (t - 1) * P : (T - 1) * P],
-                start=True,
-                stop=True,
-            )
+        def near_blocks(hd, pair):
+            near[hd, pair] = side_bank()
+            t = 2 * pair
+            for row, at in ((t, 0), (t + 1, FAR)):
+                nc.tensor.matmul(
+                    out=near[hd, pair][:, at : at + (t + 2 - row) * P],
+                    lhsT=by_token[hd][:, row * P : (row + 1) * P],
+                    rhs=by_token[hd][:, row * P : (t + 2) * P],
+                    start=True,
+                    stop=True,
+                )
 
-        def join_rows_1_3(hd):
-            times(nc.vector, score[hd][:, 512:1024], seven.pop((hd, 0))[:], score[hd][:, 512:1024])
+        def join(hd):
+            first = near.pop((hd, 0))
+            times(nc.vector, block(hd, 0, 0, 2), first[:, 0:FAR], block(hd, 0, 0, 2))
+            times(nc.vector, block(hd, 1, 1), first[:, FAR : FAR + P], block(hd, 1, 1))
+            rest = score[hd][:, ROW[2] : BLOCKS]
+            times(nc.vector, rest, near.pop((hd, 1))[:, 0 : BLOCKS - ROW[2]], rest)
 
-        def join_row_2(hd):
-            times(nc.vector, score[hd][:, 1024:1280], seven.pop((hd, 1))[:, 0:256], score[hd][:, 1024:1280])
-
-        def magnitude_of_row_0(hd):
-            nc.scalar.activation(out=score[hd][:, 0:S], in_=score[hd][:, 0:S], func=ACT.Abs)
-
-        def magnitude_of_rows_1_to_3(hd):
-            nc.scalar.activation(out=score[hd][:, S:BLOCKS], in_=score[hd][:, S:BLOCKS], func=ACT.Abs)
+        def magnitude(hd):
+            nc.scalar.activation(out=score[hd][:], in_=score[hd][:], func=ACT.Abs)
 
         mirror = {}
 
-        def turn_blocks(bank, hd, blocks):
-            for i, (t, u) in enumerate(blocks):
-                src = ROW[t] + (u - t) * P
-                nc.tensor.transpose(out=bank[:, i * P : (i + 1) * P], in_=score[hd][:, src : src + P], identity=identity[:])
-
-        def mirror_rows_3_1(hd):
-            mirror[hd, 0] = side_bank()
-            turn_blocks(mirror[hd, 0], hd, ((0, 3), (1, 3), (2, 3), (0, 1)))
-
-        def mirror_row_2(hd):
-            mirror[hd, 1] = side_bank()
-            turn_blocks(mirror[hd, 1], hd, ((0, 2), (1, 2)))
+        def mirrors(hd):
+            for i, blocks in enumerate((((0, 3), (1, 3), (2, 3), (0, 1)), ((0, 2), (1, 2)))):
+                mirror[hd, i] = side_bank()
+                for k, (t, u) in enumerate(blocks):
+                    nc.tensor.transpose(
+                        out=mirror[hd, i][:, k * P : (k + 1) * P], in_=block(hd, t, u), identity=identity[:]
+                    )
 
         e_tile = {}
         sums = {}
@@ -292,13 +300,13 @@ def tile_quantumkernelattention_t_kernel(tc, x, out):
             )
 
         def exponentials_of_blocks(hd):
-            s = score[hd]
             sums[hd] = work.tile([P, 2, T], F32, name="sums", bufs=3)
             total[hd] = work.tile([P, T], F32, name="total", bufs=3)
             e_tile[hd] = work.tile([P, T, S], BF16, name="e", bufs=2)
-            exponential(hd, 0, 0, S, s[:, 0:S], total[hd][:, 0:1])
-            for t in (1, 3, 2):
-                exponential(hd, t, t * P, (T - t) * P, s[:, ROW[t] : ROW[t] + (T - t) * P], sums[hd][:, 1, t : t + 1])
+            for t in range(T):
+                exponential(
+                    hd, t, t * P, (T - t) * P, block(hd, t, t, T - t), sums[hd][:, 1, t : t + 1] if t else total[hd][:, 0:1]
+                )
 
         def exponentials_of_mirrors(hd):
             exponential(hd, 3, 0, 384, mirror[hd, 0][:, 0:384], sums[hd][:, 0, 3:4])
@@ -311,42 +319,42 @@ def tile_quantumkernelattention_t_kernel(tc, x, out):
         packed_e = {}
         inverse = {}
 
-        def views(grouped, src):
-            return (
-                grouped[:].rearrange("p (c i) t -> p c t i", i=4),
-                src.rearrange("p t (c i) -> p c t i", i=4),
-            )
-
         def regroup_x(hd):
             b, h = divmod(hd, H)
             grouped_x[hd] = work.tile([P, DK, T], BF16, name="grouped_x", bufs=2, align_bytes=64)
-            dst, src = views(grouped_x[hd], x_tile[b][:, :, h * DK : (h + 1) * DK])
-            nc.gpsimd.tensor_scalar(out=dst, in0=src, scalar1=1.0, scalar2=0.0, op0=ALU.mult, op1=ALU.add)
+            nc.gpsimd.tensor_scalar(
+                out=grouped_x[hd][:],
+                in0=x_tile[b][:, :, h * DK : (h + 1) * DK].rearrange("p t c -> p c t"),
+                scalar1=1.0,
+                scalar2=0.0,
+                op0=ALU.mult,
+                op1=ALU.add,
+            )
 
         def regroup_e(hd):
             grouped_e[hd] = work.tile([P, S, T], BF16, name="grouped_e", bufs=2, align_bytes=64)
-            dst, src = views(grouped_e[hd], e_tile.pop(hd)[:])
-            nc.vector.tensor_copy(out=dst, in_=src)
+            nc.vector.tensor_copy(
+                out=grouped_e[hd][:].rearrange("p (c i) t -> p c t i", i=4),
+                in_=e_tile.pop(hd)[:].rearrange("p t (c i) -> p c t i", i=4),
+            )
 
-        def quantise(name, grouped, bufs):
-            codes = work.tile([P, 512], U32, name=name + "_codes", bufs=bufs, align_bytes=64)
-            scales = work.tile([P, 512], U8, name=name + "_scales", bufs=bufs, align_bytes=64)
+        def quantise(name, grouped):
+            codes = work.tile([P, 512], U32, name=name + "_codes", bufs=3, align_bytes=64)
+            scales = work.tile([P, 512], U8, name=name + "_scales", bufs=3, align_bytes=64)
             nc.vector.quantize_mx(
                 out=codes[:].bitcast(FP8X4), scales=scales[:], in_=grouped[:].rearrange("p c t -> p (c t)")
             )
             return codes, scales
 
         def quantise_x(hd):
-            packed_x[hd] = quantise("x", grouped_x.pop(hd), 3)
+            packed_x[hd] = quantise("x", grouped_x.pop(hd))
 
         def quantise_e(hd):
-            packed_e[hd] = quantise("e", grouped_e.pop(hd), 3)
+            packed_e[hd] = quantise("e", grouped_e.pop(hd))
 
         def add_sums(hd):
-            times_sums = sums.pop(hd)
-            nc.vector.tensor_tensor(
-                out=total[hd][:, 1:T], in0=times_sums[:, 0, 1:T], in1=times_sums[:, 1, 1:T], op=ALU.add
-            )
+            both = sums.pop(hd)
+            nc.vector.tensor_tensor(out=total[hd][:, 1:T], in0=both[:, 0, 1:T], in1=both[:, 1, 1:T], op=ALU.add)
 
         def invert_sums(hd):
             inverse[hd] = work.tile([P, T], F32, name="inverse", bufs=3)
@@ -380,106 +388,87 @@ def tile_quantumkernelattention_t_kernel(tc, x, out):
         def exists(hd):
             return 0 <= hd < HEADS
 
-        def factors_of_round(r):
-            both = []
-            for j in range(HALF):
-                both += [(hd, k) for hd, k in ((r, HALF + j), (r + 1, j)) if exists(hd)]
-            return both
-
-        queue = []
-        for r in range(-2, HEADS):
-            queue += factors_of_round(r)
-            if exists(r + 2):
-                queue.append((r + 2, NW))
-
-        def spread_next():
-            if queue and len(table) < TABLES:
-                hd, j = queue.pop(0)
-                if j == NW:
-                    spread_cosines(hd)
-                else:
-                    spread_tangent(hd, j)
-
         def round_of(r):
             old, last, new, next_new = r - 2, r - 1, r + 1, r + 2
-            pace = factors_of_round(r)
-            mx_left = list(range(T)) if exists(old) else []
-            div_left = list(mx_left)
 
-            def product():
-                if mx_left:
-                    mx_product(old, mx_left.pop(0))
+            def product(u):
+                if exists(old):
+                    mx_product(old, u)
 
-            def divide():
-                if div_left:
-                    divide_and_store(old, div_left.pop(0), False)
+            def divide(u):
+                if exists(old):
+                    divide_and_store(old, u, False)
 
-            blocks = [1, 3, 2] if exists(new) else []
-            product()
-            product()
-            for i, (hd, j) in enumerate(pace):
-                if i == len(pace) - 1:
-                    if exists(r):
-                        magnitude_of_rows_1_to_3(r)
-                    if exists(new):
-                        eighth_cosine(new)
-                next_factor(hd, j)
-                if i < len(pace) - 2:
-                    spread_next()
-                divide()
-                product()
-                if i >= 3 and blocks:
-                    seven_cosines(new, blocks.pop(0))
-            for t in blocks:
-                seven_cosines(new, t)
-            for u in range(T):
-                divide()
-                product()
+            def factor(*js):
+                if exists(r):
+                    for j in js:
+                        next_factor(r, j)
+
+            product(0)
+            product(1)
+            factor(0)
+            spread_next()
+            divide(0)
+            product(2)
+            factor(1)
+            spread_next()
+            divide(1)
+            product(3)
+            factor(2, 3)
+            spread_next()
+            divide(2)
+            if exists(new):
+                near_blocks(new, 0)
+            factor(4, 5)
+            divide(3)
+            if exists(new):
+                eighth_cosine(new)
+            spread_next()
+            if exists(new):
+                near_blocks(new, 1)
+            factor(6, 7)
+            spread_next()
+            if exists(new):
+                start_product(new)
+                join(new)
             if exists(r):
-                magnitude_of_row_0(r)
-            if exists(next_new):
-                start_product(next_new)
+                magnitude(r)
             if exists(last):
                 regroup_e(last)
-            if exists(new):
-                join_rows_1_3(new)
-                join_row_2(new)
             if exists(r):
                 exponentials_of_blocks(r)
-                mirror_rows_3_1(r)
-                mirror_row_2(r)
-                score.pop(r)
+                mirrors(r)
                 exponentials_of_mirrors(r)
+                score.pop(r)
             if exists(last):
+                add_sums(last)
                 quantise_e(last)
                 quantise_x(last)
-                add_sums(last)
                 invert_sums(last)
-            spread_next()
             if exists(next_new):
                 turn_terms(next_new)
                 copy_terms(next_new)
-            for i in range(TABLES):
-                spread_next()
             if exists(new) and new > 0:
                 regroup_x(new)
             if r % H == 0 and exists(r + 4):
-                make_terms((r + 4) // H)
+                b = (r + 4) // H
+                invert(b, b + 1)
+                ratios(b, b + 1)
+                make_terms(b)
 
         angles(0, 1)
-        sines_and_cosines(0, 1)
-        angles(1, B)
-        tangents(0, 1)
+        sines(0, 1)
+        invert(0, 1)
+        den_products(nc.vector, 0, 1)
+        ratios(0, 1)
         factors(0, 1)
         make_terms(0)
         for i in range(TABLES):
             spread_next()
-        sines_and_cosines(1, B)
+        angles(1, B)
+        sines(1, B)
         regroup_x(0)
+        den_products(nc.gpsimd, 1, B)
         factors(1, B)
-        make_terms(1)
-        round_of(-2)
-        round_of(-1)
-        tangents(1, B)
-        for r in range(HEADS + 2):
+        for r in range(-2, HEADS + 2):
             round_of(r)

@@ -374,6 +374,18 @@ def tile_quantumkernelattention_t_kernel(tc, x, out):
                 stop=True,
             )
 
+        def keep_warm(hd):
+            spare = psum.tile([P, DK], F32, name="mx", tag="mx", bufs=2)
+            nc.tensor.matmul_mx(
+                out=spare[:],
+                lhsT=packed_e[hd][0][:, 0:P].bitcast(FP8X4),
+                lhsT_scale=packed_e[hd][1][:, 0:P],
+                rhs=packed_x[hd][0][:].bitcast(FP8X4),
+                rhs_scale=packed_x[hd][1][:],
+                start=True,
+                stop=True,
+            )
+
         def divide_and_store(hd, u, on_vector):
             b, h = divmod(hd, H)
             result = work.tile([P, DK], F32, name="result", bufs=2 * T)
@@ -404,6 +416,11 @@ def tile_quantumkernelattention_t_kernel(tc, x, out):
                     for j in js:
                         next_factor(r, j)
 
+            def warm_passes(n):
+                if exists(old):
+                    for i in range(n):
+                        keep_warm(old)
+
             product(0)
             product(1)
             factor(0)
@@ -428,6 +445,7 @@ def tile_quantumkernelattention_t_kernel(tc, x, out):
                 near_blocks(new, 1)
             factor(6, 7)
             spread_next()
+            warm_passes(2)
             if exists(new):
                 start_product(new)
                 join(new)
@@ -438,6 +456,7 @@ def tile_quantumkernelattention_t_kernel(tc, x, out):
             if exists(r):
                 exponentials_of_blocks(r)
                 mirrors(r)
+                warm_passes(1)
                 exponentials_of_mirrors(r)
                 score.pop(r)
             if exists(last):
@@ -447,6 +466,7 @@ def tile_quantumkernelattention_t_kernel(tc, x, out):
                 invert_sums(last)
             if exists(next_new):
                 turn_terms(next_new)
+                warm_passes(1)
                 copy_terms(next_new)
             if exists(new) and new > 0:
                 regroup_x(new)

@@ -19,8 +19,8 @@ ACT = mybir.ActivationFunctionType
 P = 128
 T = 4
 HEADS = B * H
+HALF = NW // 2
 FAR = 2 * P
-ORDER = (7, 0, 1, 2, 3, 4, 5, 6)
 ROW = (0, 512, 896, 1152)
 BLOCKS = 1280
 TABLES = 3
@@ -59,6 +59,7 @@ def tile_quantumkernelattention_t_kernel(tc, x, out):
         for b in range(B):
             load_x(b)
 
+        parked = out[B - 1].rearrange("s e -> (s e)")[0 : (NTOK + 2 * HEADS) * P]
         identity = const.tile([P, P], F32, name="identity")
         make_identity(nc, identity[:])
         minus_one = const.tile([P, 1], F32, name="minus_one")
@@ -79,10 +80,16 @@ def tile_quantumkernelattention_t_kernel(tc, x, out):
         den_2 = const.tile([P, NTOK, 2], F32, name="den_2")
         den_all = const.tile([P, NTOK, 1], F32, name="den_all")
         by_feature = trig[:].rearrange("p c (k w) -> p k c w", w=NW)
+        columns = const.tile([P, P], F32, name="columns")
+        rows = const.tile([P, P], F32, name="rows")
+        inverse_7 = const.tile([P, 2, NTOK], F32, name="inverse_7")
+        inverse_ratio_7 = const.tile([P, NTOK], F32, name="inverse_ratio_7")
         last_two = const.tile([P, NTOK, 2], F32, name="last_two")
         pairs = [const.tile([P, NTOK, 2, 2], F32, name="pair%d" % q) for q in range(3)]
         sixteen = const.tile([P, NTOK, 4, 4], F32, name="sixteen")
         eight = const.tile([P, NTOK, 4, 2], F32, name="eight")
+
+        nc.gpsimd.memset(columns[:, NTOK + 2 * HEADS : P], 0.0)
 
         def times(engine, dst, a, c):
             engine.tensor_tensor(out=dst, in0=a, in1=c, op=ALU.mult)
@@ -133,6 +140,27 @@ def tile_quantumkernelattention_t_kernel(tc, x, out):
             times(engine, den_2[:, k], den_4[:, k, 0:2], den_4[:, k, 2:4])
             times(engine, den_all[:, k], den_2[:, k, 0:1], den_2[:, k, 1:2])
 
+        def seventh_ratios():
+            both = by_feature[:, :, :, 7].rearrange("p k c -> p c k")
+            nc.vector.reciprocal(out=inverse_7[:], in_=both)
+            times(nc.vector, inverse_ratio_7[:], both[:, 0, :], inverse_7[:, 1, :])
+            times(
+                nc.vector,
+                columns[:, 0:NTOK].rearrange("p (b h t) -> p b h t", h=H, t=T),
+                both[:, 1, :].rearrange("p (b t h) -> p b h t", h=H, t=T),
+                inverse_7[:, 0, :].rearrange("p (b t h) -> p b h t", h=H, t=T),
+            )
+
+        def park_columns():
+            nc.vector.tensor_copy(
+                out=columns[:, NTOK : NTOK + 2 * HEADS].rearrange("p (b h t) -> p b h t", h=H, t=2),
+                in_=den_all[:].rearrange("p (b t h) w -> p b h (t w)", t=T, h=H)[:, :, :, 2:4],
+            )
+            turned_columns = side_bank()
+            nc.tensor.transpose(out=turned_columns[:, 0:P], in_=columns[:], identity=identity[:])
+            nc.vector.tensor_copy(out=rows[:], in_=turned_columns[:, 0:P])
+            nc.sync.dma_start(out=parked.rearrange("(k p) -> k p", p=P), in_=rows[0 : NTOK + 2 * HEADS, :])
+
         def outer(engine, dst, left, n_left, right, n_right):
             shape = [P, dst.shape[1], n_left, n_right]
             times(engine, dst, left.unsqueeze(3).to_broadcast(shape), right.unsqueeze(2).to_broadcast(shape))
@@ -178,27 +206,45 @@ def tile_quantumkernelattention_t_kernel(tc, x, out):
         def spread(bank, at, column):
             nc.tensor.transpose(out=bank[:, at : at + P], in_=column.to_broadcast([P, P]), identity=identity[:])
 
-        BANKS = 5
-        queue = [(hd, i) for hd in range(HEADS) for i in range(BANKS)]
+        queue = [(r, k) for r in range(-1, HEADS) for k in range(HALF)]
         table = {}
+
+        def table_bank():
+            return psum.tile([P, S], F32, name="table", tag="table", bufs=TABLES)
+
+        def factors_of_bank(r, k):
+            return [(hd, j, i * FAR) for i, (hd, j) in enumerate(((r, HALF + k), (r + 1, k))) if 0 <= hd < HEADS]
 
         def spread_next():
             if not queue or len(table) == TABLES:
                 return
-            hd, i = queue.pop(0)
-            bank = psum.tile([P, S], F32, name="table", tag="table", bufs=TABLES)
-            table[hd, i] = bank
-            if i == 0:
-                for t in range(T):
-                    spread(bank, t * P, ratio_of(hd, t, ORDER[0]))
-                return
-            for half in range(2):
+            r, k = queue.pop(0)
+            table[r, k] = table_bank()
+            for hd, j, at in factors_of_bank(r, k):
                 for t in (2, 3):
-                    at = half * FAR + (t - 2) * P
-                    if i == 1 and half == 0:
-                        spread(bank, at, den_of(hd, t))
-                    else:
-                        spread(bank, at, ratio_of(hd, t, ORDER[2 * i - 2 + half]))
+                    spread(table[r, k], at + (t - 2) * P, ratio_of(hd, t, j))
+
+        fixed = {}
+
+        def new_fixed(hd):
+            fixed[hd] = work.tile([P, S + FAR], F32, name="fixed", bufs=3)
+
+        def spread_fixed(hd):
+            new_fixed(hd)
+            for lo, columns_of, slots in (
+                (0, lambda t: ratio_of(hd, t, 7), (0, 1, 2, 3)),
+                (S, lambda t: den_of(hd, t), (2, 3)),
+            ):
+                bank = table_bank()
+                for i, t in enumerate(slots):
+                    spread(bank, i * P, columns_of(t))
+                n = len(slots) * P
+                nc.scalar.copy(out=fixed[hd][:, lo : lo + n], in_=bank[:, 0:n])
+
+        def load_fixed(hd):
+            new_fixed(hd)
+            for lo, at, n in ((0, hd * S, S), (S, NTOK * P + hd * FAR, FAR)):
+                nc.sync.dma_start(out=fixed[hd][:, lo : lo + n], in_=parked[at : at + n].partition_broadcast(P))
 
         score = {}
         running = {}
@@ -207,38 +253,20 @@ def tile_quantumkernelattention_t_kernel(tc, x, out):
             lo = ROW[t] + (u - t) * P
             return score[hd][:, lo : lo + n * P]
 
-        def eighth_cosine(hd):
-            score[hd] = work.tile([P, BLOCKS], F32, name="score", bufs=3)
-            for t, n in ((0, 2), (1, 1), (2, 2), (3, 1)):
-                nc.scalar.activation(
-                    out=block(hd, t, t, n),
-                    in_=table[hd, 0][:, t * P : (t + n) * P],
-                    func=ACT.Identity,
-                    bias=one[:],
-                    scale=ratio_of(hd, t, ORDER[0]),
-                )
-
-        def start_product(hd):
-            running[hd] = work.tile([P, 2, FAR], F32, name="running", bufs=2)
-            for t in range(2):
-                nc.scalar.activation(
-                    out=running[hd][:, t, :], in_=table[hd, 1][:, 0:FAR], func=ACT.Copy, scale=den_of(hd, t)
-                )
-
-        def next_factor(hd, j):
-            i, half = divmod(j + 2, 2) if j else (0, 1)
-            at = half * FAR
-            for t in range(2):
-                nc.vector.scalar_tensor_tensor(
-                    out=block(hd, t, 2, 2) if j == NW - 1 else running[hd][:, t, :],
-                    in0=table[hd, i][:, at : at + FAR],
-                    scalar=ratio_of(hd, t, ORDER[j]),
-                    in1=running[hd][:, t, :],
-                    op0=ALU.add,
-                    op1=ALU.mult,
-                )
-            if half == 1:
-                table.pop((hd, i))
+        def multiply_bank(r, k):
+            for hd, j, at in factors_of_bank(r, k):
+                if j == 0:
+                    running[hd] = work.tile([P, 2, FAR], F32, name="running", bufs=3)
+                for t in range(2):
+                    nc.vector.scalar_tensor_tensor(
+                        out=block(hd, t, 2, 2) if j == NW - 1 else running[hd][:, t, :],
+                        in0=table[r, k][:, at : at + FAR],
+                        scalar=ratio_of(hd, t, j),
+                        in1=running[hd][:, t, :] if j else fixed[hd][:, S : S + FAR],
+                        op0=ALU.add,
+                        op1=ALU.mult,
+                    )
+            table.pop((r, k))
 
         turned = {}
         by_token = {}
@@ -271,14 +299,28 @@ def tile_quantumkernelattention_t_kernel(tc, x, out):
                 )
 
         def join(hd):
-            first = near.pop((hd, 0))
-            times(nc.vector, block(hd, 0, 0, 2), first[:, 0:FAR], block(hd, 0, 0, 2))
-            times(nc.vector, block(hd, 1, 1), first[:, FAR : FAR + P], block(hd, 1, 1))
-            rest = score[hd][:, ROW[2] : BLOCKS]
-            times(nc.vector, rest, near.pop((hd, 1))[:, 0 : BLOCKS - ROW[2]], rest)
+            score[hd] = work.tile([P, BLOCKS], F32, name="score", bufs=3)
+            for t in range(T):
+                pair, second = divmod(t, 2)
+                n = (2 - second) * P
+                nc.vector.scalar_tensor_tensor(
+                    out=block(hd, t, t, 2 - second),
+                    in0=fixed[hd][:, t * P : t * P + n],
+                    scalar=inverse_ratio_7[:, token(hd, t) : token(hd, t) + 1],
+                    in1=near[hd, pair][:, second * FAR : second * FAR + n],
+                    op0=ALU.add,
+                    op1=ALU.mult,
+                )
 
-        def magnitude(hd):
-            nc.scalar.activation(out=score[hd][:], in_=score[hd][:], func=ACT.Abs)
+        def near_magnitudes(hd):
+            for t in range(T):
+                part_of_row = block(hd, t, t, 2 - t % 2)
+                nc.scalar.activation(out=part_of_row, in_=part_of_row, func=ACT.Abs, scale=ratio_of(hd, t, 7))
+
+        def far_magnitudes(hd):
+            for t in range(2):
+                part_of_row = block(hd, t, 2, 2)
+                nc.scalar.activation(out=part_of_row, in_=part_of_row, func=ACT.Abs, scale=den_of(hd, t))
 
         mirror = {}
 
@@ -303,7 +345,7 @@ def tile_quantumkernelattention_t_kernel(tc, x, out):
             sums[hd] = work.tile([P, 2, T], F32, name="sums", bufs=3)
             total[hd] = work.tile([P, T], F32, name="total", bufs=3)
             e_tile[hd] = work.tile([P, T, S], BF16, name="e", bufs=2)
-            for t in range(T):
+            for t in (2, 3, 0, 1):
                 exponential(
                     hd, t, t * P, (T - t) * P, block(hd, t, t, T - t), sums[hd][:, 1, t : t + 1] if t else total[hd][:, 0:1]
                 )
@@ -411,48 +453,50 @@ def tile_quantumkernelattention_t_kernel(tc, x, out):
                 if exists(old):
                     divide_and_store(old, u, False)
 
-            def factor(*js):
-                if exists(r):
-                    for j in js:
-                        next_factor(r, j)
+            def factors_of(k):
+                if (r, k) in table:
+                    multiply_bank(r, k)
 
             def warm_passes(n):
                 if exists(old):
                     for i in range(n):
                         keep_warm(old)
 
+            batch_ahead = (r + 4) // H if r % H == 0 and exists(r + 4) else 0
             product(0)
             product(1)
-            factor(0)
+            if r >= 0 and exists(r + 3):
+                load_fixed(r + 3)
+            factors_of(0)
             spread_next()
             divide(0)
             product(2)
-            factor(1)
+            if batch_ahead:
+                invert(batch_ahead, batch_ahead + 1)
+            factors_of(1)
             spread_next()
             divide(1)
             product(3)
-            factor(2, 3)
-            spread_next()
             divide(2)
             if exists(new):
                 near_blocks(new, 0)
-            factor(4, 5)
+            if exists(r):
+                near_magnitudes(r)
+            factors_of(2)
             divide(3)
-            if exists(new):
-                eighth_cosine(new)
             spread_next()
             if exists(new):
                 near_blocks(new, 1)
-            factor(6, 7)
+            factors_of(3)
             spread_next()
             warm_passes(2)
-            if exists(new):
-                start_product(new)
-                join(new)
             if exists(r):
-                magnitude(r)
+                far_magnitudes(r)
+            if exists(new):
+                join(new)
             if exists(last):
                 regroup_e(last)
+                add_sums(last)
             if exists(r):
                 exponentials_of_blocks(r)
                 mirrors(r)
@@ -460,9 +504,8 @@ def tile_quantumkernelattention_t_kernel(tc, x, out):
                 exponentials_of_mirrors(r)
                 score.pop(r)
             if exists(last):
-                add_sums(last)
-                quantise_e(last)
                 quantise_x(last)
+                quantise_e(last)
                 invert_sums(last)
             if exists(next_new):
                 turn_terms(next_new)
@@ -470,11 +513,9 @@ def tile_quantumkernelattention_t_kernel(tc, x, out):
                 copy_terms(next_new)
             if exists(new) and new > 0:
                 regroup_x(new)
-            if r % H == 0 and exists(r + 4):
-                b = (r + 4) // H
-                invert(b, b + 1)
-                ratios(b, b + 1)
-                make_terms(b)
+            if batch_ahead:
+                ratios(batch_ahead, batch_ahead + 1)
+                make_terms(batch_ahead)
 
         angles(0, 1)
         sines(0, 1)
@@ -483,12 +524,19 @@ def tile_quantumkernelattention_t_kernel(tc, x, out):
         ratios(0, 1)
         factors(0, 1)
         make_terms(0)
-        for i in range(TABLES):
-            spread_next()
         angles(1, B)
         sines(1, B)
-        regroup_x(0)
+        for hd in range(H):
+            spread_fixed(hd)
+        for i in range(TABLES):
+            spread_next()
         den_products(nc.gpsimd, 1, B)
         factors(1, B)
-        for r in range(-2, HEADS + 2):
+        regroup_x(0)
+        round_of(-2)
+        seventh_ratios()
+        park_columns()
+        for hd in range(H, 3):
+            load_fixed(hd)
+        for r in range(-1, HEADS + 2):
             round_of(r)

@@ -23,6 +23,8 @@ HALF = NW // 2
 FAR = 2 * P
 ROW = (0, 512, 896, 1152)
 BLOCKS = 1280
+E_ON_VECTOR = 256
+X_FIRST = 2
 TABLES = 3
 TWO_PI_HIGH = 6.28125
 TWO_PI_LOW = 2.0 * math.pi - TWO_PI_HIGH
@@ -56,7 +58,7 @@ def tile_quantumkernelattention_t_kernel(tc, x, out):
 
         for b in range(B):
             load_first8(b)
-        for b in range(B):
+        for b in range(X_FIRST):
             load_x(b)
 
         parked = out[B - 1].rearrange("s e -> (s e)")[0 : (NTOK + 2 * HEADS) * P]
@@ -151,13 +153,16 @@ def tile_quantumkernelattention_t_kernel(tc, x, out):
                 inverse_7[:, 0, :].rearrange("p (b t h) -> p b h t", h=H, t=T),
             )
 
-        def park_columns():
+        def gather_columns():
             nc.vector.tensor_copy(
                 out=columns[:, NTOK : NTOK + 2 * HEADS].rearrange("p (b h t) -> p b h t", h=H, t=2),
                 in_=den_all[:].rearrange("p (b t h) w -> p b h (t w)", t=T, h=H)[:, :, :, 2:4],
             )
+
+        def park_columns():
             turned_columns = side_bank()
             nc.tensor.transpose(out=turned_columns[:, 0:P], in_=columns[:], identity=identity[:])
+            invert(1, B // 2)
             nc.vector.tensor_copy(out=rows[:], in_=turned_columns[:, 0:P])
             nc.sync.dma_start(out=parked.rearrange("(k p) -> k p", p=P), in_=rows[0 : NTOK + 2 * HEADS, :])
 
@@ -177,12 +182,13 @@ def tile_quantumkernelattention_t_kernel(tc, x, out):
 
         terms = {}
 
-        def make_terms(b):
-            terms[b] = work.tile([P, T * H, 16, 8], F32, name="terms", bufs=2)
-            k = slice(b * T * H, (b + 1) * T * H)
+        def make_terms(hd):
+            b, h = divmod(hd, H)
+            terms[hd] = work.tile([P, T, 16, 8], F32, name="terms", bufs=2)
+            k = slice(b * T * H + h, (b + 1) * T * H, H)
             outer(
                 nc.gpsimd,
-                terms[b][:],
+                terms[hd][:],
                 sixteen[:, k].rearrange("p k i j -> p k (i j)"),
                 16,
                 eight[:, k].rearrange("p k i j -> p k (i j)"),
@@ -273,12 +279,11 @@ def tile_quantumkernelattention_t_kernel(tc, x, out):
         near = {}
 
         def turn_terms(hd):
-            b, h = divmod(hd, H)
             turned[hd] = side_bank()
             for t in range(T):
                 nc.tensor.transpose(
                     out=turned[hd][:, t * P : (t + 1) * P],
-                    in_=terms[b][:, t * H + h].rearrange("p i j -> p (i j)"),
+                    in_=terms[hd][:, t].rearrange("p i j -> p (i j)"),
                     identity=identity[:],
                 )
 
@@ -361,23 +366,25 @@ def tile_quantumkernelattention_t_kernel(tc, x, out):
         packed_e = {}
         inverse = {}
 
+        def regroup_on_gpsimd(dst, src):
+            nc.gpsimd.tensor_scalar(
+                out=dst, in0=src.rearrange("p t c -> p c t"), scalar1=1.0, scalar2=0.0, op0=ALU.mult, op1=ALU.add
+            )
+
         def regroup_x(hd):
             b, h = divmod(hd, H)
             grouped_x[hd] = work.tile([P, DK, T], BF16, name="grouped_x", bufs=2, align_bytes=64)
-            nc.gpsimd.tensor_scalar(
-                out=grouped_x[hd][:],
-                in0=x_tile[b][:, :, h * DK : (h + 1) * DK].rearrange("p t c -> p c t"),
-                scalar1=1.0,
-                scalar2=0.0,
-                op0=ALU.mult,
-                op1=ALU.add,
-            )
+            regroup_on_gpsimd(grouped_x[hd][:], x_tile[b][:, :, h * DK : (h + 1) * DK])
+
+        def regroup_e_on_gpsimd(hd):
+            grouped_e[hd] = work.tile([P, S, T], BF16, name="grouped_e", bufs=2, align_bytes=64)
+            if E_ON_VECTOR < S:
+                regroup_on_gpsimd(grouped_e[hd][:, E_ON_VECTOR:S], e_tile[hd][:, :, E_ON_VECTOR:S])
 
         def regroup_e(hd):
-            grouped_e[hd] = work.tile([P, S, T], BF16, name="grouped_e", bufs=2, align_bytes=64)
             nc.vector.tensor_copy(
-                out=grouped_e[hd][:].rearrange("p (c i) t -> p c t i", i=4),
-                in_=e_tile.pop(hd)[:].rearrange("p t (c i) -> p c t i", i=4),
+                out=grouped_e[hd][:, 0:E_ON_VECTOR].rearrange("p (c i) t -> p c t i", i=4),
+                in_=e_tile.pop(hd)[:, :, 0:E_ON_VECTOR].rearrange("p t (c i) -> p c t i", i=4),
             )
 
         def quantise(name, grouped):
@@ -451,7 +458,7 @@ def tile_quantumkernelattention_t_kernel(tc, x, out):
 
             def divide(u):
                 if exists(old):
-                    divide_and_store(old, u, False)
+                    divide_and_store(old, u, r >= HEADS and u % 2 == 1)
 
             def factors_of(k):
                 if (r, k) in table:
@@ -462,17 +469,18 @@ def tile_quantumkernelattention_t_kernel(tc, x, out):
                     for i in range(n):
                         keep_warm(old)
 
-            batch_ahead = (r + 4) // H if r % H == 0 and exists(r + 4) else 0
             product(0)
             product(1)
             if r >= 0 and exists(r + 3):
                 load_fixed(r + 3)
+            if exists(last):
+                regroup_e_on_gpsimd(last)
+            if exists(r + 3):
+                make_terms(r + 3)
             factors_of(0)
             spread_next()
             divide(0)
             product(2)
-            if batch_ahead:
-                invert(batch_ahead, batch_ahead + 1)
             factors_of(1)
             spread_next()
             divide(1)
@@ -492,6 +500,13 @@ def tile_quantumkernelattention_t_kernel(tc, x, out):
             warm_passes(2)
             if exists(r):
                 far_magnitudes(r)
+            if r == -1:
+                seventh_ratios()
+                gather_columns()
+                park_columns()
+                load_fixed(2)
+                for b in range(X_FIRST, B):
+                    load_x(b)
             if exists(new):
                 join(new)
             if exists(last):
@@ -507,15 +522,16 @@ def tile_quantumkernelattention_t_kernel(tc, x, out):
                 quantise_x(last)
                 quantise_e(last)
                 invert_sums(last)
+            if r == 1:
+                invert(B // 2, B)
             if exists(next_new):
                 turn_terms(next_new)
                 warm_passes(1)
                 copy_terms(next_new)
+            if r == 1:
+                ratios(B // 2, B)
             if exists(new) and new > 0:
                 regroup_x(new)
-            if batch_ahead:
-                ratios(batch_ahead, batch_ahead + 1)
-                make_terms(batch_ahead)
 
         angles(0, 1)
         sines(0, 1)
@@ -524,19 +540,17 @@ def tile_quantumkernelattention_t_kernel(tc, x, out):
         ratios(0, 1)
         factors(0, 1)
         make_terms(0)
-        angles(1, B)
-        sines(1, B)
-        for hd in range(H):
-            spread_fixed(hd)
+        spread_fixed(0)
         for i in range(TABLES):
             spread_next()
+        round_of(-2)
+        angles(1, B)
+        sines(1, B)
         den_products(nc.gpsimd, 1, B)
         factors(1, B)
         regroup_x(0)
-        round_of(-2)
-        seventh_ratios()
-        park_columns()
-        for hd in range(H, 3):
-            load_fixed(hd)
-        for r in range(-1, HEADS + 2):
+        spread_fixed(1)
+        round_of(-1)
+        ratios(1, B // 2)
+        for r in range(HEADS + 2):
             round_of(r)

@@ -303,10 +303,12 @@ def tile_quantumkernelattention_t_kernel(tc, x, out):
                     stop=True,
                 )
 
-        def join(hd):
+        def new_score(hd):
             score[hd] = work.tile([P, BLOCKS], F32, name="score", bufs=3)
-            for t in range(T):
-                pair, second = divmod(t, 2)
+
+        def join(hd, pair):
+            for t in (2 * pair, 2 * pair + 1):
+                second = t % 2
                 n = (2 - second) * P
                 nc.vector.scalar_tensor_tensor(
                     out=block(hd, t, t, 2 - second),
@@ -376,30 +378,42 @@ def tile_quantumkernelattention_t_kernel(tc, x, out):
             grouped_x[hd] = work.tile([P, DK, T], BF16, name="grouped_x", bufs=2, align_bytes=64)
             regroup_on_gpsimd(grouped_x[hd][:], x_tile[b][:, :, h * DK : (h + 1) * DK])
 
+        def on_vector(hd):
+            return E_ON_VECTOR if hd < HEADS - 1 else S
+
         def regroup_e_on_gpsimd(hd):
             grouped_e[hd] = work.tile([P, S, T], BF16, name="grouped_e", bufs=2, align_bytes=64)
-            if E_ON_VECTOR < S:
-                regroup_on_gpsimd(grouped_e[hd][:, E_ON_VECTOR:S], e_tile[hd][:, :, E_ON_VECTOR:S])
+            n = on_vector(hd)
+            if n < S:
+                regroup_on_gpsimd(grouped_e[hd][:, n:S], e_tile[hd][:, :, n:S])
+
+        def parts_of(hd, n):
+            return ((0, n),) if hd < HEADS - 1 else ((0, S // 2), (S // 2, S))
 
         def regroup_e(hd):
-            nc.vector.tensor_copy(
-                out=grouped_e[hd][:, 0:E_ON_VECTOR].rearrange("p (c i) t -> p c t i", i=4),
-                in_=e_tile.pop(hd)[:, :, 0:E_ON_VECTOR].rearrange("p t (c i) -> p c t i", i=4),
-            )
+            e = e_tile.pop(hd)
+            for lo, hi in parts_of(hd, on_vector(hd)):
+                nc.vector.tensor_copy(
+                    out=grouped_e[hd][:, lo:hi].rearrange("p (c i) t -> p c t i", i=4),
+                    in_=e[:, :, lo:hi].rearrange("p t (c i) -> p c t i", i=4),
+                )
 
-        def quantise(name, grouped):
+        def quantise(name, grouped, parts):
             codes = work.tile([P, 512], U32, name=name + "_codes", bufs=3, align_bytes=64)
             scales = work.tile([P, 512], U8, name=name + "_scales", bufs=3, align_bytes=64)
-            nc.vector.quantize_mx(
-                out=codes[:].bitcast(FP8X4), scales=scales[:], in_=grouped[:].rearrange("p c t -> p (c t)")
-            )
+            for lo, hi in parts:
+                nc.vector.quantize_mx(
+                    out=codes[:, lo:hi].bitcast(FP8X4),
+                    scales=scales[:, lo:hi],
+                    in_=grouped[:, lo:hi].rearrange("p c t -> p (c t)"),
+                )
             return codes, scales
 
         def quantise_x(hd):
-            packed_x[hd] = quantise("x", grouped_x.pop(hd))
+            packed_x[hd] = quantise("x", grouped_x.pop(hd), ((0, DK),))
 
         def quantise_e(hd):
-            packed_e[hd] = quantise("e", grouped_e.pop(hd))
+            packed_e[hd] = quantise("e", grouped_e.pop(hd), parts_of(hd, S))
 
         def add_sums(hd):
             both = sums.pop(hd)
@@ -412,23 +426,11 @@ def tile_quantumkernelattention_t_kernel(tc, x, out):
         mx = {}
 
         def mx_product(hd, u):
-            mx[hd, u] = psum.tile([P, DK], F32, name="mx", tag="mx", bufs=2)
+            mx[hd, u] = table_bank() if hd >= HEADS - 2 and u % 2 else psum.tile([P, DK], F32, name="mx", tag="mx", bufs=2)
             nc.tensor.matmul_mx(
                 out=mx[hd, u][:],
                 lhsT=packed_e[hd][0][:, u * P : (u + 1) * P].bitcast(FP8X4),
                 lhsT_scale=packed_e[hd][1][:, u * P : (u + 1) * P],
-                rhs=packed_x[hd][0][:].bitcast(FP8X4),
-                rhs_scale=packed_x[hd][1][:],
-                start=True,
-                stop=True,
-            )
-
-        def keep_warm(hd):
-            spare = psum.tile([P, DK], F32, name="mx", tag="mx", bufs=2)
-            nc.tensor.matmul_mx(
-                out=spare[:],
-                lhsT=packed_e[hd][0][:, 0:P].bitcast(FP8X4),
-                lhsT_scale=packed_e[hd][1][:, 0:P],
                 rhs=packed_x[hd][0][:].bitcast(FP8X4),
                 rhs_scale=packed_x[hd][1][:],
                 start=True,
@@ -452,52 +454,60 @@ def tile_quantumkernelattention_t_kernel(tc, x, out):
         def round_of(r):
             old, last, new, next_new = r - 2, r - 1, r + 1, r + 2
 
-            def product(u):
+            def product(*us):
                 if exists(old):
-                    mx_product(old, u)
+                    for u in us:
+                        mx_product(old, u)
 
-            def divide(u):
+            def divide(*us):
                 if exists(old):
-                    divide_and_store(old, u, r >= HEADS and u % 2 == 1)
+                    for u in us:
+                        divide_and_store(old, u, r != HEADS and r >= HEADS - 1 and u % 2 == 1)
 
             def factors_of(k):
                 if (r, k) in table:
                     multiply_bank(r, k)
 
-            def warm_passes(n):
-                if exists(old):
-                    for i in range(n):
-                        keep_warm(old)
-
-            product(0)
-            product(1)
+            product(0, 1)
             if r >= 0 and exists(r + 3):
                 load_fixed(r + 3)
+            if r % H and X_FIRST <= (r + 5) // H < B:
+                load_x((r + 5) // H)
             if exists(last):
                 regroup_e_on_gpsimd(last)
             if exists(r + 3):
                 make_terms(r + 3)
             factors_of(0)
             spread_next()
-            divide(0)
-            product(2)
-            factors_of(1)
-            spread_next()
-            divide(1)
-            product(3)
-            divide(2)
+            if r != HEADS - 1:
+                divide(0, 1)
+            else:
+                divide(0)
             if exists(new):
                 near_blocks(new, 0)
-            if exists(r):
-                near_magnitudes(r)
-            factors_of(2)
-            divide(3)
+            factors_of(1)
             spread_next()
-            if exists(new):
-                near_blocks(new, 1)
+            if r != HEADS - 1:
+                product(2, 3)
+            else:
+                product(2)
+            if exists(r) and r != HEADS - 1:
+                near_magnitudes(r)
+            if r == 0:
+                nc.scalar.activation(out=warm[:], in_=minus_one[:], func=ACT.Exp)
+            factors_of(2)
+            if r != HEADS - 1:
+                divide(2, 3)
+            else:
+                divide(2)
+                near_magnitudes(r)
+            spread_next()
             factors_of(3)
             spread_next()
-            warm_passes(2)
+            if r == HEADS - 1:
+                divide(1)
+            if exists(new):
+                near_blocks(new, 1)
             if exists(r):
                 far_magnitudes(r)
             if r == -1:
@@ -505,28 +515,32 @@ def tile_quantumkernelattention_t_kernel(tc, x, out):
                 gather_columns()
                 park_columns()
                 load_fixed(2)
-                for b in range(X_FIRST, B):
-                    load_x(b)
-            if exists(new):
-                join(new)
+            if r == HEADS:
+                quantise_x(last)
             if exists(last):
                 regroup_e(last)
                 add_sums(last)
+            if r == HEADS - 1:
+                product(3)
+                divide(3)
+            if exists(new):
+                new_score(new)
+                join(new, 0)
+                join(new, 1)
             if exists(r):
                 exponentials_of_blocks(r)
                 mirrors(r)
-                warm_passes(1)
                 exponentials_of_mirrors(r)
                 score.pop(r)
             if exists(last):
-                quantise_x(last)
                 quantise_e(last)
+                if r < HEADS:
+                    quantise_x(last)
                 invert_sums(last)
             if r == 1:
                 invert(B // 2, B)
             if exists(next_new):
                 turn_terms(next_new)
-                warm_passes(1)
                 copy_terms(next_new)
             if r == 1:
                 ratios(B // 2, B)

@@ -348,11 +348,13 @@ def tile_quantumkernelattention_t_kernel(tc, x, out):
                 out=e_tile[hd][:, t, lo : lo + n], in_=src, func=ACT.Exp, bias=minus_one[:], accum_out=sum_out
             )
 
-        def exponentials_of_blocks(hd):
+        def start_e(hd):
             sums[hd] = work.tile([P, 2, T], F32, name="sums", bufs=3)
             total[hd] = work.tile([P, T], F32, name="total", bufs=3)
             e_tile[hd] = work.tile([P, T, S], BF16, name="e", bufs=2)
-            for t in (2, 3, 0, 1):
+
+        def exponentials_of_rows(hd, *rows_of_blocks):
+            for t in rows_of_blocks:
                 exponential(
                     hd, t, t * P, (T - t) * P, block(hd, t, t, T - t), sums[hd][:, 1, t : t + 1] if t else total[hd][:, 0:1]
                 )
@@ -417,7 +419,7 @@ def tile_quantumkernelattention_t_kernel(tc, x, out):
 
         def add_sums(hd):
             both = sums.pop(hd)
-            nc.vector.tensor_tensor(out=total[hd][:, 1:T], in0=both[:, 0, 1:T], in1=both[:, 1, 1:T], op=ALU.add)
+            nc.gpsimd.tensor_tensor(out=total[hd][:, 1:T], in0=both[:, 0, 1:T], in1=both[:, 1, 1:T], op=ALU.add)
 
         def invert_sums(hd):
             inverse[hd] = work.tile([P, T], F32, name="inverse", bufs=3)
@@ -474,6 +476,7 @@ def tile_quantumkernelattention_t_kernel(tc, x, out):
             if r % H and X_FIRST <= (r + 5) // H < B:
                 load_x((r + 5) // H)
             if exists(last):
+                add_sums(last)
                 regroup_e_on_gpsimd(last)
             if exists(r + 3):
                 make_terms(r + 3)
@@ -502,13 +505,15 @@ def tile_quantumkernelattention_t_kernel(tc, x, out):
                 divide(2)
                 near_magnitudes(r)
             spread_next()
+            if exists(new):
+                near_blocks(new, 1)
             factors_of(3)
             spread_next()
             if r == HEADS - 1:
                 divide(1)
-            if exists(new):
-                near_blocks(new, 1)
             if exists(r):
+                start_e(r)
+                exponentials_of_rows(r, 2, 3)
                 far_magnitudes(r)
             if r == -1:
                 seventh_ratios()
@@ -517,25 +522,24 @@ def tile_quantumkernelattention_t_kernel(tc, x, out):
                 load_fixed(2)
             if r == HEADS:
                 quantise_x(last)
-            if exists(last):
-                regroup_e(last)
-                add_sums(last)
-            if r == HEADS - 1:
-                product(3)
-                divide(3)
             if exists(new):
                 new_score(new)
                 join(new, 0)
                 join(new, 1)
+            if exists(last):
+                regroup_e(last)
+            if r == HEADS - 1:
+                product(3)
+                divide(3)
             if exists(r):
-                exponentials_of_blocks(r)
+                exponentials_of_rows(r, 0, 1)
                 mirrors(r)
                 exponentials_of_mirrors(r)
                 score.pop(r)
             if exists(last):
-                quantise_e(last)
                 if r < HEADS:
                     quantise_x(last)
+                quantise_e(last)
                 invert_sums(last)
             if r == 1:
                 invert(B // 2, B)

@@ -23,8 +23,9 @@ HALF = NW // 2
 FAR = 2 * P
 ROW = (0, 512, 896, 1152)
 BLOCKS = 1280
-E_ON_VECTOR = 256
+E_ON_VECTOR = 320
 X_FIRST = 2
+EXTRA, EXTRA_OF = 3, 8
 TABLES = 3
 TWO_PI_HIGH = 6.28125
 TWO_PI_LOW = 2.0 * math.pi - TWO_PI_HIGH
@@ -85,7 +86,7 @@ def tile_quantumkernelattention_t_kernel(tc, x, out):
         columns = const.tile([P, P], F32, name="columns")
         rows = const.tile([P, P], F32, name="rows")
         inverse_7 = const.tile([P, 2, NTOK], F32, name="inverse_7")
-        inverse_ratio_7 = const.tile([P, NTOK], F32, name="inverse_ratio_7")
+        cotangent_7 = const.tile([P, NTOK], F32, name="cotangent_7")
         last_two = const.tile([P, NTOK, 2], F32, name="last_two")
         pairs = [const.tile([P, NTOK, 2, 2], F32, name="pair%d" % q) for q in range(3)]
         sixteen = const.tile([P, NTOK, 4, 4], F32, name="sixteen")
@@ -96,7 +97,7 @@ def tile_quantumkernelattention_t_kernel(tc, x, out):
         def times(engine, dst, a, c):
             engine.tensor_tensor(out=dst, in0=a, in1=c, op=ALU.mult)
 
-        def angles(b0, b1):
+        def angles(second, b0, b1):
             c = slice(b0 * PER_BATCH, b1 * PER_BATCH)
             nc.vector.tensor_scalar(
                 out=turns[:, c], in0=first8[:, c], scalar1=1.0 / (2.0 * math.pi), scalar2=0.25, op0=ALU.mult, op1=ALU.add
@@ -107,62 +108,80 @@ def tile_quantumkernelattention_t_kernel(tc, x, out):
             nc.vector.scalar_tensor_tensor(
                 out=full[:, c], in0=turns[:, c], scalar=-TWO_PI_LOW, in1=part[:, c], op0=ALU.mult, op1=ALU.add
             )
-            half = T * H * NW // 2
-
-            def slots(a, pair):
-                return a.rearrange("p (b s k) -> p b s k", s=2, k=half)[:, :, pair, :]
-
-            for i in range(2):
-                for pair in range(2):
-                    nc.vector.tensor_scalar(
-                        out=slots(angle[:, i, c], pair),
-                        in0=slots(full[:, c], pair),
-                        scalar1=-PI_BELOW - math.pi / 2,
-                        scalar2=math.pi / 2 if i == pair else -math.pi / 2,
-                        op0=ALU.max,
-                        op1=ALU.add,
-                    )
+            nc.vector.tensor_scalar(
+                out=angle[:, 0, c],
+                in0=full[:, c],
+                scalar1=-PI_BELOW - math.pi / 2,
+                scalar2=-math.pi / 2,
+                op0=ALU.max,
+                op1=ALU.add,
+            )
+            second.tensor_scalar(
+                out=angle[:, 1, c], in0=full[:, c], scalar1=1.0, scalar2=math.pi / 2, op0=ALU.mult, op1=ALU.add
+            )
 
         def sines(b0, b1):
             c = slice(b0 * PER_BATCH, b1 * PER_BATCH)
             nc.scalar.activation(out=trig[:, :, c], in_=angle[:, :, c], func=ACT.Sin, scale=0.5)
 
+        def by_pair(a, b0, b1, pair, width):
+            n = T * H * width
+            return a[:, b0 * n : b1 * n].rearrange("p (b s k) -> p b s k", s=2, k=n // 2)[:, :, pair, :]
+
         def invert(b0, b1):
-            c = slice(b0 * PER_BATCH, b1 * PER_BATCH)
-            nc.vector.reciprocal(out=inverse_den[:, c], in_=trig[:, 0, c])
+            for pair in range(2):
+                nc.vector.reciprocal(
+                    out=by_pair(inverse_den, b0, b1, pair, NW), in_=by_pair(trig[:, 1 - pair, :], b0, b1, pair, NW)
+                )
 
         def ratios(b0, b1):
-            c = slice(b0 * PER_BATCH, b1 * PER_BATCH)
-            times(nc.vector, ratio[:, c], trig[:, 1, c], inverse_den[:, c])
+            for pair in range(2):
+                times(
+                    nc.vector,
+                    by_pair(ratio, b0, b1, pair, NW),
+                    by_pair(trig[:, pair, :], b0, b1, pair, NW),
+                    by_pair(inverse_den, b0, b1, pair, NW),
+                )
 
         def den_products(engine, b0, b1):
             k = slice(b0 * T * H, b1 * T * H)
-            den = by_feature[:, k, 0, :]
-            times(engine, den_4[:, k], den[:, :, 0:4], den[:, :, 4:8])
+            for pair in range(2):
+                den = by_pair(trig[:, 1 - pair, :], b0, b1, pair, NW).rearrange("p b (k w) -> p b k w", w=NW)
+                dst = by_pair(den_4[:].rearrange("p k w -> p (k w)"), b0, b1, pair, 4)
+                times(engine, dst.rearrange("p b (k w) -> p b k w", w=4), den[:, :, :, 0:4], den[:, :, :, 4:8])
             times(engine, den_2[:, k], den_4[:, k, 0:2], den_4[:, k, 2:4])
             times(engine, den_all[:, k], den_2[:, k, 0:1], den_2[:, k, 1:2])
 
-        def seventh_ratios():
-            both = by_feature[:, :, :, 7].rearrange("p k c -> p c k")
-            nc.vector.reciprocal(out=inverse_7[:], in_=both)
-            times(nc.vector, inverse_ratio_7[:], both[:, 0, :], inverse_7[:, 1, :])
+        def seventh(b0, b1):
+            k = slice(b0 * T * H, b1 * T * H)
+            return k, by_feature[:, k, :, 7].rearrange("p k c -> p c k")
+
+        def invert_seventh(b0, b1):
+            k, both = seventh(b0, b1)
+            nc.vector.reciprocal(out=inverse_7[:, :, k], in_=both)
+
+        def seventh_ratios(engine, b0, b1):
+            k, both = seventh(b0, b1)
             times(
-                nc.vector,
-                columns[:, 0:NTOK].rearrange("p (b h t) -> p b h t", h=H, t=T),
+                engine,
+                columns[:, k].rearrange("p (b h t) -> p b h t", h=H, t=T),
                 both[:, 1, :].rearrange("p (b t h) -> p b h t", h=H, t=T),
-                inverse_7[:, 0, :].rearrange("p (b t h) -> p b h t", h=H, t=T),
+                inverse_7[:, 0, k].rearrange("p (b t h) -> p b h t", h=H, t=T),
             )
+            times(engine, cotangent_7[:, k], both[:, 0, :], inverse_7[:, 1, k])
 
         def gather_columns():
-            nc.vector.tensor_copy(
+            nc.gpsimd.tensor_copy(
                 out=columns[:, NTOK : NTOK + 2 * HEADS].rearrange("p (b h t) -> p b h t", h=H, t=2),
                 in_=den_all[:].rearrange("p (b t h) w -> p b h (t w)", t=T, h=H)[:, :, :, 2:4],
             )
 
-        def park_columns():
-            turned_columns = side_bank()
-            nc.tensor.transpose(out=turned_columns[:, 0:P], in_=columns[:], identity=identity[:])
-            invert(1, B // 2)
+        def turn_columns():
+            bank = side_bank()
+            nc.tensor.transpose(out=bank[:, 0:P], in_=columns[:], identity=identity[:])
+            return bank
+
+        def park_columns(turned_columns):
             nc.vector.tensor_copy(out=rows[:], in_=turned_columns[:, 0:P])
             nc.sync.dma_start(out=parked.rearrange("(k p) -> k p", p=P), in_=rows[0 : NTOK + 2 * HEADS, :])
 
@@ -198,6 +217,9 @@ def tile_quantumkernelattention_t_kernel(tc, x, out):
         def side_bank():
             return psum.tile([P, S], F32, name="side", tag="side", bufs=3)
 
+        def near_blocks_of_row(hd, t):
+            return (2, 1)[t % 2] + (1 if t == 0 and EXTRA * hd % EXTRA_OF < EXTRA else 0)
+
         def token(hd, t):
             b, h = divmod(hd, H)
             return (b * T + t) * H + h
@@ -205,6 +227,9 @@ def tile_quantumkernelattention_t_kernel(tc, x, out):
         def ratio_of(hd, t, w):
             c = token(hd, t) * NW + w
             return ratio[:, c : c + 1]
+
+        def tangent_7_of(hd, t):
+            return columns[:, hd * T + t : hd * T + t + 1]
 
         def den_of(hd, t):
             return den_all[:, token(hd, t), :]
@@ -238,7 +263,7 @@ def tile_quantumkernelattention_t_kernel(tc, x, out):
         def spread_fixed(hd):
             new_fixed(hd)
             for lo, columns_of, slots in (
-                (0, lambda t: ratio_of(hd, t, 7), (0, 1, 2, 3)),
+                (0, lambda t: tangent_7_of(hd, t), (0, 1, 2, 3)),
                 (S, lambda t: den_of(hd, t), (2, 3)),
             ):
                 bank = table_bank()
@@ -264,11 +289,13 @@ def tile_quantumkernelattention_t_kernel(tc, x, out):
                 if j == 0:
                     running[hd] = work.tile([P, 2, FAR], F32, name="running", bufs=3)
                 for t in range(2):
+                    u = t + near_blocks_of_row(hd, t)
+                    lo = (u - 2) * P
                     nc.vector.scalar_tensor_tensor(
-                        out=block(hd, t, 2, 2) if j == NW - 1 else running[hd][:, t, :],
-                        in0=table[r, k][:, at : at + FAR],
+                        out=block(hd, t, u, T - u) if j == NW - 1 else running[hd][:, t, lo:FAR],
+                        in0=table[r, k][:, at + lo : at + FAR],
                         scalar=ratio_of(hd, t, j),
-                        in1=running[hd][:, t, :] if j else fixed[hd][:, S : S + FAR],
+                        in1=running[hd][:, t, lo:FAR] if j else fixed[hd][:, S + lo : S + FAR],
                         op0=ALU.add,
                         op1=ALU.mult,
                     )
@@ -293,40 +320,44 @@ def tile_quantumkernelattention_t_kernel(tc, x, out):
 
         def near_blocks(hd, pair):
             near[hd, pair] = side_bank()
-            t = 2 * pair
-            for row, at in ((t, 0), (t + 1, FAR)):
+            at = 0
+            for t in (2 * pair, 2 * pair + 1):
+                n = near_blocks_of_row(hd, t)
                 nc.tensor.matmul(
-                    out=near[hd, pair][:, at : at + (t + 2 - row) * P],
-                    lhsT=by_token[hd][:, row * P : (row + 1) * P],
-                    rhs=by_token[hd][:, row * P : (t + 2) * P],
+                    out=near[hd, pair][:, at : at + n * P],
+                    lhsT=by_token[hd][:, t * P : (t + 1) * P],
+                    rhs=by_token[hd][:, t * P : (t + n) * P],
                     start=True,
                     stop=True,
                 )
+                at += n * P
 
         def new_score(hd):
             score[hd] = work.tile([P, BLOCKS], F32, name="score", bufs=3)
 
         def join(hd, pair):
+            at = 0
             for t in (2 * pair, 2 * pair + 1):
-                second = t % 2
-                n = (2 - second) * P
+                n = near_blocks_of_row(hd, t)
                 nc.vector.scalar_tensor_tensor(
-                    out=block(hd, t, t, 2 - second),
-                    in0=fixed[hd][:, t * P : t * P + n],
-                    scalar=inverse_ratio_7[:, token(hd, t) : token(hd, t) + 1],
-                    in1=near[hd, pair][:, second * FAR : second * FAR + n],
+                    out=block(hd, t, t, n),
+                    in0=fixed[hd][:, t * P : (t + n) * P],
+                    scalar=cotangent_7[:, token(hd, t) : token(hd, t) + 1],
+                    in1=near[hd, pair][:, at : at + n * P],
                     op0=ALU.add,
                     op1=ALU.mult,
                 )
+                at += n * P
 
         def near_magnitudes(hd):
             for t in range(T):
-                part_of_row = block(hd, t, t, 2 - t % 2)
-                nc.scalar.activation(out=part_of_row, in_=part_of_row, func=ACT.Abs, scale=ratio_of(hd, t, 7))
+                part_of_row = block(hd, t, t, near_blocks_of_row(hd, t))
+                nc.scalar.activation(out=part_of_row, in_=part_of_row, func=ACT.Abs, scale=tangent_7_of(hd, t))
 
         def far_magnitudes(hd):
             for t in range(2):
-                part_of_row = block(hd, t, 2, 2)
+                u = t + near_blocks_of_row(hd, t)
+                part_of_row = block(hd, t, u, T - u)
                 nc.scalar.activation(out=part_of_row, in_=part_of_row, func=ACT.Abs, scale=den_of(hd, t))
 
         mirror = {}
@@ -381,7 +412,7 @@ def tile_quantumkernelattention_t_kernel(tc, x, out):
             regroup_on_gpsimd(grouped_x[hd][:], x_tile[b][:, :, h * DK : (h + 1) * DK])
 
         def on_vector(hd):
-            return E_ON_VECTOR if hd < HEADS - 1 else S
+            return E_ON_VECTOR if 0 < hd < HEADS - 1 else S
 
         def regroup_e_on_gpsimd(hd):
             grouped_e[hd] = work.tile([P, S, T], BF16, name="grouped_e", bufs=2, align_bytes=64)
@@ -471,6 +502,8 @@ def tile_quantumkernelattention_t_kernel(tc, x, out):
                     multiply_bank(r, k)
 
             product(0, 1)
+            if r == 1:
+                invert(B // 2, B)
             if r >= 0 and exists(r + 3):
                 load_fixed(r + 3)
             if r % H and X_FIRST <= (r + 5) // H < B:
@@ -478,22 +511,27 @@ def tile_quantumkernelattention_t_kernel(tc, x, out):
             if exists(last):
                 add_sums(last)
                 regroup_e_on_gpsimd(last)
-            if exists(r + 3):
+            if r >= 0 and exists(r + 3):
                 make_terms(r + 3)
             factors_of(0)
             spread_next()
+            if r == -1:
+                turn_terms(0)
+                copy_terms(0)
+            if exists(new):
+                near_blocks(new, 0)
             if r != HEADS - 1:
                 divide(0, 1)
             else:
                 divide(0)
-            if exists(new):
-                near_blocks(new, 0)
-            factors_of(1)
-            spread_next()
             if r != HEADS - 1:
                 product(2, 3)
             else:
                 product(2)
+            if exists(new):
+                near_blocks(new, 1)
+            factors_of(1)
+            spread_next()
             if exists(r) and r != HEADS - 1:
                 near_magnitudes(r)
             if r == 0:
@@ -505,8 +543,6 @@ def tile_quantumkernelattention_t_kernel(tc, x, out):
                 divide(2)
                 near_magnitudes(r)
             spread_next()
-            if exists(new):
-                near_blocks(new, 1)
             factors_of(3)
             spread_next()
             if r == HEADS - 1:
@@ -516,16 +552,23 @@ def tile_quantumkernelattention_t_kernel(tc, x, out):
                 exponentials_of_rows(r, 2, 3)
                 far_magnitudes(r)
             if r == -1:
-                seventh_ratios()
-                gather_columns()
-                park_columns()
-                load_fixed(2)
+                invert_seventh(1, B)
+                seventh_ratios(nc.gpsimd, 1, B)
+                make_terms(1)
+                factors(1, B)
+                make_terms(2)
+                regroup_x(0)
+                turned_columns = turn_columns()
+                invert(1, B // 2)
             if r == HEADS:
                 quantise_x(last)
             if exists(new):
                 new_score(new)
                 join(new, 0)
                 join(new, 1)
+            if r == -1:
+                park_columns(turned_columns)
+                load_fixed(2)
             if exists(last):
                 regroup_e(last)
             if r == HEADS - 1:
@@ -536,37 +579,35 @@ def tile_quantumkernelattention_t_kernel(tc, x, out):
                 mirrors(r)
                 exponentials_of_mirrors(r)
                 score.pop(r)
+            if r == 1:
+                ratios(B // 2, B)
             if exists(last):
                 if r < HEADS:
                     quantise_x(last)
                 quantise_e(last)
                 invert_sums(last)
-            if r == 1:
-                invert(B // 2, B)
             if exists(next_new):
                 turn_terms(next_new)
                 copy_terms(next_new)
-            if r == 1:
-                ratios(B // 2, B)
             if exists(new) and new > 0:
                 regroup_x(new)
 
-        angles(0, 1)
+        angles(nc.vector, 0, 1)
         sines(0, 1)
         invert(0, 1)
-        den_products(nc.vector, 0, 1)
+        den_products(nc.gpsimd, 0, 1)
+        invert_seventh(0, 1)
         ratios(0, 1)
+        seventh_ratios(nc.vector, 0, 1)
         factors(0, 1)
-        make_terms(0)
         spread_fixed(0)
         for i in range(TABLES):
             spread_next()
-        round_of(-2)
-        angles(1, B)
+        angles(nc.gpsimd, 1, B)
+        make_terms(0)
         sines(1, B)
         den_products(nc.gpsimd, 1, B)
-        factors(1, B)
-        regroup_x(0)
+        gather_columns()
         spread_fixed(1)
         round_of(-1)
         ratios(1, B // 2)

@@ -23,7 +23,8 @@ HALF = NW // 2
 FAR = 2 * P
 ROW = (0, 512, 896, 1152)
 BLOCKS = 1280
-E_ON_VECTOR = 320
+E_ON_VECTOR = 256
+X_ON_SCALAR = 96
 X_FIRST = 2
 EXTRA, EXTRA_OF = 3, 8
 TABLES = 3
@@ -182,7 +183,7 @@ def tile_quantumkernelattention_t_kernel(tc, x, out):
             return bank
 
         def park_columns(turned_columns):
-            nc.vector.tensor_copy(out=rows[:], in_=turned_columns[:, 0:P])
+            nc.scalar.copy(out=rows[:], in_=turned_columns[:, 0:P])
             nc.sync.dma_start(out=parked.rearrange("(k p) -> k p", p=P), in_=rows[0 : NTOK + 2 * HEADS, :])
 
         def outer(engine, dst, left, n_left, right, n_right):
@@ -218,7 +219,7 @@ def tile_quantumkernelattention_t_kernel(tc, x, out):
             return psum.tile([P, S], F32, name="side", tag="side", bufs=3)
 
         def near_blocks_of_row(hd, t):
-            return (2, 1)[t % 2] + (1 if t == 0 and EXTRA * hd % EXTRA_OF < EXTRA else 0)
+            return (2, 1)[t % 2] + (1 if t == 0 and (EXTRA * hd + 5) % EXTRA_OF < EXTRA else 0)
 
         def token(hd, t):
             b, h = divmod(hd, H)
@@ -406,13 +407,21 @@ def tile_quantumkernelattention_t_kernel(tc, x, out):
                 out=dst, in0=src.rearrange("p t c -> p c t"), scalar1=1.0, scalar2=0.0, op0=ALU.mult, op1=ALU.add
             )
 
-        def regroup_x(hd):
+        def x_of(hd):
             b, h = divmod(hd, H)
+            return x_tile[b][:, :, h * DK : (h + 1) * DK]
+
+        def regroup_x(hd):
             grouped_x[hd] = work.tile([P, DK, T], BF16, name="grouped_x", bufs=2, align_bytes=64)
-            regroup_on_gpsimd(grouped_x[hd][:], x_tile[b][:, :, h * DK : (h + 1) * DK])
+            n = DK - X_ON_SCALAR
+            regroup_on_gpsimd(grouped_x[hd][:, 0:n], x_of(hd)[:, :, 0:n])
+
+        def regroup_x_on_scalar(hd):
+            n = DK - X_ON_SCALAR
+            nc.scalar.copy(out=grouped_x[hd][:, n:DK], in_=x_of(hd)[:, :, n:DK].rearrange("p t c -> p c t"))
 
         def on_vector(hd):
-            return E_ON_VECTOR if 0 < hd < HEADS - 1 else S
+            return E_ON_VECTOR if 0 < hd < HEADS - 2 else S
 
         def regroup_e_on_gpsimd(hd):
             grouped_e[hd] = work.tile([P, S, T], BF16, name="grouped_e", bufs=2, align_bytes=64)
@@ -534,6 +543,8 @@ def tile_quantumkernelattention_t_kernel(tc, x, out):
             spread_next()
             if exists(r) and r != HEADS - 1:
                 near_magnitudes(r)
+            if exists(r):
+                regroup_x_on_scalar(r)
             if r == 0:
                 nc.scalar.activation(out=warm[:], in_=minus_one[:], func=ACT.Exp)
             factors_of(2)

import math
from contextlib import ExitStack

import concourse.mybir as mybir
from concourse.masks import make_identity

B, S, H, DK, NW = 8, 512, 2, 512, 8
FLOPS = 2 * B * H * S * S * DK

F32 = mybir.dt.float32
BF16 = mybir.dt.bfloat16
I32 = mybir.dt.int32
U32 = mybir.dt.uint32
U8 = mybir.dt.uint8
FP8X4 = mybir.dt.float8_e4m3fn_x4
ALU = mybir.AluOpType
ACT = mybir.ActivationFunctionType

P = 128
T = 4
HEADS = B * H
HALF = NW // 2
FAR = 2 * P
ROW = (0, 512, 896, 1152)
BLOCKS = 1280
E_ON_VECTOR = 256
X_ON_SCALAR = 96
X_FIRST = 2
EXTRA, EXTRA_OF = 3, 8
TABLES = 3
TWO_PI_HIGH = 6.28125
TWO_PI_LOW = 2.0 * math.pi - TWO_PI_HIGH
PI_BELOW = 3.1415925025939941


def tile_quantumkernelattention_t_kernel(tc, x, out):
    nc = tc.nc
    with ExitStack() as ctx:
        ctx.enter_context(tc.manual_schedule())
        const = ctx.enter_context(tc.tile_pool(name="const", bufs=1))
        work = ctx.enter_context(tc.tile_pool(name="work", bufs=2))
        psum = ctx.enter_context(tc.psum_pool(name="psum", bufs=1))

        PER_BATCH = T * H * NW
        NCOL = B * PER_BATCH
        NTOK = B * T * H
        first8 = const.tile([P, NCOL], BF16, name="first8")

        def load_first8(b):
            nc.sync.dma_start(
                out=first8[:, b * PER_BATCH : (b + 1) * PER_BATCH].rearrange("p (k w) -> p k w", w=NW),
                in_=x[b].rearrange("(p t) (h d) -> p (t h) d", t=T, h=H)[:, :, 0:NW],
            )

        x_tile = {}

        def load_x(b):
            x_tile[b] = work.tile([P, T, H * DK], BF16, name="x_tile", bufs=B)
            nc.sync.dma_start(out=x_tile[b][:], in_=x[b].rearrange("(p t) e -> p t e", t=T))

        for b in range(B):
            load_first8(b)
        for b in range(X_FIRST):
            load_x(b)

        parked = out[B - 1].rearrange("s e -> (s e)")[0 : (NTOK + 2 * HEADS) * P]
        identity = const.tile([P, P], F32, name="identity")
        make_identity(nc, identity[:])
        minus_one = const.tile([P, 1], F32, name="minus_one")
        nc.vector.memset(minus_one[:], -1.0)
        one = const.tile([P, 1], F32, name="one")
        nc.vector.memset(one[:], 1.0)
        warm = const.tile([P, 1], F32, name="warm")
        nc.scalar.activation(out=warm[:], in_=minus_one[:], func=ACT.Sin)

        turns = const.tile([P, NCOL], I32, name="turns")
        part = const.tile([P, NCOL], F32, name="part")
        full = const.tile([P, NCOL], F32, name="full")
        angle = const.tile([P, 2, NCOL], F32, name="angle")
        trig = const.tile([P, 2, NCOL], F32, name="trig")
        inverse_den = const.tile([P, NCOL], F32, name="inverse_den")
        ratio = const.tile([P, NCOL], F32, name="ratio")
        den_4 = const.tile([P, NTOK, 4], F32, name="den_4")
        den_2 = const.tile([P, NTOK, 2], F32, name="den_2")
        den_all = const.tile([P, NTOK, 1], F32, name="den_all")
        by_feature = trig[:].rearrange("p c (k w) -> p k c w", w=NW)
        columns = const.tile([P, P], F32, name="columns")
        rows = const.tile([P, P], F32, name="rows")
        inverse_7 = const.tile([P, 2, NTOK], F32, name="inverse_7")
        cotangent_7 = const.tile([P, NTOK], F32, name="cotangent_7")
        last_two = const.tile([P, NTOK, 2], F32, name="last_two")
        pairs = [const.tile([P, NTOK, 2, 2], F32, name="pair%d" % q) for q in range(3)]
        sixteen = const.tile([P, NTOK, 4, 4], F32, name="sixteen")
        eight = const.tile([P, NTOK, 4, 2], F32, name="eight")

        nc.gpsimd.memset(columns[:, NTOK + 2 * HEADS : P], 0.0)

        def times(engine, dst, a, c):
            engine.tensor_tensor(out=dst, in0=a, in1=c, op=ALU.mult)

        def angles(second, b0, b1):
            c = slice(b0 * PER_BATCH, b1 * PER_BATCH)
            nc.vector.tensor_scalar(
                out=turns[:, c], in0=first8[:, c], scalar1=1.0 / (2.0 * math.pi), scalar2=0.25, op0=ALU.mult, op1=ALU.add
            )
            nc.vector.scalar_tensor_tensor(
                out=part[:, c], in0=turns[:, c], scalar=-TWO_PI_HIGH, in1=first8[:, c], op0=ALU.mult, op1=ALU.add
            )
            nc.vector.scalar_tensor_tensor(
                out=full[:, c], in0=turns[:, c], scalar=-TWO_PI_LOW, in1=part[:, c], op0=ALU.mult, op1=ALU.add
            )
            nc.vector.tensor_scalar(
                out=angle[:, 0, c],
                in0=full[:, c],
                scalar1=-PI_BELOW - math.pi / 2,
                scalar2=-math.pi / 2,
                op0=ALU.max,
                op1=ALU.add,
            )
            second.tensor_scalar(
                out=angle[:, 1, c], in0=full[:, c], scalar1=1.0, scalar2=math.pi / 2, op0=ALU.mult, op1=ALU.add
            )

        def sines(b0, b1):
            c = slice(b0 * PER_BATCH, b1 * PER_BATCH)
            nc.scalar.activation(out=trig[:, :, c], in_=angle[:, :, c], func=ACT.Sin, scale=0.5)

        def by_pair(a, b0, b1, pair, width):
            n = T * H * width
            return a[:, b0 * n : b1 * n].rearrange("p (b s k) -> p b s k", s=2, k=n // 2)[:, :, pair, :]

        def invert(b0, b1):
            for pair in range(2):
                nc.vector.reciprocal(
                    out=by_pair(inverse_den, b0, b1, pair, NW), in_=by_pair(trig[:, 1 - pair, :], b0, b1, pair, NW)
                )

        def ratios(b0, b1):
            for pair in range(2):
                times(
                    nc.vector,
                    by_pair(ratio, b0, b1, pair, NW),
                    by_pair(trig[:, pair, :], b0, b1, pair, NW),
                    by_pair(inverse_den, b0, b1, pair, NW),
                )

        def den_products(engine, b0, b1):
            k = slice(b0 * T * H, b1 * T * H)
            for pair in range(2):
                den = by_pair(trig[:, 1 - pair, :], b0, b1, pair, NW).rearrange("p b (k w) -> p b k w", w=NW)
                dst = by_pair(den_4[:].rearrange("p k w -> p (k w)"), b0, b1, pair, 4)
                times(engine, dst.rearrange("p b (k w) -> p b k w", w=4), den[:, :, :, 0:4], den[:, :, :, 4:8])
            times(engine, den_2[:, k], den_4[:, k, 0:2], den_4[:, k, 2:4])
            times(engine, den_all[:, k], den_2[:, k, 0:1], den_2[:, k, 1:2])

        def seventh(b0, b1):
            k = slice(b0 * T * H, b1 * T * H)
            return k, by_feature[:, k, :, 7].rearrange("p k c -> p c k")

        def invert_seventh(b0, b1):
            k, both = seventh(b0, b1)
            nc.vector.reciprocal(out=inverse_7[:, :, k], in_=both)

        def seventh_ratios(engine, b0, b1):
            k, both = seventh(b0, b1)
            times(
                engine,
                columns[:, k].rearrange("p (b h t) -> p b h t", h=H, t=T),
                both[:, 1, :].rearrange("p (b t h) -> p b h t", h=H, t=T),
                inverse_7[:, 0, k].rearrange("p (b t h) -> p b h t", h=H, t=T),
            )
            times(engine, cotangent_7[:, k], both[:, 0, :], inverse_7[:, 1, k])

        def gather_columns():
            nc.gpsimd.tensor_copy(
                out=columns[:, NTOK : NTOK + 2 * HEADS].rearrange("p (b h t) -> p b h t", h=H, t=2),
                in_=den_all[:].rearrange("p (b t h) w -> p b h (t w)", t=T, h=H)[:, :, :, 2:4],
            )

        def turn_columns():
            bank = side_bank()
            nc.tensor.transpose(out=bank[:, 0:P], in_=columns[:], identity=identity[:])
            return bank

        def park_columns(turned_columns):
            nc.scalar.copy(out=rows[:], in_=turned_columns[:, 0:P])
            nc.sync.dma_start(out=parked.rearrange("(k p) -> k p", p=P), in_=rows[0 : NTOK + 2 * HEADS, :])

        def outer(engine, dst, left, n_left, right, n_right):
            shape = [P, dst.shape[1], n_left, n_right]
            times(engine, dst, left.unsqueeze(3).to_broadcast(shape), right.unsqueeze(2).to_broadcast(shape))

        def factors(b0, b1):
            k = slice(b0 * T * H, b1 * T * H)
            n = (b1 - b0) * T * H
            for q in range(3):
                outer(nc.gpsimd, pairs[q][:, k], by_feature[:, k, :, 2 * q], 2, by_feature[:, k, :, 2 * q + 1], 2)
            times(nc.gpsimd, last_two[:, k], by_feature[:, k, :, 6], by_feature[:, k, 0:1, 7].to_broadcast([P, n, 2]))
            flat = [pairs[q][:, k].rearrange("p k i j -> p k (i j)") for q in range(3)]
            outer(nc.gpsimd, sixteen[:, k], flat[0], 4, flat[1], 4)
            outer(nc.gpsimd, eight[:, k], flat[2], 4, last_two[:, k], 2)

        terms = {}

        def make_terms(hd):
            b, h = divmod(hd, H)
            terms[hd] = work.tile([P, T, 16, 8], F32, name="terms", bufs=2)
            k = slice(b * T * H + h, (b + 1) * T * H, H)
            outer(
                nc.gpsimd,
                terms[hd][:],
                sixteen[:, k].rearrange("p k i j -> p k (i j)"),
                16,
                eight[:, k].rearrange("p k i j -> p k (i j)"),
                8,
            )

        def side_bank():
            return psum.tile([P, S], F32, name="side", tag="side", bufs=3)

        def near_blocks_of_row(hd, t):
            return (2, 1)[t % 2] + (1 if t == 0 and (EXTRA * hd + 5) % EXTRA_OF < EXTRA else 0)

        def token(hd, t):
            b, h = divmod(hd, H)
            return (b * T + t) * H + h

        def ratio_of(hd, t, w):
            c = token(hd, t) * NW + w
            return ratio[:, c : c + 1]

        def tangent_7_of(hd, t):
            return columns[:, hd * T + t : hd * T + t + 1]

        def den_of(hd, t):
            return den_all[:, token(hd, t), :]

        def spread(bank, at, column):
            nc.tensor.transpose(out=bank[:, at : at + P], in_=column.to_broadcast([P, P]), identity=identity[:])

        queue = [(r, k) for r in range(-1, HEADS) for k in range(HALF)]
        table = {}

        def table_bank():
            return psum.tile([P, S], F32, name="table", tag="table", bufs=TABLES)

        def factors_of_bank(r, k):
            return [(hd, j, i * FAR) for i, (hd, j) in enumerate(((r, HALF + k), (r + 1, k))) if 0 <= hd < HEADS]

        def spread_next():
            if not queue or len(table) == TABLES:
                return
            r, k = queue.pop(0)
            table[r, k] = table_bank()
            for hd, j, at in factors_of_bank(r, k):
                for t in (2, 3):
                    spread(table[r, k], at + (t - 2) * P, ratio_of(hd, t, j))

        fixed = {}

        def new_fixed(hd):
            fixed[hd] = work.tile([P, S + FAR], F32, name="fixed", bufs=3)

        def spread_fixed(hd):
            new_fixed(hd)
            for lo, columns_of, slots in (
                (0, lambda t: tangent_7_of(hd, t), (0, 1, 2, 3)),
                (S, lambda t: den_of(hd, t), (2, 3)),
            ):
                bank = table_bank()
                for i, t in enumerate(slots):
                    spread(bank, i * P, columns_of(t))
                n = len(slots) * P
                nc.scalar.copy(out=fixed[hd][:, lo : lo + n], in_=bank[:, 0:n])

        def load_fixed(hd):
            new_fixed(hd)
            for lo, at, n in ((0, hd * S, S), (S, NTOK * P + hd * FAR, FAR)):
                nc.sync.dma_start(out=fixed[hd][:, lo : lo + n], in_=parked[at : at + n].partition_broadcast(P))

        score = {}
        running = {}

        def block(hd, t, u, n=1):
            lo = ROW[t] + (u - t) * P
            return score[hd][:, lo : lo + n * P]

        def multiply_bank(r, k):
            for hd, j, at in factors_of_bank(r, k):
                if j == 0:
                    running[hd] = work.tile([P, 2, FAR], F32, name="running", bufs=3)
                for t in range(2):
                    u = t + near_blocks_of_row(hd, t)
                    lo = (u - 2) * P
                    nc.vector.scalar_tensor_tensor(
                        out=block(hd, t, u, T - u) if j == NW - 1 else running[hd][:, t, lo:FAR],
                        in0=table[r, k][:, at + lo : at + FAR],
                        scalar=ratio_of(hd, t, j),
                        in1=running[hd][:, t, lo:FAR] if j else fixed[hd][:, S + lo : S + FAR],
                        op0=ALU.add,
                        op1=ALU.mult,
                    )
            table.pop((r, k))

        turned = {}
        by_token = {}
        near = {}

        def turn_terms(hd):
            turned[hd] = side_bank()
            for t in range(T):
                nc.tensor.transpose(
                    out=turned[hd][:, t * P : (t + 1) * P],
                    in_=terms[hd][:, t].rearrange("p i j -> p (i j)"),
                    identity=identity[:],
                )

        def copy_terms(hd):
            by_token[hd] = work.tile([P, S], F32, name="by_token", bufs=2)
            nc.scalar.copy(out=by_token[hd][:], in_=turned.pop(hd)[:])

        def near_blocks(hd, pair):
            near[hd, pair] = side_bank()
            at = 0
            for t in (2 * pair, 2 * pair + 1):
                n = near_blocks_of_row(hd, t)
                nc.tensor.matmul(
                    out=near[hd, pair][:, at : at + n * P],
                    lhsT=by_token[hd][:, t * P : (t + 1) * P],
                    rhs=by_token[hd][:, t * P : (t + n) * P],
                    start=True,
                    stop=True,
                )
                at += n * P

        def new_score(hd):
            score[hd] = work.tile([P, BLOCKS], F32, name="score", bufs=3)

        def join(hd, pair):
            at = 0
            for t in (2 * pair, 2 * pair + 1):
                n = near_blocks_of_row(hd, t)
                nc.vector.scalar_tensor_tensor(
                    out=block(hd, t, t, n),
                    in0=fixed[hd][:, t * P : (t + n) * P],
                    scalar=cotangent_7[:, token(hd, t) : token(hd, t) + 1],
                    in1=near[hd, pair][:, at : at + n * P],
                    op0=ALU.add,
                    op1=ALU.mult,
                )
                at += n * P

        def near_magnitudes(hd):
            for t in range(T):
                part_of_row = block(hd, t, t, near_blocks_of_row(hd, t))
                nc.scalar.activation(out=part_of_row, in_=part_of_row, func=ACT.Abs, scale=tangent_7_of(hd, t))

        def far_magnitudes(hd):
            for t in range(2):
                u = t + near_blocks_of_row(hd, t)
                part_of_row = block(hd, t, u, T - u)
                nc.scalar.activation(out=part_of_row, in_=part_of_row, func=ACT.Abs, scale=den_of(hd, t))

        mirror = {}

        def mirrors(hd):
            for i, blocks in enumerate((((0, 3), (1, 3), (2, 3), (0, 1)), ((0, 2), (1, 2)))):
                mirror[hd, i] = side_bank()
                for k, (t, u) in enumerate(blocks):
                    nc.tensor.transpose(
                        out=mirror[hd, i][:, k * P : (k + 1) * P], in_=block(hd, t, u), identity=identity[:]
                    )

        e_tile = {}
        sums = {}
        total = {}

        def exponential(hd, t, lo, n, src, sum_out):
            nc.scalar.activation(
                out=e_tile[hd][:, t, lo : lo + n], in_=src, func=ACT.Exp, bias=minus_one[:], accum_out=sum_out
            )

        def start_e(hd):
            sums[hd] = work.tile([P, 2, T], F32, name="sums", bufs=3)
            total[hd] = work.tile([P, T], F32, name="total", bufs=3)
            e_tile[hd] = work.tile([P, T, S], BF16, name="e", bufs=2)

        def exponentials_of_rows(hd, *rows_of_blocks):
            for t in rows_of_blocks:
                exponential(
                    hd, t, t * P, (T - t) * P, block(hd, t, t, T - t), sums[hd][:, 1, t : t + 1] if t else total[hd][:, 0:1]
                )

        def exponentials_of_mirrors(hd):
            exponential(hd, 3, 0, 384, mirror[hd, 0][:, 0:384], sums[hd][:, 0, 3:4])
            exponential(hd, 1, 0, 128, mirror.pop((hd, 0))[:, 384:512], sums[hd][:, 0, 1:2])
            exponential(hd, 2, 0, 256, mirror.pop((hd, 1))[:, 0:256], sums[hd][:, 0, 2:3])

        grouped_x = {}
        grouped_e = {}
        packed_x = {}
        packed_e = {}
        inverse = {}

        def regroup_on_gpsimd(dst, src):
            nc.gpsimd.tensor_scalar(
                out=dst, in0=src.rearrange("p t c -> p c t"), scalar1=1.0, scalar2=0.0, op0=ALU.mult, op1=ALU.add
            )

        def x_of(hd):
            b, h = divmod(hd, H)
            return x_tile[b][:, :, h * DK : (h + 1) * DK]

        def regroup_x(hd):
            grouped_x[hd] = work.tile([P, DK, T], BF16, name="grouped_x", bufs=2, align_bytes=64)
            n = DK - X_ON_SCALAR
            regroup_on_gpsimd(grouped_x[hd][:, 0:n], x_of(hd)[:, :, 0:n])

        def regroup_x_on_scalar(hd):
            n = DK - X_ON_SCALAR
            nc.scalar.copy(out=grouped_x[hd][:, n:DK], in_=x_of(hd)[:, :, n:DK].rearrange("p t c -> p c t"))

        def on_vector(hd):
            return E_ON_VECTOR if 0 < hd < HEADS - 2 else S

        def regroup_e_on_gpsimd(hd):
            grouped_e[hd] = work.tile([P, S, T], BF16, name="grouped_e", bufs=2, align_bytes=64)
            n = on_vector(hd)
            if n < S:
                regroup_on_gpsimd(grouped_e[hd][:, n:S], e_tile[hd][:, :, n:S])

        def parts_of(hd, n):
            return ((0, n),) if hd < HEADS - 1 else ((0, S // 2), (S // 2, S))

        def regroup_e(hd):
            e = e_tile.pop(hd)
            for lo, hi in parts_of(hd, on_vector(hd)):
                nc.vector.tensor_copy(
                    out=grouped_e[hd][:, lo:hi].rearrange("p (c i) t -> p c t i", i=4),
                    in_=e[:, :, lo:hi].rearrange("p t (c i) -> p c t i", i=4),
                )

        def quantise(name, grouped, parts):
            codes = work.tile([P, 512], U32, name=name + "_codes", bufs=3, align_bytes=64)
            scales = work.tile([P, 512], U8, name=name + "_scales", bufs=3, align_bytes=64)
            for lo, hi in parts:
                nc.vector.quantize_mx(
                    out=codes[:, lo:hi].bitcast(FP8X4),
                    scales=scales[:, lo:hi],
                    in_=grouped[:, lo:hi].rearrange("p c t -> p (c t)"),
                )
            return codes, scales

        def quantise_x(hd):
            packed_x[hd] = quantise("x", grouped_x.pop(hd), ((0, DK),))

        def quantise_e(hd):
            packed_e[hd] = quantise("e", grouped_e.pop(hd), parts_of(hd, S))

        def add_sums(hd):
            both = sums.pop(hd)
            nc.gpsimd.tensor_tensor(out=total[hd][:, 1:T], in0=both[:, 0, 1:T], in1=both[:, 1, 1:T], op=ALU.add)

        def invert_sums(hd):
            inverse[hd] = work.tile([P, T], F32, name="inverse", bufs=3)
            nc.vector.reciprocal(out=inverse[hd][:], in_=total.pop(hd)[:])

        mx = {}

        def mx_product(hd, u):
            mx[hd, u] = table_bank() if hd >= HEADS - 2 and u % 2 else psum.tile([P, DK], F32, name="mx", tag="mx", bufs=2)
            nc.tensor.matmul_mx(
                out=mx[hd, u][:],
                lhsT=packed_e[hd][0][:, u * P : (u + 1) * P].bitcast(FP8X4),
                lhsT_scale=packed_e[hd][1][:, u * P : (u + 1) * P],
                rhs=packed_x[hd][0][:].bitcast(FP8X4),
                rhs_scale=packed_x[hd][1][:],
                start=True,
                stop=True,
            )

        def divide_and_store(hd, u, on_vector):
            b, h = divmod(hd, H)
            result = work.tile([P, DK], F32, name="result", bufs=2 * T)
            if on_vector:
                nc.vector.tensor_scalar(
                    out=result[:], in0=mx.pop((hd, u))[:], scalar1=inverse[hd][:, u : u + 1], scalar2=None, op0=ALU.mult
                )
            else:
                nc.scalar.activation(out=result[:], in_=mx.pop((hd, u))[:], func=ACT.Copy, scale=inverse[hd][:, u : u + 1])
            nc.sync.dma_start(out=out[b].rearrange("(p t) e -> p t e", t=T)[:, u, h * DK : (h + 1) * DK], in_=result[:])

        def exists(hd):
            return 0 <= hd < HEADS

        def round_of(r):
            old, last, new, next_new = r - 2, r - 1, r + 1, r + 2

            def product(*us):
                if exists(old):
                    for u in us:
                        mx_product(old, u)

            def divide(*us):
                if exists(old):
                    for u in us:
                        divide_and_store(old, u, r != HEADS and r >= HEADS - 1 and u % 2 == 1)

            def factors_of(k):
                if (r, k) in table:
                    multiply_bank(r, k)

            product(0, 1)
            if r == 1:
                invert(B // 2, B)
            if r >= 0 and exists(r + 3):
                load_fixed(r + 3)
            if r % H and X_FIRST <= (r + 5) // H < B:
                load_x((r + 5) // H)
            if exists(last):
                add_sums(last)
                regroup_e_on_gpsimd(last)
            if r >= 0 and exists(r + 3):
                make_terms(r + 3)
            factors_of(0)
            spread_next()
            if r == -1:
                turn_terms(0)
                copy_terms(0)
            if exists(new):
                near_blocks(new, 0)
            if r != HEADS - 1:
                divide(0, 1)
            else:
                divide(0)
            if r != HEADS - 1:
                product(2, 3)
            else:
                product(2)
            if exists(new):
                near_blocks(new, 1)
            factors_of(1)
            spread_next()
            if exists(r) and r != HEADS - 1:
                near_magnitudes(r)
            if exists(r):
                regroup_x_on_scalar(r)
            if r == 0:
                nc.scalar.activation(out=warm[:], in_=minus_one[:], func=ACT.Exp)
            factors_of(2)
            if r != HEADS - 1:
                divide(2, 3)
            else:
                divide(2)
                near_magnitudes(r)
            spread_next()
            factors_of(3)
            spread_next()
            if r == HEADS - 1:
                divide(1)
            if exists(r):
                start_e(r)
                exponentials_of_rows(r, 2, 3)
                far_magnitudes(r)
            if r == -1:
                invert_seventh(1, B)
                seventh_ratios(nc.gpsimd, 1, B)
                make_terms(1)
                factors(1, B)
                make_terms(2)
                regroup_x(0)
                turned_columns = turn_columns()
                invert(1, B // 2)
            if r == HEADS:
                quantise_x(last)
            if exists(new):
                new_score(new)
                join(new, 0)
                join(new, 1)
            if r == -1:
                park_columns(turned_columns)
                load_fixed(2)
            if exists(last):
                regroup_e(last)
            if r == HEADS - 1:
                product(3)
                divide(3)
            if exists(r):
                exponentials_of_rows(r, 0, 1)
                mirrors(r)
                exponentials_of_mirrors(r)
                score.pop(r)
            if r == 1:
                ratios(B // 2, B)
            if exists(last):
                if r < HEADS:
                    quantise_x(last)
                quantise_e(last)
                invert_sums(last)
            if exists(next_new):
                turn_terms(next_new)
                copy_terms(next_new)
            if exists(new) and new > 0:
                regroup_x(new)

        angles(nc.vector, 0, 1)
        sines(0, 1)
        invert(0, 1)
        den_products(nc.gpsimd, 0, 1)
        invert_seventh(0, 1)
        ratios(0, 1)
        seventh_ratios(nc.vector, 0, 1)
        factors(0, 1)
        spread_fixed(0)
        for i in range(TABLES):
            spread_next()
        angles(nc.gpsimd, 1, B)
        make_terms(0)
        sines(1, B)
        den_products(nc.gpsimd, 1, B)
        gather_columns()
        spread_fixed(1)
        round_of(-1)
        ratios(1, B // 2)
        for r in range(HEADS + 2):
            round_of(r)
